import numpy as np
import ml_dtypes


def mxq(x, axis, fmt="e4m3"):
    dtype, down = {"e4m3": (ml_dtypes.float8_e4m3fn, 7), "e5m2": (ml_dtypes.float8_e5m2, 14)}[fmt]
    v = np.moveaxis(np.asarray(x, np.float32).astype(ml_dtypes.bfloat16).astype(np.float64), axis, -1)
    blocks = v.reshape(v.shape[:-1] + (-1, 32))
    amax = np.abs(blocks).max(-1, keepdims=True)
    byte = np.maximum(np.where(amax > 0, np.frexp(amax)[1] - 1 + 127, 0) - down, 1)
    scale = np.exp2(byte - 127.0)
    codes = (blocks / scale).astype(np.float32).astype(dtype).astype(np.float64)
    return np.moveaxis((codes * scale).reshape(v.shape), -1, axis)


WIDE = False


def mx_kscale(k):
    if not WIDE:
        return np.ones(k)
    levels = np.array([10, -10, 5, -5, 0])
    a = np.random.permutation(np.resize(levels, k // 512 * 4)).reshape(k // 512, 4)
    idx = np.arange(k)
    return np.exp2(a[idx // 512, idx % 128 // 32])


BF16 = ml_dtypes.bfloat16


def bf(x):
    return np.asarray(x, np.float32).astype(BF16)


def f64(x):
    return np.asarray(x).astype(np.float64)


B, H, W, D, Dh, Dq, R, T = 16, 16, 16, 512, 512, 128, 16, 8
EPS = 1e-6


def layer_norm(v, g, b):
    mu = v.mean(-1, keepdims=True)
    var = ((v - mu) ** 2).mean(-1, keepdims=True)
    return (v - mu) / np.sqrt(var + EPS) * g + b


def setup_inputs():
    rn = np.random.standard_normal
    s, t = mx_kscale(D), mx_kscale(Dh)
    return {
        "x": bf(rn((B, H, W, D)) * s),
        "z2": bf(rn((B, H, W, Dq)) * 1.5),
        "U1_w": bf(rn((Dh, D)) * np.sqrt(2.0 / D) / s),
        "U1_b": bf(rn(Dh) * 0.5),
        "U3_w": bf(rn((Dh, Dq)) * np.sqrt(2.0 / Dq)),
        "U3_b": bf(rn(Dh) * 0.5),
        "C_w": bf(rn((D, Dh)) / np.sqrt(Dh) / t),
        "C_b": bf(rn(D) * 0.3),
        "ln1_g": bf((1.0 + 0.1 * rn(Dh)) * t),
        "ln1_b": bf(0.2 * rn(Dh) * t),
        "ln3_g": bf(1.0 + 0.1 * rn(Dh)),
        "ln3_b": bf(0.2 * rn(Dh)),
        "alpha": bf(0.6 + 0.2 * np.random.random(1)),
    }


def reference(x, z2, U1_w, U1_b, U3_w, U3_b, C_w, C_b, ln1_g, ln1_b, ln3_g, ln3_b, alpha):
    out1 = (mxq(f64(x), 3, "e4m3") @ mxq(f64(U1_w), 1, "e4m3").T) + f64(U1_b)
    out3 = f64(z2) @ f64(U3_w).T + f64(U3_b)
    o1 = layer_norm(out1, f64(ln1_g), f64(ln1_b))
    o3 = layer_norm(out3, f64(ln3_g), f64(ln3_b))
    h = o1 + f64(alpha) * (o1 * o3)
    return (mxq(h, 3, "e4m3") @ mxq(f64(C_w), 1, "e4m3").T) + f64(C_b)

@@ -1,0 +1,360 @@
+from contextlib import ExitStack
+
+import concourse.mybir as mybir
+from concourse.masks import make_identity
+
+F32 = mybir.dt.float32
+BF16 = mybir.dt.bfloat16
+U32 = mybir.dt.uint32
+U8 = mybir.dt.uint8
+FP8X4 = mybir.dt.float8_e4m3fn_x4
+ALU = mybir.AluOpType
+ACT = mybir.ActivationFunctionType
+
+P = 128
+TOK = 4096
+NT = TOK // P
+NG = NT // 2
+D = 512
+DQ = 128
+EPS = 1e-6
+FLOPS = 2 * TOK * (D * D * 2 + DQ * D)
+
+BODY = [["O",5,1],["A1",0,0],["A",0,"x0",0],["T",2,3,1],["A",1,"e1",0],["T",2,3,0],["B1",0,0],["OB",5,1],["D",2,3,1],["QH",4],["D",2,3,0],["O",5,0],["A",0,"e0",0],["Y1",0,1],["A1",0,1],["C1",1,0],["B1",0,1],["Y3",0,0],["A",0,"q",1],["Y3",0,1],["PR",3,1],["ST",6],["A",0,"z",1],["PR",3,0],["T",2,1,0],["B3",0,0],["B3",0,1],["C1",1,1],["A",0,"ez",1],["OB",5,0],["D",2,1,0],["SQ",0],["T",2,1,1],["D",2,1,1],["RN",0],["Y1",-1,0],["A",0,"x1",0],["C3",0,0],["C3",0,1]]
+BUFS = {"y1":1,"y3":2,"nT":2,"o":2,"xz":1}
+DENG = {"10":"S","11":"S","30":"S","31":"S"}
+DENG_T = {"10":"S","11":"S","30":"S","31":"V"}
+PRENG = ["G","G"]
+PRENG_T = ["G","V"]
+TAILK = 14
+C1ENG = "g"
+PIN = True
+BIAS_FIRST = True
+
+
+def tile_polymlp_skiplora_pa_t_kernel(
+    tc, x, z2, U1_w, U1_b, U3_w, U3_b, C_w, C_b, ln1_g, ln1_b, ln3_g, ln3_b, alpha, out
+):
+    nc = tc.nc
+    xv = x.flatten_outer_dims().rearrange("(p i) k -> p i k", i=NT)
+    zv = z2.flatten_outer_dims().rearrange("(p i) k -> p i k", i=NT)
+    ov = out.flatten_outer_dims().rearrange("(p i) d -> p i d", i=NT)
+
+    with ExitStack() as ctx:
+        keep = ctx.enter_context(tc.tile_pool(name="keep", bufs=1))
+        work = ctx.enter_context(tc.tile_pool(name="work", bufs=2))
+        small = ctx.enter_context(tc.tile_pool(name="small", bufs=4))
+        psum = ctx.enter_context(tc.psum_pool(name="psum", bufs=1))
+
+        prm = keep.tile([P, P], BF16, name="prm")
+        nc.vector.memset(prm[:], 0.0)
+        vecs = [U1_b, U3_b, C_b, ln1_g, ln1_b, ln3_g, ln3_b]
+        for j, vec in enumerate(vecs):
+            nc.scalar.dma_start(out=prm[4 * j : 4 * j + 4, :], in_=vec.rearrange("(c p) -> c p", p=P))
+        al_b = keep.tile([P, 1], BF16, name="al_b")
+        nc.scalar.dma_start(out=al_b[:], in_=alpha.partition_broadcast(P))
+
+        x_sb = keep.tile([P, NT, D], BF16, name="x_sb")
+        z_sb = keep.tile([P, NT, DQ], BF16, name="z_sb")
+        u1_raw = keep.tile([P, 4, D], BF16, name="u1_raw")
+        u3_raw = keep.tile([P, 4, DQ], BF16, name="u3_raw")
+        c_raw = keep.tile([P, 4, D], BF16, name="c_raw")
+        nc.sync.dma_start(out=u1_raw[:], in_=U1_w.rearrange("(c p) k -> p c k", p=P))
+        nc.sync.dma_start(out=x_sb[:, 0:4, :], in_=xv[:, 0:4, :])
+        nc.sync.dma_start(out=z_sb[:, 0:16, :], in_=zv[:, 0:16, :])
+        nc.sync.dma_start(out=u3_raw[:], in_=U3_w.rearrange("(c p) k -> p c k", p=P))
+        nc.sync.dma_start(out=x_sb[:, 4:8, :], in_=xv[:, 4:8, :])
+        nc.sync.dma_start(out=c_raw[:], in_=C_w.rearrange("(c p) k -> p c k", p=P))
+        nc.sync.dma_start(out=z_sb[:, 16:32, :], in_=zv[:, 16:32, :])
+        for q in range(2, 8):
+            nc.sync.dma_start(out=x_sb[:, 4 * q : 4 * q + 4, :], in_=xv[:, 4 * q : 4 * q + 4, :])
+
+        ident_f = keep.tile([P, P], F32, name="ident_f")
+        make_identity(nc, ident_f[:])
+        ident_b = keep.tile([P, P], BF16, name="ident_b")
+        make_identity(nc, ident_b[:])
+        eps_t = keep.tile([P, 1], F32, name="eps_t")
+        nc.vector.memset(eps_t[:], EPS)
+
+        xq = keep.tile([P, TOK], U32, name="xq", align_bytes=64)
+        xs = keep.tile([P, TOK], U8, name="xs", align_bytes=64)
+        hq = keep.tile([P, TOK], U32, name="hq", align_bytes=64)
+        hs = keep.tile([P, TOK], U8, name="hs", align_bytes=64)
+        z2T = keep.tile([P, TOK], BF16, name="z2T")
+        live = {}
+
+        def words_T(rows_pair):
+            bank = psum.tile([P, 2, 2, P], F32, name="wbank", tag="xz", bufs=BUFS["xz"])
+            for j, rows in enumerate(rows_pair):
+                w = rows.bitcast(F32)
+                for u in range(2):
+                    nc.tensor.transpose(bank[:, j, u, :], w[:, u * P : (u + 1) * P], ident_f[:])
+            return bank
+
+        def words_E(bank, grouped32, eng):
+            if eng == "S":
+                nc.scalar.copy(out=grouped32, in_=bank[:].rearrange("p j u r -> p j r u"))
+            else:
+                nc.vector.tensor_copy(out=grouped32, in_=bank[:].rearrange("p j u r -> p j r u"))
+
+        def xg_view(q):
+            if ("xg", q) not in live:
+                live[("xg", q)] = work.tile([P, 4 * D], BF16, name="xg", tag="xg", align_bytes=64)
+            return live[("xg", q)]
+
+        def p_AX(q, h):
+            live[("xb", q, h)] = words_T([x_sb[:, 4 * q + 2 * h + j, :] for j in range(2)])
+
+        def p_EX(q, h):
+            v32 = xg_view(q)[:].bitcast(F32).rearrange("p (j r u) -> p j r u", j=4, u=2)
+            words_E(live[("xb", q, h)], v32[:, 2 * h : 2 * h + 2], "S")
+
+        def p_AZ(q):
+            zt = psum.tile([P, 4, P], BF16, name="zt", tag="xz", bufs=BUFS["xz"])
+            for j in range(4):
+                nc.tensor.transpose(zt[:, j, :], z_sb[:, 4 * q + j, :], ident_b[:])
+            live[("zb", q)] = zt
+
+        def p_EZ(q):
+            nc.scalar.copy(out=z2T[:, 512 * q : 512 * q + 512], in_=live[("zb", q)][:].rearrange("p j r -> p (j r)"))
+
+        def p_QX(q):
+            nc.vector.quantize_mx(
+                out=xq[:, 512 * q : 512 * q + 512].bitcast(FP8X4),
+                scales=xs[:, 512 * q : 512 * q + 512],
+                in_=xg_view(q)[:],
+            )
+
+        u1g = keep.tile([P, 4 * D], BF16, name="u1g", align_bytes=64)
+        u1v = u1g[:].bitcast(F32).rearrange("p (j r u) -> p j r u", j=4, u=2)
+        for h in range(2):
+            words_E(words_T([u1_raw[:, 2 * h + j, :] for j in range(2)]), u1v[:, 2 * h : 2 * h + 2], "SV"[h])
+        u1q = keep.tile([P, D], U32, name="u1q", align_bytes=64)
+        u1s = keep.tile([P, D], U8, name="u1s", align_bytes=64)
+        nc.vector.quantize_mx(out=u1q[:].bitcast(FP8X4), scales=u1s[:], in_=u1g[:])
+
+        for h in range(2):
+            p_AX(0, h)
+            p_EX(0, h)
+        p_QX(0)
+        p_AZ(0)
+        p_EZ(0)
+
+        pT = psum.tile([P, P], BF16, name="pT", tag="o", bufs=BUFS["o"])
+        nc.tensor.transpose(pT[:], prm[:], ident_b[:])
+        prmT = keep.tile([P, 28], F32, name="prmT")
+        nc.vector.tensor_copy(out=prmT[:], in_=pT[:, 0:28])
+        al = keep.tile([P, 1], F32, name="al")
+        nc.vector.tensor_copy(out=al[:], in_=al_b[:])
+        g1 = prmT[:, 12:16]
+        be1 = prmT[:, 16:20]
+        a3 = keep.tile([P, 4], F32, name="a3")
+        c3 = keep.tile([P, 4], F32, name="c3")
+        nc.vector.tensor_scalar(out=a3[:], in0=prmT[:, 20:24], scalar1=al[:, 0:1], scalar2=None, op0=ALU.mult)
+        nc.vector.tensor_scalar(
+            out=c3[:], in0=prmT[:, 24:28], scalar1=al[:, 0:1], scalar2=1.0, op0=ALU.mult, op1=ALU.add
+        )
+        rep = keep.tile([P, 12, P], F32, name="rep")
+        nc.vector.tensor_copy(out=rep[:], in_=prmT[:, 0:12].unsqueeze(2).to_broadcast([P, 12, P]))
+
+        def spread(first, name, tag):
+            bank = psum.tile([P, D], F32, name="sbank", tag=tag, bufs=BUFS[tag])
+            for c in range(4):
+                nc.tensor.transpose(bank[:, c * P : (c + 1) * P], rep[:, first + c, :], ident_f[:])
+            row = keep.tile([P, D], F32, name=name)
+            nc.vector.tensor_copy(out=row[:], in_=bank[:])
+            return row
+
+        b1row = spread(0, "b1row", "y1")
+
+        ut = psum.tile([P, 4, P], BF16, name="ut", tag="y3", bufs=BUFS["y3"])
+        for c in range(4):
+            nc.tensor.transpose(ut[:, c, :], u3_raw[:, c, :], ident_b[:])
+        u3T = keep.tile([P, D], BF16, name="u3T")
+        nc.scalar.copy(out=u3T[:], in_=ut[:].rearrange("p c r -> p (c r)"))
+
+        cbrow = spread(8, "cbrow", "y3")
+
+        cg = keep.tile([P, D, 4], BF16, name="cg", align_bytes=64)
+        for dc in range(4):
+            ct = psum.tile([P, 4, P], BF16, name="ct", tag="nT", bufs=BUFS["nT"])
+            for t in range(4):
+                nc.tensor.transpose(ct[:, t, :], c_raw[:, dc, t * P : (t + 1) * P], ident_b[:])
+            if dc % 2 == 0:
+                nc.vector.tensor_copy(out=cg[:, dc * P : (dc + 1) * P, :], in_=ct[:].rearrange("p t r -> p r t"))
+            else:
+                nc.scalar.copy(out=cg[:, dc * P : (dc + 1) * P, :], in_=ct[:].rearrange("p t r -> p r t"))
+        cq = keep.tile([P, D], U32, name="cq", align_bytes=64)
+        cs = keep.tile([P, D], U8, name="cs", align_bytes=64)
+        nc.vector.quantize_mx(out=cq[:].bitcast(FP8X4), scales=cs[:], in_=cg[:].rearrange("p d t -> p (d t)"))
+
+        def get(tag, k, shape, dtype, pool, bufs, align=None):
+            if (tag, k) not in live:
+                if align is None:
+                    live[(tag, k)] = pool.tile(shape, dtype, name=tag, tag=tag, bufs=bufs)
+                else:
+                    live[(tag, k)] = pool.tile(shape, dtype, name=tag, tag=tag, bufs=bufs, align_bytes=align)
+            return live[(tag, k)]
+
+        def p_Y1(t):
+            cols = slice(t * P, (t + 1) * P)
+            y1 = get("y1", t, [P, D], F32, psum, BUFS["y1"])
+            nc.tensor.matmul_mx(
+                out=y1[:], lhsT=xq[:, cols].bitcast(FP8X4), lhsT_scale=xs[:, cols],
+                rhs=u1q[:].bitcast(FP8X4), rhs_scale=u1s[:], start=True, stop=True,
+            )
+
+        def p_Y3(t):
+            cols = slice(t * P, (t + 1) * P)
+            y3 = get("y3", t, [P, D], F32, psum, BUFS["y3"])
+            if not BIAS_FIRST:
+                nc.tensor.matmul(y3[:], lhsT=z2T[:, cols], rhs=u3T[:], start=True, stop=False)
+            for c in range(4):
+                nc.tensor.matmul(
+                    y3[:, c * P : (c + 1) * P], lhsT=rep[:, 4 + c, :], rhs=ident_f[:], is_transpose=True,
+                    start=(BIAS_FIRST and c == 0), stop=((not BIAS_FIRST) and c == 3),
+                )
+            if BIAS_FIRST:
+                nc.tensor.matmul(y3[:], lhsT=z2T[:, cols], rhs=u3T[:], start=False, stop=True)
+
+        def mv_of(k):
+            return get("mv", k, [P, 2, 2, 2], F32, small, 4)
+
+        def p_A1(t):
+            t1 = get("t1", t, [P, D], F32, work, 4)
+            nc.vector.tensor_tensor(out=t1[:], in0=live[("y1", t)][:], in1=b1row[:], op=ALU.add)
+
+        def stats(t, br, src):
+            st = small.tile([P, 6], F32, name="st", tag="st", bufs=4)
+            nc.vector.bn_stats(out=st[:], in_=src)
+            nc.vector.bn_aggr(out=mv_of(t // 2)[:, t % 2, br, :], in_=st[:])
+
+        def p_B1(t):
+            stats(t, 0, live[("t1", t)][:])
+
+        def p_B3(t):
+            stats(t, 1, live[("y3", t)][:])
+
+        def p_SQ(k):
+            sd = get("sd", k, [P, 2, 2], F32, small, 4)
+            nc.scalar.activation(out=sd[:], in_=mv_of(k)[:, :, :, 1], func=ACT.Sqrt, bias=eps_t[:, 0:1], scale=1.0)
+
+        def p_RN(k):
+            rs = get("rs", k, [P, 2, 2], F32, small, 4)
+            nm = get("nm", k, [P, 2, 2], F32, small, 4)
+            nc.vector.reciprocal(out=rs[:], in_=live[("sd", k)][:])
+            nc.vector.scalar_tensor_tensor(
+                out=nm[:], in0=mv_of(k)[:, :, :, 0], scalar=-1.0, in1=rs[:], op0=ALU.mult, op1=ALU.mult
+            )
+
+        def p_C1(t):
+            k, j = t // 2, t % 2
+            n1 = get("n1", k, [P, 2, D], F32, work, 3)
+            rs, nm = live[("rs", k)], live[("nm", k)]
+            if C1ENG == "g":
+                nc.gpsimd.tensor_scalar(
+                    out=n1[:, j, :], in0=live[("t1", t)][:], scalar1=rs[:, j, 0:1], scalar2=nm[:, j, 0:1],
+                    op0=ALU.mult, op1=ALU.add,
+                )
+            else:
+                nc.vector.tensor_scalar(
+                    out=n1[:, j, :], in0=live[("t1", t)][:], scalar1=mv_of(k)[:, j, 0, 0:1], scalar2=rs[:, j, 0:1],
+                    op0=ALU.subtract, op1=ALU.mult,
+                )
+
+        def p_C3(t):
+            k, j = t // 2, t % 2
+            n3 = get("n3", k, [P, 2, D], F32, work, 3)
+            rs, nm = live[("rs", k)], live[("nm", k)]
+            nc.scalar.activation(
+                out=n3[:, j, :], in_=live[("y3", t)][:], func=ACT.Identity, scale=rs[:, j, 1:2], bias=nm[:, j, 1:2]
+            )
+
+        def p_T(k, br, h):
+            src = live[("n%d" % br, k)]
+            bank = psum.tile([P, 2, 2, P], F32, name="nT", tag="nT", bufs=BUFS["nT"])
+            for cc in range(2):
+                c = 2 * h + cc
+                for j in range(2):
+                    nc.tensor.transpose(bank[:, cc, j, :], src[:, j, c * P : (c + 1) * P], ident_f[:])
+            live[("nT", k, br, h)] = bank
+
+        def p_D(k, br, h):
+            bank = live[("nT", k, br, h)]
+            dst = get("av" if br == 1 else "bv", k, [P, 4, 2, P], F32, work, 2)
+            sc, bi = (g1, be1) if br == 1 else (a3, c3)
+            eng = (DENG_T if k >= TAILK else DENG)["%d%d" % (br, h)]
+            for cc in range(2):
+                c = 2 * h + cc
+                if eng == "S":
+                    nc.scalar.activation(
+                        out=dst[:, c, :, :], in_=bank[:, cc, :, :], func=ACT.Identity,
+                        scale=sc[:, c : c + 1], bias=bi[:, c : c + 1],
+                    )
+                else:
+                    nc.vector.tensor_scalar(
+                        out=dst[:, c, :, :], in0=bank[:, cc, :, :], scalar1=sc[:, c : c + 1],
+                        scalar2=bi[:, c : c + 1], op0=ALU.mult, op1=ALU.add,
+                    )
+
+        def p_PR(k, j):
+            hg = get("hg", k, [P, 2, P, 4], BF16, work, 2, 64)
+            eng = nc.gpsimd if (PRENG_T if k >= TAILK else PRENG)[j] == "G" else nc.vector
+            eng.tensor_tensor(
+                out=hg[:, j, :, :],
+                in0=live[("av", k)][:, :, j, :].rearrange("p c r -> p r c"),
+                in1=live[("bv", k)][:, :, j, :].rearrange("p c r -> p r c"),
+                op=ALU.mult,
+            )
+
+        def p_QH(k):
+            cols = slice(2 * k * P, 2 * (k + 1) * P)
+            nc.vector.quantize_mx(
+                out=hq[:, cols].bitcast(FP8X4), scales=hs[:, cols],
+                in_=live[("hg", k)][:].rearrange("p j r c -> p (j r c)"),
+            )
+
+        def p_O(t):
+            cols = slice(t * P, (t + 1) * P)
+            o = get("o", t, [P, D], F32, psum, BUFS["o"])
+            nc.tensor.matmul_mx(
+                out=o[:], lhsT=hq[:, cols].bitcast(FP8X4), lhsT_scale=hs[:, cols],
+                rhs=cq[:].bitcast(FP8X4), rhs_scale=cs[:], start=True, stop=True,
+            )
+
+        def p_OB(t):
+            ost = get("ost", t // 2, [P, 2, D], F32, work, 3)
+            nc.vector.tensor_tensor(out=ost[:, t % 2, :], in0=live[("o", t)][:], in1=cbrow[:], op=ALU.add)
+
+        def p_ST(k):
+            nc.sync.dma_start(out=ov[:, 2 * k : 2 * k + 2, :], in_=live[("ost", k)][:])
+
+        tile_pieces = {"Y1": p_Y1, "Y3": p_Y3, "A1": p_A1, "B1": p_B1, "B3": p_B3, "C1": p_C1, "C3": p_C3, "O": p_O, "OB": p_OB}
+        pair_pieces = {"SQ": p_SQ, "RN": p_RN, "QH": p_QH, "ST": p_ST}
+        a_pieces = {
+            "x0": lambda q: p_AX(q, 0), "e0": lambda q: p_EX(q, 0), "x1": lambda q: p_AX(q, 1),
+            "e1": lambda q: p_EX(q, 1), "z": p_AZ, "ez": p_EZ, "q": p_QX,
+        }
+
+        if PIN:
+            ctx.enter_context(tc.manual_schedule())
+        lags = [b[1] for b in BODY]
+        for k in range(min(lags), NG + max(lags)):
+            for b in BODY:
+                i = k - b[1]
+                if i < 0 or i >= NG:
+                    continue
+                if b[0] == "A":
+                    q = i // 2 + 1
+                    if q < 8 and i % 2 == b[3]:
+                        a_pieces[b[2]](q)
+                elif b[0] == "T":
+                    p_T(i, b[2], b[3])
+                elif b[0] == "D":
+                    p_D(i, b[2], b[3])
+                elif b[0] == "PR":
+                    p_PR(i, b[2])
+                elif b[0] in tile_pieces:
+                    tile_pieces[b[0]](2 * i + b[2])
+                else:
+                    pair_pieces[b[0]](i)

@@ -20,14 +20,16 @@ DQ = 128
 EPS = 1e-6
 FLOPS = 2 * TOK * (D * D * 2 + DQ * D)
 
-BODY = [["O",5,1],["A1",0,0],["A",0,"x0",0],["T",2,3,1],["A",1,"e1",0],["T",2,3,0],["B1",0,0],["OB",5,1],["D",2,3,1],["QH",4],["D",2,3,0],["O",5,0],["A",0,"e0",0],["Y1",0,1],["A1",0,1],["C1",1,0],["B1",0,1],["Y3",0,0],["A",0,"q",1],["Y3",0,1],["PR",3,1],["ST",6],["A",0,"z",1],["PR",3,0],["T",2,1,0],["B3",0,0],["B3",0,1],["C1",1,1],["A",0,"ez",1],["OB",5,0],["D",2,1,0],["SQ",0],["T",2,1,1],["D",2,1,1],["RN",0],["Y1",-1,0],["A",0,"x1",0],["C3",0,0],["C3",0,1]]
+BODY = [["A1",0,0],["RG",4],["O",6,1],["OB",6,1],["ST",8],["T",2,3,1],["A",0,"x0",0],["B1",0,0],["O",6,0],["T",2,3,0],["D",2,3,1],["A",1,"e1",0],["PRP",3],["D",2,3,0],["QH",5],["Y1",0,1],["A1",0,1],["A",0,"e0",0],["C1",1,0],["Y3",0,0],["B1",0,1],["A",0,"q",1],["Y3",0,1],["B3",0,0],["B3",0,1],["A",0,"z",1],["A",0,"ez",1],["T",2,1,0],["D",2,1,0],["OB",6,0],["SQ",0],["T",2,1,1],["C1",1,1],["A",0,"x1",0],["D",2,1,1],["RN",0],["Y1",-1,0],["C3",0,0],["C3",0,1]]
 BUFS = {"y1":1,"y3":2,"nT":2,"o":2,"xz":1}
 DENG = {"10":"S","11":"S","30":"S","31":"S"}
-DENG_T = {"10":"S","11":"S","30":"S","31":"V"}
-PRENG = ["G","G"]
-PRENG_T = ["G","V"]
+DENG_T = {"10":"S","11":"V","30":"V","31":"V"}
+PRENG = "G"
+PRENG_T = "G"
+RGENG = "G"
+RGENG_T = "S"
 TAILK = 14
-C1ENG = "g"
+C1ENG = ["S","V"]
 PIN = True
 BIAS_FIRST = True
 
@@ -251,7 +253,11 @@ def tile_polymlp_skiplora_pa_t_kernel(
             k, j = t // 2, t % 2
             n1 = get("n1", k, [P, 2, D], F32, work, 3)
             rs, nm = live[("rs", k)], live[("nm", k)]
-            if C1ENG == "g":
+            if C1ENG[j] == "S":
+                nc.scalar.activation(
+                    out=n1[:, j, :], in_=live[("t1", t)][:], func=ACT.Identity, scale=rs[:, j, 0:1], bias=nm[:, j, 0:1]
+                )
+            elif C1ENG[j] == "G":
                 nc.gpsimd.tensor_scalar(
                     out=n1[:, j, :], in0=live[("t1", t)][:], scalar1=rs[:, j, 0:1], scalar2=nm[:, j, 0:1],
                     op0=ALU.mult, op1=ALU.add,
@@ -297,15 +303,26 @@ def tile_polymlp_skiplora_pa_t_kernel(
                         scalar2=bi[:, c : c + 1], op0=ALU.mult, op1=ALU.add,
                     )
 
-        def p_PR(k, j):
-            hg = get("hg", k, [P, 2, P, 4], BF16, work, 2, 64)
-            eng = nc.gpsimd if (PRENG_T if k >= TAILK else PRENG)[j] == "G" else nc.vector
+        def p_PRP(k):
+            hp = get("hp", k, [P, 4, 2, P], BF16, work, 2)
+            eng = nc.gpsimd if (PRENG_T if k >= TAILK else PRENG) == "G" else nc.vector
             eng.tensor_tensor(
-                out=hg[:, j, :, :],
-                in0=live[("av", k)][:, :, j, :].rearrange("p c r -> p r c"),
-                in1=live[("bv", k)][:, :, j, :].rearrange("p c r -> p r c"),
+                out=hp[:].rearrange("p c j r -> p (c j r)"),
+                in0=live[("av", k)][:].rearrange("p c j r -> p (c j r)"),
+                in1=live[("bv", k)][:].rearrange("p c j r -> p (c j r)"),
                 op=ALU.mult,
             )
+
+        def p_RG(k):
+            hg = get("hg", k, [P, 2, P, 4], BF16, work, 2, 64)
+            src = live[("hp", k)][:].rearrange("p c j r -> p j r c")
+            eng = RGENG_T if k >= TAILK else RGENG
+            if eng == "G":
+                nc.gpsimd.tensor_scalar(out=hg[:], in0=src, scalar1=1.0, scalar2=0.0, op0=ALU.mult, op1=ALU.add)
+            elif eng == "V":
+                nc.vector.tensor_copy(out=hg[:], in_=src)
+            else:
+                nc.scalar.copy(out=hg[:], in_=src)
 
         def p_QH(k):
             cols = slice(2 * k * P, 2 * (k + 1) * P)
@@ -330,7 +347,7 @@ def tile_polymlp_skiplora_pa_t_kernel(
             nc.sync.dma_start(out=ov[:, 2 * k : 2 * k + 2, :], in_=live[("ost", k)][:])
 
         tile_pieces = {"Y1": p_Y1, "Y3": p_Y3, "A1": p_A1, "B1": p_B1, "B3": p_B3, "C1": p_C1, "C3": p_C3, "O": p_O, "OB": p_OB}
-        pair_pieces = {"SQ": p_SQ, "RN": p_RN, "QH": p_QH, "ST": p_ST}
+        pair_pieces = {"SQ": p_SQ, "RN": p_RN, "QH": p_QH, "ST": p_ST, "PRP": p_PRP, "RG": p_RG}
         a_pieces = {
             "x0": lambda q: p_AX(q, 0), "e0": lambda q: p_EX(q, 0), "x1": lambda q: p_AX(q, 1),
             "e1": lambda q: p_EX(q, 1), "z": p_AZ, "ez": p_EZ, "q": p_QX,
@@ -352,8 +369,6 @@ def tile_polymlp_skiplora_pa_t_kernel(
                     p_T(i, b[2], b[3])
                 elif b[0] == "D":
                     p_D(i, b[2], b[3])
-                elif b[0] == "PR":
-                    p_PR(i, b[2])
                 elif b[0] in tile_pieces:
                     tile_pieces[b[0]](2 * i + b[2])
                 else:

@@ -32,6 +32,7 @@ TAILK = 14
 C1ENG = ["S","V"]
 PIN = True
 BIAS_FIRST = True
+DUP = 2
 
 
 def tile_polymlp_skiplora_pa_t_kernel(
@@ -201,10 +202,11 @@ def tile_polymlp_skiplora_pa_t_kernel(
         def p_Y1(t):
             cols = slice(t * P, (t + 1) * P)
             y1 = get("y1", t, [P, D], F32, psum, BUFS["y1"])
-            nc.tensor.matmul_mx(
-                out=y1[:], lhsT=xq[:, cols].bitcast(FP8X4), lhsT_scale=xs[:, cols],
-                rhs=u1q[:].bitcast(FP8X4), rhs_scale=u1s[:], start=True, stop=True,
-            )
+            for rep_i in range(DUP):
+                nc.tensor.matmul_mx(
+                    out=y1[:], lhsT=xq[:, cols].bitcast(FP8X4), lhsT_scale=xs[:, cols],
+                    rhs=u1q[:].bitcast(FP8X4), rhs_scale=u1s[:], start=True, stop=True,
+                )
 
         def p_Y3(t):
             cols = slice(t * P, (t + 1) * P)
@@ -334,10 +336,11 @@ def tile_polymlp_skiplora_pa_t_kernel(
         def p_O(t):
             cols = slice(t * P, (t + 1) * P)
             o = get("o", t, [P, D], F32, psum, BUFS["o"])
-            nc.tensor.matmul_mx(
-                out=o[:], lhsT=hq[:, cols].bitcast(FP8X4), lhsT_scale=hs[:, cols],
-                rhs=cq[:].bitcast(FP8X4), rhs_scale=cs[:], start=True, stop=True,
-            )
+            for rep_i in range(DUP):
+                nc.tensor.matmul_mx(
+                    out=o[:], lhsT=hq[:, cols].bitcast(FP8X4), lhsT_scale=hs[:, cols],
+                    rhs=cq[:].bitcast(FP8X4), rhs_scale=cs[:], start=True, stop=True,
+                )
 
         def p_OB(t):
             ost = get("ost", t // 2, [P, 2, D], F32, work, 3)

@@ -18,21 +18,23 @@ NG = NT // 2
 D = 512
 DQ = 128
 EPS = 1e-6
+GW = DQ + 2
 FLOPS = 2 * TOK * (D * D * 2 + DQ * D)
 
-BODY = [["A1",0,0],["RG",4],["O",6,1],["OB",6,1],["ST",8],["T",2,3,1],["A",0,"x0",0],["B1",0,0],["O",6,0],["T",2,3,0],["D",2,3,1],["A",1,"e1",0],["PRP",3],["D",2,3,0],["QH",5],["Y1",0,1],["A1",0,1],["A",0,"e0",0],["C1",1,0],["Y3",0,0],["B1",0,1],["A",0,"q",1],["Y3",0,1],["B3",0,0],["B3",0,1],["A",0,"z",1],["A",0,"ez",1],["T",2,1,0],["D",2,1,0],["OB",6,0],["SQ",0],["T",2,1,1],["C1",1,1],["A",0,"x1",0],["D",2,1,1],["RN",0],["Y1",-1,0],["C3",0,0],["C3",0,1]]
-BUFS = {"y1":1,"y3":2,"nT":2,"o":2,"xz":1}
+BODY = [["B1",1,0],["B1",1,1],["T",3,3,1],["Y1",0,0],["T",3,3,0],["ST",10],["A",-37,"x0",0],["D",3,3,1],["RN",2],["C1",2,1],["Y1",0,1],["D",3,3,0],["A1",0,0],["O",8,0],["A",-63,"z",1],["Y3",0,1],["A",-33,"e0",0],["A",-54,"ez",1],["O",7,1],["T",3,1,1],["C1",2,0],["A1",0,1],["C3",0,1],["RG",5],["A",-34,"e1",0],["A",-34,"q",1],["R3",-15],["SQ",1],["PRP",4],["OB",8,0],["A",-19,"zc",1],["A",-39,"x1",0],["OB",7,1],["S3",-17],["QH",5],["W",-19],["T",3,1,0],["D",3,1,1],["Y3",0,0],["D",3,1,0],["WS",-18],["C3",0,0]]
+BUFS = {"t1":6,"n1":3,"n3":3,"ab":3,"hp":2,"hg":2,"ost":3}
 DENG = {"10":"S","11":"S","30":"S","31":"S"}
-DENG_T = {"10":"S","11":"V","30":"V","31":"V"}
+DENG_T = {"10":"S","11":"S","30":"S","31":"S"}
 PRENG = "G"
-PRENG_T = "G"
+PRENG_T = "V"
 RGENG = "G"
-RGENG_T = "S"
-TAILK = 14
-C1ENG = ["S","V"]
+RGENG_T = "G"
+TAILK = 13
+C1ENG = ["V","V"]
 PIN = True
 BIAS_FIRST = True
-DUP = 2
+DUP = 1
+SB = 17
 
 
 def tile_polymlp_skiplora_pa_t_kernel(
@@ -62,10 +64,10 @@ def tile_polymlp_skiplora_pa_t_kernel(
         u1_raw = keep.tile([P, 4, D], BF16, name="u1_raw")
         u3_raw = keep.tile([P, 4, DQ], BF16, name="u3_raw")
         c_raw = keep.tile([P, 4, D], BF16, name="c_raw")
+        nc.sync.dma_start(out=u3_raw[:], in_=U3_w.rearrange("(c p) k -> p c k", p=P))
         nc.sync.dma_start(out=u1_raw[:], in_=U1_w.rearrange("(c p) k -> p c k", p=P))
         nc.sync.dma_start(out=x_sb[:, 0:4, :], in_=xv[:, 0:4, :])
         nc.sync.dma_start(out=z_sb[:, 0:16, :], in_=zv[:, 0:16, :])
-        nc.sync.dma_start(out=u3_raw[:], in_=U3_w.rearrange("(c p) k -> p c k", p=P))
         nc.sync.dma_start(out=x_sb[:, 4:8, :], in_=xv[:, 4:8, :])
         nc.sync.dma_start(out=c_raw[:], in_=C_w.rearrange("(c p) k -> p c k", p=P))
         nc.sync.dma_start(out=z_sb[:, 16:32, :], in_=zv[:, 16:32, :])
@@ -87,7 +89,7 @@ def tile_polymlp_skiplora_pa_t_kernel(
         live = {}
 
         def words_T(rows_pair):
-            bank = psum.tile([P, 2, 2, P], F32, name="wbank", tag="xz", bufs=BUFS["xz"])
+            bank = psum.tile([P, 2, 2, P], F32, name="wbank", tag="ps", bufs=8)
             for j, rows in enumerate(rows_pair):
                 w = rows.bitcast(F32)
                 for u in range(2):
@@ -113,7 +115,7 @@ def tile_polymlp_skiplora_pa_t_kernel(
             words_E(live[("xb", q, h)], v32[:, 2 * h : 2 * h + 2], "S")
 
         def p_AZ(q):
-            zt = psum.tile([P, 4, P], BF16, name="zt", tag="xz", bufs=BUFS["xz"])
+            zt = psum.tile([P, 4, P], BF16, name="zt", tag="ps", bufs=8)
             for j in range(4):
                 nc.tensor.transpose(zt[:, j, :], z_sb[:, 4 * q + j, :], ident_b[:])
             live[("zb", q)] = zt
@@ -143,7 +145,7 @@ def tile_polymlp_skiplora_pa_t_kernel(
         p_AZ(0)
         p_EZ(0)
 
-        pT = psum.tile([P, P], BF16, name="pT", tag="o", bufs=BUFS["o"])
+        pT = psum.tile([P, P], BF16, name="pT", tag="ps", bufs=8)
         nc.tensor.transpose(pT[:], prm[:], ident_b[:])
         prmT = keep.tile([P, 28], F32, name="prmT")
         nc.vector.tensor_copy(out=prmT[:], in_=pT[:, 0:28])
@@ -161,7 +163,7 @@ def tile_polymlp_skiplora_pa_t_kernel(
         nc.vector.tensor_copy(out=rep[:], in_=prmT[:, 0:12].unsqueeze(2).to_broadcast([P, 12, P]))
 
         def spread(first, name, tag):
-            bank = psum.tile([P, D], F32, name="sbank", tag=tag, bufs=BUFS[tag])
+            bank = psum.tile([P, D], F32, name="sbank", tag="ps", bufs=8)
             for c in range(4):
                 nc.tensor.transpose(bank[:, c * P : (c + 1) * P], rep[:, first + c, :], ident_f[:])
             row = keep.tile([P, D], F32, name=name)
@@ -170,7 +172,7 @@ def tile_polymlp_skiplora_pa_t_kernel(
 
         b1row = spread(0, "b1row", "y1")
 
-        ut = psum.tile([P, 4, P], BF16, name="ut", tag="y3", bufs=BUFS["y3"])
+        ut = psum.tile([P, 4, P], BF16, name="ut", tag="ps", bufs=8)
         for c in range(4):
             nc.tensor.transpose(ut[:, c, :], u3_raw[:, c, :], ident_b[:])
         u3T = keep.tile([P, D], BF16, name="u3T")
@@ -178,9 +180,48 @@ def tile_polymlp_skiplora_pa_t_kernel(
 
         cbrow = spread(8, "cbrow", "y3")
 
+        ones_f = keep.tile([P, P], F32, name="ones_f")
+        nc.vector.memset(ones_f[:], 1.0)
+        negc = keep.tile([P, 2], F32, name="negc")
+        nc.vector.memset(negc[:], -1.0 / D)
+        u3f = keep.tile([P, 4, GW], F32, name="u3f")
+        nc.vector.memset(u3f[:], 0.0)
+        nc.vector.tensor_copy(out=u3f[:, :, 0:DQ], in_=u3_raw[:])
+        nc.vector.tensor_copy(out=u3f[:, :, DQ : DQ + 1], in_=prmT[:, 4:8].unsqueeze(2))
+        ps1 = psum.tile([P, GW], F32, name="ps1", tag="ps", bufs=8)
+        for c in range(4):
+            nc.tensor.matmul(ps1[:], lhsT=ones_f[:], rhs=u3f[:, c, :], start=(c == 0), stop=(c == 3))
+        u3c = keep.tile([P, 4, GW], F32, name="u3c")
+        for c in range(4):
+            nc.vector.scalar_tensor_tensor(
+                out=u3c[:, c, :], in0=ps1[:], scalar=-1.0 / D, in1=u3f[:, c, :], op0=ALU.mult, op1=ALU.add
+            )
+        negb = keep.tile([P, 1], F32, name="negb")
+        nc.vector.tensor_scalar(out=negb[:], in0=ps1[:, DQ : DQ + 1], scalar1=-1.0 / D, scalar2=None, op0=ALU.mult)
+        ps2 = psum.tile([P, GW], F32, name="ps2", tag="ps", bufs=8)
+        for c in range(4):
+            nc.tensor.matmul(ps2[:], lhsT=u3c[:, c, 0:DQ], rhs=u3c[:, c, :], start=(c == 0), stop=(c == 3))
+        ps3 = psum.tile([P, 2], F32, name="ps3", tag="ps", bufs=8)
+        for c in range(4):
+            nc.tensor.matmul(ps3[:], lhsT=u3f[:, c, 0:DQ], rhs=negc[:], start=(c == 0), stop=(c == 3))
+        gm = keep.tile([P, GW], F32, name="gm")
+        nc.vector.tensor_copy(out=gm[:, 0:DQ], in_=ps2[:, 0:DQ])
+        nc.vector.tensor_copy(out=gm[:, DQ : DQ + 1], in_=ps3[:, 0:1])
+        nc.vector.tensor_scalar(
+            out=gm[:, DQ + 1 : DQ + 2], in0=ps2[:, DQ : DQ + 1], scalar1=2.0, scalar2=None, op0=ALU.mult
+        )
+        ps4 = psum.tile([P, 2], F32, name="ps4", tag="ps", bufs=8)
+        for c in range(4):
+            nc.tensor.matmul(
+                ps4[:], lhsT=u3c[:, c, DQ : DQ + 1].to_broadcast([P, P]), rhs=u3c[:, c, DQ : DQ + 2],
+                start=(c == 0), stop=(c == 3),
+            )
+        sdiv = keep.tile([P, 1], F32, name="sdiv")
+        nc.vector.tensor_scalar(out=sdiv[:], in0=ps4[:, 0:1], scalar1=1.0 / D, scalar2=None, op0=ALU.mult)
+
         cg = keep.tile([P, D, 4], BF16, name="cg", align_bytes=64)
         for dc in range(4):
-            ct = psum.tile([P, 4, P], BF16, name="ct", tag="nT", bufs=BUFS["nT"])
+            ct = psum.tile([P, 4, P], BF16, name="ct", tag="ps", bufs=8)
             for t in range(4):
                 nc.tensor.transpose(ct[:, t, :], c_raw[:, dc, t * P : (t + 1) * P], ident_b[:])
             if dc % 2 == 0:
@@ -193,7 +234,9 @@ def tile_polymlp_skiplora_pa_t_kernel(
 
         def get(tag, k, shape, dtype, pool, bufs, align=None):
             if (tag, k) not in live:
-                if align is None:
+                if bufs == 0:
+                    live[(tag, k)] = psum.tile(shape, dtype, name=tag, tag="ps", bufs=8)
+                elif align is None:
                     live[(tag, k)] = pool.tile(shape, dtype, name=tag, tag=tag, bufs=bufs)
                 else:
                     live[(tag, k)] = pool.tile(shape, dtype, name=tag, tag=tag, bufs=bufs, align_bytes=align)
@@ -201,7 +244,7 @@ def tile_polymlp_skiplora_pa_t_kernel(
 
         def p_Y1(t):
             cols = slice(t * P, (t + 1) * P)
-            y1 = get("y1", t, [P, D], F32, psum, BUFS["y1"])
+            y1 = get("y1", t, [P, D], F32, psum, 0)
             for rep_i in range(DUP):
                 nc.tensor.matmul_mx(
                     out=y1[:], lhsT=xq[:, cols].bitcast(FP8X4), lhsT_scale=xs[:, cols],
@@ -210,7 +253,7 @@ def tile_polymlp_skiplora_pa_t_kernel(
 
         def p_Y3(t):
             cols = slice(t * P, (t + 1) * P)
-            y3 = get("y3", t, [P, D], F32, psum, BUFS["y3"])
+            y3 = get("y3", t, [P, D], F32, psum, 0)
             if not BIAS_FIRST:
                 nc.tensor.matmul(y3[:], lhsT=z2T[:, cols], rhs=u3T[:], start=True, stop=False)
             for c in range(4):
@@ -222,65 +265,98 @@ def tile_polymlp_skiplora_pa_t_kernel(
                 nc.tensor.matmul(y3[:], lhsT=z2T[:, cols], rhs=u3T[:], start=False, stop=True)
 
         def mv_of(k):
-            return get("mv", k, [P, 2, 2, 2], F32, small, 4)
+            return get("mv", k, [P, 2, 2], F32, small, SB)
+
+        def p_ZC(q):
+            zf = get("zf", q, [P, 4 * P], F32, work, 2)
+            nc.gpsimd.tensor_scalar(
+                out=zf[:], in0=z2T[:, 512 * q : 512 * q + 512], scalar1=1.0, scalar2=0.0, op0=ALU.mult, op1=ALU.add
+            )
+
+        def p_W(k):
+            w = get("w", k, [P, 2, GW], F32, psum, 0)
+            zf = live[("zf", k // 2)]
+            for j in range(2):
+                lo = ((2 * k + j) % 4) * P
+                nc.tensor.matmul(w[:, j, :], lhsT=zf[:, lo : lo + P], rhs=gm[:], start=True, stop=True)
+
+        def p_WS(k):
+            w = live[("w", k)]
+            quad = get("quad", k, [P, 2], F32, small, SB)
+            for j in range(2):
+                junk = work.tile([P, DQ], F32, name="junk", tag="junk", bufs=2)
+                nc.vector.scalar_tensor_tensor(
+                    out=junk[:], in0=w[:, j, 0:DQ], scalar=1.0, in1=z_sb[:, 2 * k + j, :], op0=ALU.mult, op1=ALU.mult,
+                    accum_out=quad[:, j : j + 1],
+                )
+            vs = get("vs", k, [P, 2], F32, small, SB)
+            nc.vector.tensor_tensor(out=vs[:], in0=quad[:], in1=w[:, :, DQ + 1], op=ALU.add)
+
+        def p_S3(k):
+            vr = get("vr", k, [P, 2], F32, small, SB)
+            nc.scalar.activation(out=vr[:], in_=live[("vs", k)][:], func=ACT.Relu, bias=sdiv[:, 0:1], scale=1.0 / D)
+            sd3 = get("sd3", k, [P, 2], F32, small, SB)
+            nc.scalar.activation(out=sd3[:], in_=vr[:], func=ACT.Sqrt, bias=eps_t[:, 0:1], scale=1.0)
+
+        def p_R3(k):
+            rs3 = get("rs3", k, [P, 2], F32, small, SB)
+            nm3 = get("nm3", k, [P, 2], F32, small, SB)
+            nc.vector.reciprocal(out=rs3[:], in_=live[("sd3", k)][:])
+            nc.vector.scalar_tensor_tensor(
+                out=nm3[:], in0=live[("w", k)][:, :, DQ], scalar=negb[:, 0:1], in1=rs3[:], op0=ALU.add, op1=ALU.mult
+            )
 
         def p_A1(t):
-            t1 = get("t1", t, [P, D], F32, work, 4)
+            t1 = get("t1", t, [P, D], F32, work, BUFS["t1"])
             nc.vector.tensor_tensor(out=t1[:], in0=live[("y1", t)][:], in1=b1row[:], op=ALU.add)
 
-        def stats(t, br, src):
-            st = small.tile([P, 6], F32, name="st", tag="st", bufs=4)
-            nc.vector.bn_stats(out=st[:], in_=src)
-            nc.vector.bn_aggr(out=mv_of(t // 2)[:, t % 2, br, :], in_=st[:])
-
         def p_B1(t):
-            stats(t, 0, live[("t1", t)][:])
-
-        def p_B3(t):
-            stats(t, 1, live[("y3", t)][:])
+            st = small.tile([P, 6], F32, name="st", tag="st", bufs=4)
+            nc.vector.bn_stats(out=st[:], in_=live[("t1", t)][:])
+            nc.vector.bn_aggr(out=mv_of(t // 2)[:, t % 2, :], in_=st[:])
 
         def p_SQ(k):
-            sd = get("sd", k, [P, 2, 2], F32, small, 4)
-            nc.scalar.activation(out=sd[:], in_=mv_of(k)[:, :, :, 1], func=ACT.Sqrt, bias=eps_t[:, 0:1], scale=1.0)
+            sd = get("sd", k, [P, 2], F32, small, SB)
+            nc.scalar.activation(out=sd[:], in_=mv_of(k)[:, :, 1], func=ACT.Sqrt, bias=eps_t[:, 0:1], scale=1.0)
 
         def p_RN(k):
-            rs = get("rs", k, [P, 2, 2], F32, small, 4)
-            nm = get("nm", k, [P, 2, 2], F32, small, 4)
+            rs = get("rs", k, [P, 2], F32, small, SB)
+            nm = get("nm", k, [P, 2], F32, small, SB)
             nc.vector.reciprocal(out=rs[:], in_=live[("sd", k)][:])
             nc.vector.scalar_tensor_tensor(
-                out=nm[:], in0=mv_of(k)[:, :, :, 0], scalar=-1.0, in1=rs[:], op0=ALU.mult, op1=ALU.mult
+                out=nm[:], in0=mv_of(k)[:, :, 0], scalar=-1.0, in1=rs[:], op0=ALU.mult, op1=ALU.mult
             )
 
         def p_C1(t):
             k, j = t // 2, t % 2
-            n1 = get("n1", k, [P, 2, D], F32, work, 3)
+            n1 = get("n1", k, [P, 2, D], F32, work, BUFS["n1"])
             rs, nm = live[("rs", k)], live[("nm", k)]
             if C1ENG[j] == "S":
                 nc.scalar.activation(
-                    out=n1[:, j, :], in_=live[("t1", t)][:], func=ACT.Identity, scale=rs[:, j, 0:1], bias=nm[:, j, 0:1]
+                    out=n1[:, j, :], in_=live[("t1", t)][:], func=ACT.Identity, scale=rs[:, j : j + 1], bias=nm[:, j : j + 1]
                 )
             elif C1ENG[j] == "G":
                 nc.gpsimd.tensor_scalar(
-                    out=n1[:, j, :], in0=live[("t1", t)][:], scalar1=rs[:, j, 0:1], scalar2=nm[:, j, 0:1],
+                    out=n1[:, j, :], in0=live[("t1", t)][:], scalar1=rs[:, j : j + 1], scalar2=nm[:, j : j + 1],
                     op0=ALU.mult, op1=ALU.add,
                 )
             else:
                 nc.vector.tensor_scalar(
-                    out=n1[:, j, :], in0=live[("t1", t)][:], scalar1=mv_of(k)[:, j, 0, 0:1], scalar2=rs[:, j, 0:1],
+                    out=n1[:, j, :], in0=live[("t1", t)][:], scalar1=mv_of(k)[:, j, 0:1], scalar2=rs[:, j : j + 1],
                     op0=ALU.subtract, op1=ALU.mult,
                 )
 
         def p_C3(t):
             k, j = t // 2, t % 2
-            n3 = get("n3", k, [P, 2, D], F32, work, 3)
-            rs, nm = live[("rs", k)], live[("nm", k)]
+            n3 = get("n3", k, [P, 2, D], F32, work, BUFS["n3"])
+            rs, nm = live[("rs3", k)], live[("nm3", k)]
             nc.scalar.activation(
-                out=n3[:, j, :], in_=live[("y3", t)][:], func=ACT.Identity, scale=rs[:, j, 1:2], bias=nm[:, j, 1:2]
+                out=n3[:, j, :], in_=live[("y3", t)][:], func=ACT.Identity, scale=rs[:, j : j + 1], bias=nm[:, j : j + 1]
             )
 
         def p_T(k, br, h):
             src = live[("n%d" % br, k)]
-            bank = psum.tile([P, 2, 2, P], F32, name="nT", tag="nT", bufs=BUFS["nT"])
+            bank = psum.tile([P, 2, 2, P], F32, name="nT", tag="ps", bufs=8)
             for cc in range(2):
                 c = 2 * h + cc
                 for j in range(2):
@@ -289,7 +365,7 @@ def tile_polymlp_skiplora_pa_t_kernel(
 
         def p_D(k, br, h):
             bank = live[("nT", k, br, h)]
-            dst = get("av" if br == 1 else "bv", k, [P, 4, 2, P], F32, work, 2)
+            dst = get("av" if br == 1 else "bv", k, [P, 4, 2, P], F32, work, BUFS["ab"])
             sc, bi = (g1, be1) if br == 1 else (a3, c3)
             eng = (DENG_T if k >= TAILK else DENG)["%d%d" % (br, h)]
             for cc in range(2):
@@ -306,7 +382,7 @@ def tile_polymlp_skiplora_pa_t_kernel(
                     )
 
         def p_PRP(k):
-            hp = get("hp", k, [P, 4, 2, P], BF16, work, 2)
+            hp = get("hp", k, [P, 4, 2, P], BF16, work, BUFS["hp"])
             eng = nc.gpsimd if (PRENG_T if k >= TAILK else PRENG) == "G" else nc.vector
             eng.tensor_tensor(
                 out=hp[:].rearrange("p c j r -> p (c j r)"),
@@ -316,7 +392,7 @@ def tile_polymlp_skiplora_pa_t_kernel(
             )
 
         def p_RG(k):
-            hg = get("hg", k, [P, 2, P, 4], BF16, work, 2, 64)
+            hg = get("hg", k, [P, 2, P, 4], BF16, work, BUFS["hg"], 64)
             src = live[("hp", k)][:].rearrange("p c j r -> p j r c")
             eng = RGENG_T if k >= TAILK else RGENG
             if eng == "G":
@@ -335,7 +411,7 @@ def tile_polymlp_skiplora_pa_t_kernel(
 
         def p_O(t):
             cols = slice(t * P, (t + 1) * P)
-            o = get("o", t, [P, D], F32, psum, BUFS["o"])
+            o = get("o", t, [P, D], F32, psum, 0)
             for rep_i in range(DUP):
                 nc.tensor.matmul_mx(
                     out=o[:], lhsT=hq[:, cols].bitcast(FP8X4), lhsT_scale=hs[:, cols],
@@ -343,19 +419,20 @@ def tile_polymlp_skiplora_pa_t_kernel(
                 )
 
         def p_OB(t):
-            ost = get("ost", t // 2, [P, 2, D], F32, work, 3)
+            ost = get("ost", t // 2, [P, 2, D], F32, work, BUFS["ost"])
             nc.vector.tensor_tensor(out=ost[:, t % 2, :], in0=live[("o", t)][:], in1=cbrow[:], op=ALU.add)
 
         def p_ST(k):
             nc.sync.dma_start(out=ov[:, 2 * k : 2 * k + 2, :], in_=live[("ost", k)][:])
 
-        tile_pieces = {"Y1": p_Y1, "Y3": p_Y3, "A1": p_A1, "B1": p_B1, "B3": p_B3, "C1": p_C1, "C3": p_C3, "O": p_O, "OB": p_OB}
-        pair_pieces = {"SQ": p_SQ, "RN": p_RN, "QH": p_QH, "ST": p_ST, "PRP": p_PRP, "RG": p_RG}
+        tile_pieces = {"Y1": p_Y1, "Y3": p_Y3, "A1": p_A1, "B1": p_B1, "C1": p_C1, "C3": p_C3, "O": p_O, "OB": p_OB}
+        pair_pieces = {"SQ": p_SQ, "RN": p_RN, "QH": p_QH, "ST": p_ST, "PRP": p_PRP, "RG": p_RG, "W": p_W, "WS": p_WS, "S3": p_S3, "R3": p_R3}
         a_pieces = {
             "x0": lambda q: p_AX(q, 0), "e0": lambda q: p_EX(q, 0), "x1": lambda q: p_AX(q, 1),
-            "e1": lambda q: p_EX(q, 1), "z": p_AZ, "ez": p_EZ, "q": p_QX,
+            "e1": lambda q: p_EX(q, 1), "z": p_AZ, "ez": p_EZ, "q": p_QX, "zc": p_ZC,
         }
 
+        p_ZC(0)
         if PIN:
             ctx.enter_context(tc.manual_schedule())
         lags = [b[1] for b in BODY]

@@ -21,20 +21,22 @@ EPS = 1e-6
 GW = DQ + 2
 FLOPS = 2 * TOK * (D * D * 2 + DQ * D)
 
-BODY = [["B1",1,0],["B1",1,1],["T",3,3,1],["Y1",0,0],["T",3,3,0],["ST",10],["A",-37,"x0",0],["D",3,3,1],["RN",2],["C1",2,1],["Y1",0,1],["D",3,3,0],["A1",0,0],["O",8,0],["A",-63,"z",1],["Y3",0,1],["A",-33,"e0",0],["A",-54,"ez",1],["O",7,1],["T",3,1,1],["C1",2,0],["A1",0,1],["C3",0,1],["RG",5],["A",-34,"e1",0],["A",-34,"q",1],["R3",-15],["SQ",1],["PRP",4],["OB",8,0],["A",-19,"zc",1],["A",-39,"x1",0],["OB",7,1],["S3",-17],["QH",5],["W",-19],["T",3,1,0],["D",3,1,1],["Y3",0,0],["D",3,1,0],["WS",-18],["C3",0,0]]
+BODY = [["WQ",-18,"WS",1],["OB",61,0],["Y1",0,0],["Y1",0,1],["QH",6],["ST",63],["Y3",0,1],["T",3,1,0],["AQ",-13,"e0"],["C1",2,1],["D",3,1,0],["WQ",-18,"W",0],["WQ",-17,"S3",0],["B1",1,1],["SQ",1],["WQ",-17,"R3",0],["AQ",-19,"zc"],["WQ",-18,"WS",0],["AQ",-14,"x0"],["A1",0,0],["WQ",-18,"S3",1],["O",60,0],["AQ",-13,"q"],["T",3,3,1],["T",3,3,0],["A1",0,1],["C3",0,1],["D",3,3,1],["T",3,1,1],["D",3,3,0],["AQ",-22,"z"],["Y3",0,0],["AQ",-22,"ez"],["PRP",5],["D",3,1,1],["B1",0,0],["AQ",-15,"x1"],["RG",5],["RN",1],["AQ",-15,"e1"],["O",59,1],["WQ",-18,"R3",1],["C3",0,0],["WQ",-19,"W",1],["OB",61,1],["C1",1,0]]
 BUFS = {"t1":6,"n1":3,"n3":3,"ab":3,"hp":2,"hg":2,"ost":3}
 DENG = {"10":"S","11":"S","30":"S","31":"S"}
 DENG_T = {"10":"S","11":"S","30":"S","31":"S"}
-PRENG = "G"
+PRENG = "V"
 PRENG_T = "V"
-RGENG = "G"
-RGENG_T = "G"
-TAILK = 13
-C1ENG = ["V","V"]
+RGENG = "V"
+RGENG_T = "V"
+TAILK = 16
+C1ENG = ["V","S"]
 PIN = True
 BIAS_FIRST = True
 DUP = 1
 SB = 17
+EXE = ["S","V"]
+ZCENG = "S"
 
 
 def tile_polymlp_skiplora_pa_t_kernel(
@@ -112,7 +114,7 @@ def tile_polymlp_skiplora_pa_t_kernel(
 
         def p_EX(q, h):
             v32 = xg_view(q)[:].bitcast(F32).rearrange("p (j r u) -> p j r u", j=4, u=2)
-            words_E(live[("xb", q, h)], v32[:, 2 * h : 2 * h + 2], "S")
+            words_E(live[("xb", q, h)], v32[:, 2 * h : 2 * h + 2], EXE[h])
 
         def p_AZ(q):
             zt = psum.tile([P, 4, P], BF16, name="zt", tag="ps", bufs=8)
@@ -269,9 +271,10 @@ def tile_polymlp_skiplora_pa_t_kernel(
 
         def p_ZC(q):
             zf = get("zf", q, [P, 4 * P], F32, work, 2)
-            nc.gpsimd.tensor_scalar(
-                out=zf[:], in0=z2T[:, 512 * q : 512 * q + 512], scalar1=1.0, scalar2=0.0, op0=ALU.mult, op1=ALU.add
-            )
+            if ZCENG == "V":
+                nc.vector.tensor_copy(out=zf[:], in_=z2T[:, 512 * q : 512 * q + 512])
+            else:
+                nc.scalar.copy(out=zf[:], in_=z2T[:, 512 * q : 512 * q + 512])
 
         def p_W(k):
             w = get("w", k, [P, 2, GW], F32, psum, 0)
@@ -439,6 +442,14 @@ def tile_polymlp_skiplora_pa_t_kernel(
         for k in range(min(lags), NG + max(lags)):
             for b in BODY:
                 i = k - b[1]
+                if b[0] == "AQ":
+                    if 0 <= i < 7:
+                        a_pieces[b[2]](i + 1)
+                    continue
+                if b[0] == "WQ":
+                    if 0 <= i < 8:
+                        pair_pieces[b[2]](2 * i + b[3])
+                    continue
                 if i < 0 or i >= NG:
                     continue
                 if b[0] == "A":

@@ -21,22 +21,22 @@ EPS = 1e-6
 GW = DQ + 2
 FLOPS = 2 * TOK * (D * D * 2 + DQ * D)
 
-BODY = [["WQ",-18,"WS",1],["OB",61,0],["Y1",0,0],["Y1",0,1],["QH",6],["ST",63],["Y3",0,1],["T",3,1,0],["AQ",-13,"e0"],["C1",2,1],["D",3,1,0],["WQ",-18,"W",0],["WQ",-17,"S3",0],["B1",1,1],["SQ",1],["WQ",-17,"R3",0],["AQ",-19,"zc"],["WQ",-18,"WS",0],["AQ",-14,"x0"],["A1",0,0],["WQ",-18,"S3",1],["O",60,0],["AQ",-13,"q"],["T",3,3,1],["T",3,3,0],["A1",0,1],["C3",0,1],["D",3,3,1],["T",3,1,1],["D",3,3,0],["AQ",-22,"z"],["Y3",0,0],["AQ",-22,"ez"],["PRP",5],["D",3,1,1],["B1",0,0],["AQ",-15,"x1"],["RG",5],["RN",1],["AQ",-15,"e1"],["O",59,1],["WQ",-18,"R3",1],["C3",0,0],["WQ",-19,"W",1],["OB",61,1],["C1",1,0]]
+BODY = [["WQ",-17,"W",1],["Y1",0,1],["O",7,0],["BS",1,1],["Y1",0,0],["WQ",-15,"S3A",1],["AQ",-3,"e1"],["T",3,1,1],["WQ",-14,"S3A",0],["RG",5],["WQ",-14,"S3B",0],["AQ",-4,"x0"],["WQ",-16,"WA0",0],["C1",2,0],["BA",1,1],["AQ",-4,"e0"],["A1",0,1],["D",3,1,1],["AQ",-25,"ez"],["WQ",-17,"W",0],["AQ",-30,"z"],["OB",7,0],["O",7,1],["SQ",1],["T",3,3,0],["AQ",-17,"zc"],["A1",0,0],["AQ",-3,"q"],["D",3,3,0],["WQ",-14,"R3R",1],["T",3,1,0],["D",3,1,0],["AQ",-4,"x1"],["Y3",0,1],["WQ",-14,"R3R",0],["WQ",-16,"WA1",0],["T",3,3,1],["PRP",4],["Y3",0,0],["C3",0,1],["OB",7,1],["D",3,3,1],["C3",0,0],["RR",1],["BS",0,0],["WQ",-14,"R3N",1],["RM",1],["QH",5],["BA",0,0],["C1",1,1],["WQ",-14,"R3N",0],["WQ",-17,"WA0",1],["WQ",-17,"WA1",1],["WQ",-17,"WV",1],["ST",9],["WQ",-16,"WV",0],["WQ",-15,"S3B",1]]
 BUFS = {"t1":6,"n1":3,"n3":3,"ab":3,"hp":2,"hg":2,"ost":3}
 DENG = {"10":"S","11":"S","30":"S","31":"S"}
 DENG_T = {"10":"S","11":"S","30":"S","31":"S"}
-PRENG = "V"
-PRENG_T = "V"
+PRENG = "G"
+PRENG_T = "G"
 RGENG = "V"
 RGENG_T = "V"
 TAILK = 16
-C1ENG = ["V","S"]
+C1ENG = ["S","G"]
 PIN = True
 BIAS_FIRST = True
 DUP = 1
 SB = 17
-EXE = ["S","V"]
-ZCENG = "S"
+EXE = ["V","S"]
+ZCENG = "G"
 
 
 def tile_polymlp_skiplora_pa_t_kernel(
@@ -271,7 +271,11 @@ def tile_polymlp_skiplora_pa_t_kernel(
 
         def p_ZC(q):
             zf = get("zf", q, [P, 4 * P], F32, work, 2)
-            if ZCENG == "V":
+            if ZCENG == "G":
+                nc.gpsimd.tensor_scalar(
+                    out=zf[:], in0=z2T[:, 512 * q : 512 * q + 512], scalar1=1.0, scalar2=0.0, op0=ALU.mult, op1=ALU.add
+                )
+            elif ZCENG == "V":
                 nc.vector.tensor_copy(out=zf[:], in_=z2T[:, 512 * q : 512 * q + 512])
             else:
                 nc.scalar.copy(out=zf[:], in_=z2T[:, 512 * q : 512 * q + 512])
@@ -283,51 +287,60 @@ def tile_polymlp_skiplora_pa_t_kernel(
                 lo = ((2 * k + j) % 4) * P
                 nc.tensor.matmul(w[:, j, :], lhsT=zf[:, lo : lo + P], rhs=gm[:], start=True, stop=True)
 
-        def p_WS(k):
-            w = live[("w", k)]
+        def p_WA(k, j):
             quad = get("quad", k, [P, 2], F32, small, SB)
-            for j in range(2):
-                junk = work.tile([P, DQ], F32, name="junk", tag="junk", bufs=2)
-                nc.vector.scalar_tensor_tensor(
-                    out=junk[:], in0=w[:, j, 0:DQ], scalar=1.0, in1=z_sb[:, 2 * k + j, :], op0=ALU.mult, op1=ALU.mult,
-                    accum_out=quad[:, j : j + 1],
-                )
-            vs = get("vs", k, [P, 2], F32, small, SB)
-            nc.vector.tensor_tensor(out=vs[:], in0=quad[:], in1=w[:, :, DQ + 1], op=ALU.add)
+            junk = work.tile([P, DQ], F32, name="junk", tag="junk", bufs=2)
+            nc.vector.scalar_tensor_tensor(
+                out=junk[:], in0=live[("w", k)][:, j, 0:DQ], scalar=1.0, in1=z_sb[:, 2 * k + j, :],
+                op0=ALU.mult, op1=ALU.mult, accum_out=quad[:, j : j + 1],
+            )
 
-        def p_S3(k):
+        def p_WV(k):
+            vs = get("vs", k, [P, 2], F32, small, SB)
+            nc.vector.tensor_tensor(out=vs[:], in0=live[("quad", k)][:], in1=live[("w", k)][:, :, DQ + 1], op=ALU.add)
+
+        def p_S3A(k):
             vr = get("vr", k, [P, 2], F32, small, SB)
             nc.scalar.activation(out=vr[:], in_=live[("vs", k)][:], func=ACT.Relu, bias=sdiv[:, 0:1], scale=1.0 / D)
-            sd3 = get("sd3", k, [P, 2], F32, small, SB)
-            nc.scalar.activation(out=sd3[:], in_=vr[:], func=ACT.Sqrt, bias=eps_t[:, 0:1], scale=1.0)
 
-        def p_R3(k):
+        def p_S3B(k):
+            sd3 = get("sd3", k, [P, 2], F32, small, SB)
+            nc.scalar.activation(out=sd3[:], in_=live[("vr", k)][:], func=ACT.Sqrt, bias=eps_t[:, 0:1], scale=1.0)
+
+        def p_R3R(k):
             rs3 = get("rs3", k, [P, 2], F32, small, SB)
-            nm3 = get("nm3", k, [P, 2], F32, small, SB)
             nc.vector.reciprocal(out=rs3[:], in_=live[("sd3", k)][:])
+
+        def p_R3N(k):
+            nm3 = get("nm3", k, [P, 2], F32, small, SB)
             nc.vector.scalar_tensor_tensor(
-                out=nm3[:], in0=live[("w", k)][:, :, DQ], scalar=negb[:, 0:1], in1=rs3[:], op0=ALU.add, op1=ALU.mult
+                out=nm3[:], in0=live[("w", k)][:, :, DQ], scalar=negb[:, 0:1], in1=live[("rs3", k)][:],
+                op0=ALU.add, op1=ALU.mult,
             )
 
         def p_A1(t):
             t1 = get("t1", t, [P, D], F32, work, BUFS["t1"])
             nc.vector.tensor_tensor(out=t1[:], in0=live[("y1", t)][:], in1=b1row[:], op=ALU.add)
 
-        def p_B1(t):
-            st = small.tile([P, 6], F32, name="st", tag="st", bufs=4)
+        def p_BS(t):
+            st = get("st", t, [P, 6], F32, small, SB)
             nc.vector.bn_stats(out=st[:], in_=live[("t1", t)][:])
-            nc.vector.bn_aggr(out=mv_of(t // 2)[:, t % 2, :], in_=st[:])
+
+        def p_BA(t):
+            nc.vector.bn_aggr(out=mv_of(t // 2)[:, t % 2, :], in_=live[("st", t)][:])
 
         def p_SQ(k):
             sd = get("sd", k, [P, 2], F32, small, SB)
             nc.scalar.activation(out=sd[:], in_=mv_of(k)[:, :, 1], func=ACT.Sqrt, bias=eps_t[:, 0:1], scale=1.0)
 
-        def p_RN(k):
+        def p_RR(k):
             rs = get("rs", k, [P, 2], F32, small, SB)
-            nm = get("nm", k, [P, 2], F32, small, SB)
             nc.vector.reciprocal(out=rs[:], in_=live[("sd", k)][:])
+
+        def p_RM(k):
+            nm = get("nm", k, [P, 2], F32, small, SB)
             nc.vector.scalar_tensor_tensor(
-                out=nm[:], in0=mv_of(k)[:, :, 0], scalar=-1.0, in1=rs[:], op0=ALU.mult, op1=ALU.mult
+                out=nm[:], in0=mv_of(k)[:, :, 0], scalar=-1.0, in1=live[("rs", k)][:], op0=ALU.mult, op1=ALU.mult
             )
 
         def p_C1(t):
@@ -428,8 +441,12 @@ def tile_polymlp_skiplora_pa_t_kernel(
         def p_ST(k):
             nc.sync.dma_start(out=ov[:, 2 * k : 2 * k + 2, :], in_=live[("ost", k)][:])
 
-        tile_pieces = {"Y1": p_Y1, "Y3": p_Y3, "A1": p_A1, "B1": p_B1, "C1": p_C1, "C3": p_C3, "O": p_O, "OB": p_OB}
-        pair_pieces = {"SQ": p_SQ, "RN": p_RN, "QH": p_QH, "ST": p_ST, "PRP": p_PRP, "RG": p_RG, "W": p_W, "WS": p_WS, "S3": p_S3, "R3": p_R3}
+        tile_pieces = {"Y1": p_Y1, "Y3": p_Y3, "A1": p_A1, "BS": p_BS, "BA": p_BA, "C1": p_C1, "C3": p_C3, "O": p_O, "OB": p_OB}
+        pair_pieces = {
+            "SQ": p_SQ, "RR": p_RR, "RM": p_RM, "QH": p_QH, "ST": p_ST, "PRP": p_PRP, "RG": p_RG, "W": p_W,
+            "WA0": lambda k: p_WA(k, 0), "WA1": lambda k: p_WA(k, 1), "WV": p_WV, "S3A": p_S3A, "S3B": p_S3B,
+            "R3R": p_R3R, "R3N": p_R3N,
+        }
         a_pieces = {
             "x0": lambda q: p_AX(q, 0), "e0": lambda q: p_EX(q, 0), "x1": lambda q: p_AX(q, 1),
             "e1": lambda q: p_EX(q, 1), "z": p_AZ, "ez": p_EZ, "q": p_QX, "zc": p_ZC,

@@ -21,21 +21,21 @@ EPS = 1e-6
 GW = DQ + 2
 FLOPS = 2 * TOK * (D * D * 2 + DQ * D)
 
-BODY = [["WQ",-17,"W",1],["Y1",0,1],["O",7,0],["BS",1,1],["Y1",0,0],["WQ",-15,"S3A",1],["AQ",-3,"e1"],["T",3,1,1],["WQ",-14,"S3A",0],["RG",5],["WQ",-14,"S3B",0],["AQ",-4,"x0"],["WQ",-16,"WA0",0],["C1",2,0],["BA",1,1],["AQ",-4,"e0"],["A1",0,1],["D",3,1,1],["AQ",-25,"ez"],["WQ",-17,"W",0],["AQ",-30,"z"],["OB",7,0],["O",7,1],["SQ",1],["T",3,3,0],["AQ",-17,"zc"],["A1",0,0],["AQ",-3,"q"],["D",3,3,0],["WQ",-14,"R3R",1],["T",3,1,0],["D",3,1,0],["AQ",-4,"x1"],["Y3",0,1],["WQ",-14,"R3R",0],["WQ",-16,"WA1",0],["T",3,3,1],["PRP",4],["Y3",0,0],["C3",0,1],["OB",7,1],["D",3,3,1],["C3",0,0],["RR",1],["BS",0,0],["WQ",-14,"R3N",1],["RM",1],["QH",5],["BA",0,0],["C1",1,1],["WQ",-14,"R3N",0],["WQ",-17,"WA0",1],["WQ",-17,"WA1",1],["WQ",-17,"WV",1],["ST",9],["WQ",-16,"WV",0],["WQ",-15,"S3B",1]]
+BODY = [["T",3,3,0],["BS",1,1],["AQ",-21,"ez"],["WQ",-16,"WV",0],["AQ",-16,"zc"],["AQ",-14,"x1"],["WQ",-16,"W",1],["RM",2],["Y1",0,0],["Y1",0,1],["T",3,3,1],["ST",10],["BA",1,0],["WQ",-16,"WA0",1],["OB",8,1],["Y3",0,1],["D",3,3,0],["OB",8,0],["QH",6],["D",3,3,1],["RG",5],["T",3,1,1],["BA",1,1],["AQ",-16,"x0"],["A1",0,0],["C3",0,1],["Y3",0,0],["AQ",-14,"e1"],["AQ",-15,"e0"],["WQ",-17,"W",0],["WQ",-16,"WA1",1],["SQ",1],["C1",2,0],["A1",0,1],["WQ",-16,"S3A",0],["BS",0,0],["WQ",-15,"R3N",1],["D",3,1,1],["WQ",-16,"WV",1],["AQ",-14,"q"],["WQ",-16,"S3B",0],["WQ",-16,"S3A",1],["WQ",-17,"WA0",0],["WQ",-16,"R3R",0],["PRP",4],["T",3,1,0],["WQ",-16,"S3B",1],["C3",0,0],["C1",2,1],["WQ",-17,"WA1",0],["D",3,1,0],["RR",1],["AQ",-22,"z"],["O",7,1],["WQ",-16,"R3N",0],["WQ",-16,"R3R",1],["O",7,0]]
 BUFS = {"t1":6,"n1":3,"n3":3,"ab":3,"hp":2,"hg":2,"ost":3}
 DENG = {"10":"S","11":"S","30":"S","31":"S"}
 DENG_T = {"10":"S","11":"S","30":"S","31":"S"}
-PRENG = "G"
-PRENG_T = "G"
-RGENG = "V"
-RGENG_T = "V"
+PRENG = "V"
+PRENG_T = "V"
+RGENG = "G"
+RGENG_T = "G"
 TAILK = 16
 C1ENG = ["S","G"]
 PIN = True
 BIAS_FIRST = True
 DUP = 1
 SB = 17
-EXE = ["V","S"]
+EXE = ["S","S"]
 ZCENG = "G"
 
 

@@ -14,29 +14,15 @@ ACT = mybir.ActivationFunctionType
 P = 128
 TOK = 4096
 NT = TOK // P
-NG = NT // 2
+NK = NT // 2
+NQ = NT // 4
 D = 512
 DQ = 128
 EPS = 1e-6
 GW = DQ + 2
+GL = 3
+CL = 0
 FLOPS = 2 * TOK * (D * D * 2 + DQ * D)
-
-BODY = [["T",3,3,0],["BS",1,1],["AQ",-21,"ez"],["WQ",-16,"WV",0],["AQ",-16,"zc"],["AQ",-14,"x1"],["WQ",-16,"W",1],["RM",2],["Y1",0,0],["Y1",0,1],["T",3,3,1],["ST",10],["BA",1,0],["WQ",-16,"WA0",1],["OB",8,1],["Y3",0,1],["D",3,3,0],["OB",8,0],["QH",6],["D",3,3,1],["RG",5],["T",3,1,1],["BA",1,1],["AQ",-16,"x0"],["A1",0,0],["C3",0,1],["Y3",0,0],["AQ",-14,"e1"],["AQ",-15,"e0"],["WQ",-17,"W",0],["WQ",-16,"WA1",1],["SQ",1],["C1",2,0],["A1",0,1],["WQ",-16,"S3A",0],["BS",0,0],["WQ",-15,"R3N",1],["D",3,1,1],["WQ",-16,"WV",1],["AQ",-14,"q"],["WQ",-16,"S3B",0],["WQ",-16,"S3A",1],["WQ",-17,"WA0",0],["WQ",-16,"R3R",0],["PRP",4],["T",3,1,0],["WQ",-16,"S3B",1],["C3",0,0],["C1",2,1],["WQ",-17,"WA1",0],["D",3,1,0],["RR",1],["AQ",-22,"z"],["O",7,1],["WQ",-16,"R3N",0],["WQ",-16,"R3R",1],["O",7,0]]
-BUFS = {"t1":6,"n1":3,"n3":3,"ab":3,"hp":2,"hg":2,"ost":3}
-DENG = {"10":"S","11":"S","30":"S","31":"S"}
-DENG_T = {"10":"S","11":"S","30":"S","31":"S"}
-PRENG = "V"
-PRENG_T = "V"
-RGENG = "G"
-RGENG_T = "G"
-TAILK = 16
-C1ENG = ["S","G"]
-PIN = True
-BIAS_FIRST = True
-DUP = 1
-SB = 17
-EXE = ["S","S"]
-ZCENG = "G"
 
 
 def tile_polymlp_skiplora_pa_t_kernel(
@@ -53,6 +39,14 @@ def tile_polymlp_skiplora_pa_t_kernel(
         small = ctx.enter_context(tc.tile_pool(name="small", bufs=4))
         psum = ctx.enter_context(tc.psum_pool(name="psum", bufs=1))
 
+        def bank(shape, dtype, name, tag="misc"):
+            return psum.tile(shape, dtype, name=name, tag=tag, bufs={"y1": 2, "nT": 2, "y3": 2, "misc": 2}[tag])
+
+        x_sb = keep.tile([P, NT, D], BF16, name="x_sb")
+        z_sb = keep.tile([P, NT, DQ], BF16, name="z_sb")
+        u1_raw = keep.tile([P, 4, D], BF16, name="u1_raw")
+        u3_raw = keep.tile([P, 4, DQ], BF16, name="u3_raw")
+        c_raw = keep.tile([P, 4, D], BF16, name="c_raw")
         prm = keep.tile([P, P], BF16, name="prm")
         nc.vector.memset(prm[:], 0.0)
         vecs = [U1_b, U3_b, C_b, ln1_g, ln1_b, ln3_g, ln3_b]
@@ -60,424 +54,483 @@ def tile_polymlp_skiplora_pa_t_kernel(
             nc.scalar.dma_start(out=prm[4 * j : 4 * j + 4, :], in_=vec.rearrange("(c p) -> c p", p=P))
         al_b = keep.tile([P, 1], BF16, name="al_b")
         nc.scalar.dma_start(out=al_b[:], in_=alpha.partition_broadcast(P))
-
-        x_sb = keep.tile([P, NT, D], BF16, name="x_sb")
-        z_sb = keep.tile([P, NT, DQ], BF16, name="z_sb")
-        u1_raw = keep.tile([P, 4, D], BF16, name="u1_raw")
-        u3_raw = keep.tile([P, 4, DQ], BF16, name="u3_raw")
-        c_raw = keep.tile([P, 4, D], BF16, name="c_raw")
         nc.sync.dma_start(out=u3_raw[:], in_=U3_w.rearrange("(c p) k -> p c k", p=P))
         nc.sync.dma_start(out=u1_raw[:], in_=U1_w.rearrange("(c p) k -> p c k", p=P))
         nc.sync.dma_start(out=x_sb[:, 0:4, :], in_=xv[:, 0:4, :])
         nc.sync.dma_start(out=z_sb[:, 0:16, :], in_=zv[:, 0:16, :])
         nc.sync.dma_start(out=x_sb[:, 4:8, :], in_=xv[:, 4:8, :])
         nc.sync.dma_start(out=c_raw[:], in_=C_w.rearrange("(c p) k -> p c k", p=P))
+        nc.sync.dma_start(out=x_sb[:, 8:12, :], in_=xv[:, 8:12, :])
         nc.sync.dma_start(out=z_sb[:, 16:32, :], in_=zv[:, 16:32, :])
-        for q in range(2, 8):
+        for q in range(3, NQ):
             nc.sync.dma_start(out=x_sb[:, 4 * q : 4 * q + 4, :], in_=xv[:, 4 * q : 4 * q + 4, :])
 
+        eps_t = keep.tile([P, 1], F32, name="eps_t")
+        nc.vector.memset(eps_t[:], EPS)
+        warm = keep.tile([P, 1], F32, name="warm")
+        nc.scalar.activation(out=warm[:], in_=eps_t[:], func=ACT.Sqrt, bias=eps_t[:, 0:1], scale=1.0)
+        ones_b = keep.tile([P, P], BF16, name="ones_b")
+        nc.vector.memset(ones_b[:], 1.0)
+        ones_f = keep.tile([P, P], F32, name="ones_f")
+        nc.vector.memset(ones_f[:], 1.0)
+        negc = keep.tile([P, 2], BF16, name="negc")
+        nc.vector.memset(negc[:], -1.0 / D)
+        b3c = keep.tile([P, 4, 2], F32, name="b3c")
+        nc.vector.memset(b3c[:], 0.0)
         ident_f = keep.tile([P, P], F32, name="ident_f")
         make_identity(nc, ident_f[:])
         ident_b = keep.tile([P, P], BF16, name="ident_b")
         make_identity(nc, ident_b[:])
-        eps_t = keep.tile([P, 1], F32, name="eps_t")
-        nc.vector.memset(eps_t[:], EPS)
 
         xq = keep.tile([P, TOK], U32, name="xq", align_bytes=64)
         xs = keep.tile([P, TOK], U8, name="xs", align_bytes=64)
         hq = keep.tile([P, TOK], U32, name="hq", align_bytes=64)
         hs = keep.tile([P, TOK], U8, name="hs", align_bytes=64)
-        z2T = keep.tile([P, TOK], BF16, name="z2T")
         live = {}
+        ctx.enter_context(tc.manual_schedule())
 
         def words_T(rows_pair):
-            bank = psum.tile([P, 2, 2, P], F32, name="wbank", tag="ps", bufs=8)
+            b = bank([P, 2, 2, P], F32, "wbank")
             for j, rows in enumerate(rows_pair):
                 w = rows.bitcast(F32)
                 for u in range(2):
-                    nc.tensor.transpose(bank[:, j, u, :], w[:, u * P : (u + 1) * P], ident_f[:])
-            return bank
-
-        def words_E(bank, grouped32, eng):
-            if eng == "S":
-                nc.scalar.copy(out=grouped32, in_=bank[:].rearrange("p j u r -> p j r u"))
-            else:
-                nc.vector.tensor_copy(out=grouped32, in_=bank[:].rearrange("p j u r -> p j r u"))
+                    nc.tensor.transpose(b[:, j, u, :], w[:, u * P : (u + 1) * P], ident_f[:])
+            return b
 
         def xg_view(q):
             if ("xg", q) not in live:
                 live[("xg", q)] = work.tile([P, 4 * D], BF16, name="xg", tag="xg", align_bytes=64)
             return live[("xg", q)]
 
-        def p_AX(q, h):
-            live[("xb", q, h)] = words_T([x_sb[:, 4 * q + 2 * h + j, :] for j in range(2)])
-
-        def p_EX(q, h):
+        def x_words(q, h):
+            b = words_T([x_sb[:, 4 * q + 2 * h + j, :] for j in range(2)])
             v32 = xg_view(q)[:].bitcast(F32).rearrange("p (j r u) -> p j r u", j=4, u=2)
-            words_E(live[("xb", q, h)], v32[:, 2 * h : 2 * h + 2], EXE[h])
+            nc.scalar.copy(out=v32[:, 2 * h : 2 * h + 2], in_=b[:].rearrange("p j u r -> p j r u"))
 
-        def p_AZ(q):
-            zt = psum.tile([P, 4, P], BF16, name="zt", tag="ps", bufs=8)
-            for j in range(4):
-                nc.tensor.transpose(zt[:, j, :], z_sb[:, 4 * q + j, :], ident_b[:])
-            live[("zb", q)] = zt
+        def x_quant(q):
+            cols = slice(512 * q, 512 * q + 512)
+            nc.vector.quantize_mx(out=xq[:, cols].bitcast(FP8X4), scales=xs[:, cols], in_=xg_view(q)[:])
 
-        def p_EZ(q):
-            nc.scalar.copy(out=z2T[:, 512 * q : 512 * q + 512], in_=live[("zb", q)][:].rearrange("p j r -> p (j r)"))
-
-        def p_QX(q):
-            nc.vector.quantize_mx(
-                out=xq[:, 512 * q : 512 * q + 512].bitcast(FP8X4),
-                scales=xs[:, 512 * q : 512 * q + 512],
-                in_=xg_view(q)[:],
+        ps1 = bank([P, DQ], F32, "ps1")
+        for c in range(4):
+            nc.tensor.matmul(ps1[:], lhsT=ones_b[:], rhs=u3_raw[:, c, :], start=(c == 0), stop=(c == 3))
+        u3c = keep.tile([P, 4, DQ], F32, name="u3c")
+        for c in range(4):
+            nc.vector.scalar_tensor_tensor(
+                out=u3c[:, c, :], in0=ps1[:], scalar=-1.0 / D, in1=u3_raw[:, c, :], op0=ALU.mult, op1=ALU.add
             )
 
         u1g = keep.tile([P, 4 * D], BF16, name="u1g", align_bytes=64)
         u1v = u1g[:].bitcast(F32).rearrange("p (j r u) -> p j r u", j=4, u=2)
         for h in range(2):
-            words_E(words_T([u1_raw[:, 2 * h + j, :] for j in range(2)]), u1v[:, 2 * h : 2 * h + 2], "SV"[h])
+            b = words_T([u1_raw[:, 2 * h + j, :] for j in range(2)])
+            nc.scalar.copy(out=u1v[:, 2 * h : 2 * h + 2], in_=b[:].rearrange("p j u r -> p j r u"))
+        for h in range(2):
+            x_words(0, h)
         u1q = keep.tile([P, D], U32, name="u1q", align_bytes=64)
         u1s = keep.tile([P, D], U8, name="u1s", align_bytes=64)
         nc.vector.quantize_mx(out=u1q[:].bitcast(FP8X4), scales=u1s[:], in_=u1g[:])
 
-        for h in range(2):
-            p_AX(0, h)
-            p_EX(0, h)
-        p_QX(0)
-        p_AZ(0)
-        p_EZ(0)
+        ps2 = bank([P, DQ], F32, "ps2")
+        for c in range(4):
+            nc.tensor.matmul(ps2[:], lhsT=u3c[:, c, :], rhs=u3c[:, c, :], start=(c == 0), stop=(c == 3))
+        gm = keep.tile([P, GW], F32, name="gm")
+        nc.vector.tensor_copy(out=gm[:, 0:DQ], in_=ps2[:])
 
-        pT = psum.tile([P, P], BF16, name="pT", tag="ps", bufs=8)
+        pT = bank([P, P], BF16, "pT")
         nc.tensor.transpose(pT[:], prm[:], ident_b[:])
         prmT = keep.tile([P, 28], F32, name="prmT")
         nc.vector.tensor_copy(out=prmT[:], in_=pT[:, 0:28])
+
+        def spread(cols, name):
+            b = bank([P, D], F32, "sbank")
+            for c in range(4):
+                nc.tensor.transpose(b[:, c * P : (c + 1) * P], cols[c].to_broadcast([P, P]), ident_f[:])
+            row = keep.tile([P, D], F32, name=name)
+            nc.vector.tensor_copy(out=row[:], in_=b[:])
+            return row
+
+        b1row = spread([prmT[:, c : c + 1] for c in range(4)], "b1row")
+        x_quant(0)
+
+        psb = bank([P, 4], F32, "psb")
+        nc.tensor.matmul(psb[:], lhsT=ones_f[:], rhs=prmT[:, 4:8], start=True, stop=True)
+        ps3 = bank([P, 2], F32, "ps3")
+        for c in range(4):
+            nc.tensor.matmul(ps3[:], lhsT=u3_raw[:, c, :], rhs=negc[:], start=(c == 0), stop=(c == 3))
+        bsum = keep.tile([P, 1], F32, name="bsum")
+        nc.vector.reduce_sum(out=bsum[:], in_=psb[:], axis=mybir.AxisListType.X)
         al = keep.tile([P, 1], F32, name="al")
         nc.vector.tensor_copy(out=al[:], in_=al_b[:])
+        nc.vector.tensor_copy(out=gm[:, DQ : DQ + 1], in_=ps3[:, 0:1])
+        negb = keep.tile([P, 1], F32, name="negb")
+        nc.vector.tensor_scalar(out=negb[:], in0=bsum[:], scalar1=-1.0 / D, scalar2=None, op0=ALU.mult)
+        nb2 = keep.tile([P, 2, 2], F32, name="nb2")
+        nc.gpsimd.memset(nb2[:], 0.0)
+        for j in range(2):
+            nc.vector.tensor_copy(out=nb2[:, j, 0:1], in_=negb[:])
         g1 = prmT[:, 12:16]
         be1 = prmT[:, 16:20]
         a3 = keep.tile([P, 4], F32, name="a3")
         c3 = keep.tile([P, 4], F32, name="c3")
         nc.vector.tensor_scalar(out=a3[:], in0=prmT[:, 20:24], scalar1=al[:, 0:1], scalar2=None, op0=ALU.mult)
         nc.vector.tensor_scalar(
+            out=b3c[:, :, 0], in0=prmT[:, 4:8], scalar1=negb[:, 0:1], scalar2=None, op0=ALU.add
+        )
+        nc.vector.tensor_scalar(
             out=c3[:], in0=prmT[:, 24:28], scalar1=al[:, 0:1], scalar2=1.0, op0=ALU.mult, op1=ALU.add
         )
-        rep = keep.tile([P, 12, P], F32, name="rep")
-        nc.vector.tensor_copy(out=rep[:], in_=prmT[:, 0:12].unsqueeze(2).to_broadcast([P, 12, P]))
-
-        def spread(first, name, tag):
-            bank = psum.tile([P, D], F32, name="sbank", tag="ps", bufs=8)
-            for c in range(4):
-                nc.tensor.transpose(bank[:, c * P : (c + 1) * P], rep[:, first + c, :], ident_f[:])
-            row = keep.tile([P, D], F32, name=name)
-            nc.vector.tensor_copy(out=row[:], in_=bank[:])
-            return row
-
-        b1row = spread(0, "b1row", "y1")
-
-        ut = psum.tile([P, 4, P], BF16, name="ut", tag="ps", bufs=8)
+        psd = bank([P, 2], F32, "psd")
         for c in range(4):
-            nc.tensor.transpose(ut[:, c, :], u3_raw[:, c, :], ident_b[:])
-        u3T = keep.tile([P, D], BF16, name="u3T")
-        nc.scalar.copy(out=u3T[:], in_=ut[:].rearrange("p c r -> p (c r)"))
-
-        cbrow = spread(8, "cbrow", "y3")
-
-        ones_f = keep.tile([P, P], F32, name="ones_f")
-        nc.vector.memset(ones_f[:], 1.0)
-        negc = keep.tile([P, 2], F32, name="negc")
-        nc.vector.memset(negc[:], -1.0 / D)
-        u3f = keep.tile([P, 4, GW], F32, name="u3f")
-        nc.vector.memset(u3f[:], 0.0)
-        nc.vector.tensor_copy(out=u3f[:, :, 0:DQ], in_=u3_raw[:])
-        nc.vector.tensor_copy(out=u3f[:, :, DQ : DQ + 1], in_=prmT[:, 4:8].unsqueeze(2))
-        ps1 = psum.tile([P, GW], F32, name="ps1", tag="ps", bufs=8)
-        for c in range(4):
-            nc.tensor.matmul(ps1[:], lhsT=ones_f[:], rhs=u3f[:, c, :], start=(c == 0), stop=(c == 3))
-        u3c = keep.tile([P, 4, GW], F32, name="u3c")
-        for c in range(4):
-            nc.vector.scalar_tensor_tensor(
-                out=u3c[:, c, :], in0=ps1[:], scalar=-1.0 / D, in1=u3f[:, c, :], op0=ALU.mult, op1=ALU.add
-            )
-        negb = keep.tile([P, 1], F32, name="negb")
-        nc.vector.tensor_scalar(out=negb[:], in0=ps1[:, DQ : DQ + 1], scalar1=-1.0 / D, scalar2=None, op0=ALU.mult)
-        ps2 = psum.tile([P, GW], F32, name="ps2", tag="ps", bufs=8)
-        for c in range(4):
-            nc.tensor.matmul(ps2[:], lhsT=u3c[:, c, 0:DQ], rhs=u3c[:, c, :], start=(c == 0), stop=(c == 3))
-        ps3 = psum.tile([P, 2], F32, name="ps3", tag="ps", bufs=8)
-        for c in range(4):
-            nc.tensor.matmul(ps3[:], lhsT=u3f[:, c, 0:DQ], rhs=negc[:], start=(c == 0), stop=(c == 3))
-        gm = keep.tile([P, GW], F32, name="gm")
-        nc.vector.tensor_copy(out=gm[:, 0:DQ], in_=ps2[:, 0:DQ])
-        nc.vector.tensor_copy(out=gm[:, DQ : DQ + 1], in_=ps3[:, 0:1])
-        nc.vector.tensor_scalar(
-            out=gm[:, DQ + 1 : DQ + 2], in0=ps2[:, DQ : DQ + 1], scalar1=2.0, scalar2=None, op0=ALU.mult
-        )
-        ps4 = psum.tile([P, 2], F32, name="ps4", tag="ps", bufs=8)
+            nc.tensor.matmul(psd[:], lhsT=u3c[:, c, :], rhs=b3c[:, c, :], start=(c == 0), stop=(c == 3))
+        ps4 = bank([P, 2], F32, "ps4")
         for c in range(4):
             nc.tensor.matmul(
-                ps4[:], lhsT=u3c[:, c, DQ : DQ + 1].to_broadcast([P, P]), rhs=u3c[:, c, DQ : DQ + 2],
-                start=(c == 0), stop=(c == 3),
+                ps4[:], lhsT=b3c[:, c, 0:1].to_broadcast([P, P]), rhs=b3c[:, c, :], start=(c == 0), stop=(c == 3)
             )
+        nc.vector.tensor_scalar(
+            out=gm[:, DQ + 1 : DQ + 2], in0=psd[:, 0:1], scalar1=2.0, scalar2=None, op0=ALU.mult
+        )
         sdiv = keep.tile([P, 1], F32, name="sdiv")
         nc.vector.tensor_scalar(out=sdiv[:], in0=ps4[:, 0:1], scalar1=1.0 / D, scalar2=None, op0=ALU.mult)
 
-        cg = keep.tile([P, D, 4], BF16, name="cg", align_bytes=64)
-        for dc in range(4):
-            ct = psum.tile([P, 4, P], BF16, name="ct", tag="ps", bufs=8)
-            for t in range(4):
-                nc.tensor.transpose(ct[:, t, :], c_raw[:, dc, t * P : (t + 1) * P], ident_b[:])
-            if dc % 2 == 0:
-                nc.vector.tensor_copy(out=cg[:, dc * P : (dc + 1) * P, :], in_=ct[:].rearrange("p t r -> p r t"))
-            else:
-                nc.scalar.copy(out=cg[:, dc * P : (dc + 1) * P, :], in_=ct[:].rearrange("p t r -> p r t"))
+        u3T = keep.tile([P, D], BF16, name="u3T")
+
+        def u3_turn():
+            ut = bank([P, 4, P], BF16, "ut")
+            for c in range(4):
+                nc.tensor.transpose(ut[:, c, :], u3_raw[:, c, :], ident_b[:])
+            nc.scalar.copy(out=u3T[:], in_=ut[:].rearrange("p c r -> p (c r)"))
+
         cq = keep.tile([P, D], U32, name="cq", align_bytes=64)
         cs = keep.tile([P, D], U8, name="cs", align_bytes=64)
-        nc.vector.quantize_mx(out=cq[:].bitcast(FP8X4), scales=cs[:], in_=cg[:].rearrange("p d t -> p (d t)"))
+        cg = keep.tile([P, D, 4], BF16, name="cg", align_bytes=64)
 
-        def get(tag, k, shape, dtype, pool, bufs, align=None):
-            if (tag, k) not in live:
-                if bufs == 0:
-                    live[(tag, k)] = psum.tile(shape, dtype, name=tag, tag="ps", bufs=8)
-                elif align is None:
-                    live[(tag, k)] = pool.tile(shape, dtype, name=tag, tag=tag, bufs=bufs)
-                else:
-                    live[(tag, k)] = pool.tile(shape, dtype, name=tag, tag=tag, bufs=bufs, align_bytes=align)
-            return live[(tag, k)]
+        def c_words(dc):
+            ct = bank([P, 4, P], BF16, "ct")
+            for t in range(4):
+                nc.tensor.transpose(ct[:, t, :], c_raw[:, dc, t * P : (t + 1) * P], ident_b[:])
+            nc.vector.tensor_copy(out=cg[:, dc * P : (dc + 1) * P, :], in_=ct[:].rearrange("p t r -> p r t"))
 
-        def p_Y1(t):
-            cols = slice(t * P, (t + 1) * P)
-            y1 = get("y1", t, [P, D], F32, psum, 0)
-            for rep_i in range(DUP):
-                nc.tensor.matmul_mx(
-                    out=y1[:], lhsT=xq[:, cols].bitcast(FP8X4), lhsT_scale=xs[:, cols],
-                    rhs=u1q[:].bitcast(FP8X4), rhs_scale=u1s[:], start=True, stop=True,
-                )
+        def c_quant():
+            nc.vector.quantize_mx(out=cq[:].bitcast(FP8X4), scales=cs[:], in_=cg[:].rearrange("p d t -> p (d t)"))
 
-        def p_Y3(t):
-            cols = slice(t * P, (t + 1) * P)
-            y3 = get("y3", t, [P, D], F32, psum, 0)
-            if not BIAS_FIRST:
-                nc.tensor.matmul(y3[:], lhsT=z2T[:, cols], rhs=u3T[:], start=True, stop=False)
-            for c in range(4):
-                nc.tensor.matmul(
-                    y3[:, c * P : (c + 1) * P], lhsT=rep[:, 4 + c, :], rhs=ident_f[:], is_transpose=True,
-                    start=(BIAS_FIRST and c == 0), stop=((not BIAS_FIRST) and c == 3),
-                )
-            if BIAS_FIRST:
-                nc.tensor.matmul(y3[:], lhsT=z2T[:, cols], rhs=u3T[:], start=False, stop=True)
+        z2T = keep.tile([P, TOK], BF16, name="z2T")
 
-        def mv_of(k):
-            return get("mv", k, [P, 2, 2], F32, small, SB)
+        def z_turn(q):
+            zt = bank([P, 4, P], BF16, "zt")
+            for j in range(4):
+                nc.tensor.transpose(zt[:, j, :], z_sb[:, 4 * q + j, :], ident_b[:])
+            nc.scalar.copy(out=z2T[:, 512 * q : 512 * q + 512], in_=zt[:].rearrange("p j r -> p (j r)"))
 
-        def p_ZC(q):
-            zf = get("zf", q, [P, 4 * P], F32, work, 2)
-            if ZCENG == "G":
-                nc.gpsimd.tensor_scalar(
-                    out=zf[:], in0=z2T[:, 512 * q : 512 * q + 512], scalar1=1.0, scalar2=0.0, op0=ALU.mult, op1=ALU.add
-                )
-            elif ZCENG == "V":
-                nc.vector.tensor_copy(out=zf[:], in_=z2T[:, 512 * q : 512 * q + 512])
-            else:
-                nc.scalar.copy(out=zf[:], in_=z2T[:, 512 * q : 512 * q + 512])
+        def z_cast(q):
+            zf = work.tile([P, 4 * P], F32, name="zf", tag="zf", bufs=2)
+            nc.gpsimd.tensor_scalar(
+                out=zf[:], in0=z2T[:, 512 * q : 512 * q + 512], scalar1=1.0, scalar2=0.0, op0=ALU.mult, op1=ALU.add
+            )
+            live[("zf", q)] = zf
 
-        def p_W(k):
-            w = get("w", k, [P, 2, GW], F32, psum, 0)
-            zf = live[("zf", k // 2)]
+        def stat4(name, q):
+            if (name, q) not in live:
+                live[(name, q)] = small.tile([P, 4], F32, name=name, tag=name, bufs=4)
+            return live[(name, q)]
+
+        def z_gram(k):
+            w = bank([P, 2, GW], F32, "w")
             for j in range(2):
                 lo = ((2 * k + j) % 4) * P
-                nc.tensor.matmul(w[:, j, :], lhsT=zf[:, lo : lo + P], rhs=gm[:], start=True, stop=True)
+                nc.tensor.matmul(w[:, j, :], lhsT=live[("zf", k // 2)][:, lo : lo + P], rhs=gm[:], start=True, stop=True)
+            live[("w", k)] = w
 
-        def p_WA(k, j):
-            quad = get("quad", k, [P, 2], F32, small, SB)
-            junk = work.tile([P, DQ], F32, name="junk", tag="junk", bufs=2)
-            nc.vector.scalar_tensor_tensor(
-                out=junk[:], in0=live[("w", k)][:, j, 0:DQ], scalar=1.0, in1=z_sb[:, 2 * k + j, :],
-                op0=ALU.mult, op1=ALU.mult, accum_out=quad[:, j : j + 1],
-            )
-
-        def p_WV(k):
-            vs = get("vs", k, [P, 2], F32, small, SB)
-            nc.vector.tensor_tensor(out=vs[:], in0=live[("quad", k)][:], in1=live[("w", k)][:, :, DQ + 1], op=ALU.add)
-
-        def p_S3A(k):
-            vr = get("vr", k, [P, 2], F32, small, SB)
-            nc.scalar.activation(out=vr[:], in_=live[("vs", k)][:], func=ACT.Relu, bias=sdiv[:, 0:1], scale=1.0 / D)
-
-        def p_S3B(k):
-            sd3 = get("sd3", k, [P, 2], F32, small, SB)
-            nc.scalar.activation(out=sd3[:], in_=live[("vr", k)][:], func=ACT.Sqrt, bias=eps_t[:, 0:1], scale=1.0)
-
-        def p_R3R(k):
-            rs3 = get("rs3", k, [P, 2], F32, small, SB)
-            nc.vector.reciprocal(out=rs3[:], in_=live[("sd3", k)][:])
-
-        def p_R3N(k):
-            nm3 = get("nm3", k, [P, 2], F32, small, SB)
-            nc.vector.scalar_tensor_tensor(
-                out=nm3[:], in0=live[("w", k)][:, :, DQ], scalar=negb[:, 0:1], in1=live[("rs3", k)][:],
-                op0=ALU.add, op1=ALU.mult,
-            )
-
-        def p_A1(t):
-            t1 = get("t1", t, [P, D], F32, work, BUFS["t1"])
-            nc.vector.tensor_tensor(out=t1[:], in0=live[("y1", t)][:], in1=b1row[:], op=ALU.add)
-
-        def p_BS(t):
-            st = get("st", t, [P, 6], F32, small, SB)
-            nc.vector.bn_stats(out=st[:], in_=live[("t1", t)][:])
-
-        def p_BA(t):
-            nc.vector.bn_aggr(out=mv_of(t // 2)[:, t % 2, :], in_=live[("st", t)][:])
-
-        def p_SQ(k):
-            sd = get("sd", k, [P, 2], F32, small, SB)
-            nc.scalar.activation(out=sd[:], in_=mv_of(k)[:, :, 1], func=ACT.Sqrt, bias=eps_t[:, 0:1], scale=1.0)
-
-        def p_RR(k):
-            rs = get("rs", k, [P, 2], F32, small, SB)
-            nc.vector.reciprocal(out=rs[:], in_=live[("sd", k)][:])
-
-        def p_RM(k):
-            nm = get("nm", k, [P, 2], F32, small, SB)
-            nc.vector.scalar_tensor_tensor(
-                out=nm[:], in0=mv_of(k)[:, :, 0], scalar=-1.0, in1=live[("rs", k)][:], op0=ALU.mult, op1=ALU.mult
-            )
-
-        def p_C1(t):
-            k, j = t // 2, t % 2
-            n1 = get("n1", k, [P, 2, D], F32, work, BUFS["n1"])
-            rs, nm = live[("rs", k)], live[("nm", k)]
-            if C1ENG[j] == "S":
-                nc.scalar.activation(
-                    out=n1[:, j, :], in_=live[("t1", t)][:], func=ACT.Identity, scale=rs[:, j : j + 1], bias=nm[:, j : j + 1]
-                )
-            elif C1ENG[j] == "G":
-                nc.gpsimd.tensor_scalar(
-                    out=n1[:, j, :], in0=live[("t1", t)][:], scalar1=rs[:, j : j + 1], scalar2=nm[:, j : j + 1],
-                    op0=ALU.mult, op1=ALU.add,
-                )
-            else:
-                nc.vector.tensor_scalar(
-                    out=n1[:, j, :], in0=live[("t1", t)][:], scalar1=mv_of(k)[:, j, 0:1], scalar2=rs[:, j : j + 1],
-                    op0=ALU.subtract, op1=ALU.mult,
+        def z_quad(k):
+            for j in range(2):
+                junk = work.tile([P, DQ], F32, name="junk", tag="junk", bufs=2)
+                jj = 2 * (k % 2) + j
+                nc.vector.scalar_tensor_tensor(
+                    out=junk[:], in0=live[("w", k)][:, j, 0:DQ], scalar=1.0, in1=z_sb[:, 2 * k + j, :],
+                    op0=ALU.mult, op1=ALU.mult, accum_out=stat4("quad", k // 2)[:, jj : jj + 1],
                 )
 
-        def p_C3(t):
-            k, j = t // 2, t % 2
-            n3 = get("n3", k, [P, 2, D], F32, work, BUFS["n3"])
-            rs, nm = live[("rs3", k)], live[("nm3", k)]
+        def z_var(k):
+            lo = 2 * (k % 2)
+            wm = small.tile([P, 2, 2], F32, name="wm", tag="wm", bufs=6)
+            live[("wm", k)] = wm
+            nc.vector.tensor_tensor(
+                out=wm[:], in0=live[("w", k)][:, :, DQ : DQ + 2], in1=nb2[:], op=ALU.add
+            )
+
+        def z_sum(k):
+            lo = 2 * (k % 2)
+            nc.gpsimd.tensor_tensor(
+                out=stat4("vs", k // 2)[:, lo : lo + 2], in0=stat4("quad", k // 2)[:, lo : lo + 2],
+                in1=live[("wm", k)][:, :, 1], op=ALU.add,
+            )
+
+        def z_std(q):
             nc.scalar.activation(
-                out=n3[:, j, :], in_=live[("y3", t)][:], func=ACT.Identity, scale=rs[:, j : j + 1], bias=nm[:, j : j + 1]
+                out=stat4("vr", q)[:], in_=stat4("vs", q)[:], func=ACT.Relu, bias=sdiv[:, 0:1], scale=1.0 / D
+            )
+            nc.scalar.activation(
+                out=stat4("sd3", q)[:], in_=stat4("vr", q)[:], func=ACT.Sqrt, bias=eps_t[:, 0:1], scale=1.0
             )
 
-        def p_T(k, br, h):
-            src = live[("n%d" % br, k)]
-            bank = psum.tile([P, 2, 2, P], F32, name="nT", tag="ps", bufs=8)
+        def z_rstd(q):
+            nc.vector.reciprocal(out=stat4("rs3", q)[:], in_=stat4("sd3", q)[:])
+
+        def z_mean(k):
+            lo = 2 * (k % 2)
+            nc.gpsimd.tensor_tensor(
+                out=stat4("nm3", k // 2)[:, lo : lo + 2], in0=live[("wm", k)][:, :, 0],
+                in1=stat4("rs3", k // 2)[:, lo : lo + 2], op=ALU.mult,
+            )
+
+        def y3_mm(t):
+            y3 = bank([P, D], F32, "y3", "y3")
+            for c in range(4):
+                nc.tensor.matmul(
+                    y3[:, c * P : (c + 1) * P], lhsT=prmT[:, 4 + c : 5 + c].to_broadcast([P, P]), rhs=ident_f[:],
+                    is_transpose=True, start=(c == 0), stop=False,
+                )
+            nc.tensor.matmul(y3[:], lhsT=z2T[:, t * P : (t + 1) * P], rhs=u3T[:], start=False, stop=True)
+            live[("y3", t)] = y3
+
+        def norm3(t):
+            k, j = t // 2, t % 2
+            if ("n3", k) not in live:
+                live[("n3", k)] = work.tile([P, 2, D], F32, name="n3", tag="n3", bufs=4)
+            jj = t % 4
+            nc.scalar.activation(
+                out=live[("n3", k)][:, j, :], in_=live[("y3", t)][:], func=ACT.Identity,
+                scale=stat4("rs3", t // 4)[:, jj : jj + 1], bias=stat4("nm3", t // 4)[:, jj : jj + 1],
+            )
+
+        def row_scaled(k):
+            return k % 2 == 1
+
+        def scale3(k):
+            n3a = work.tile([P, 2, D], F32, name="n3a", tag="n3a", bufs=2)
+            for j in range(2):
+                nc.gpsimd.tensor_tensor(out=n3a[:, j, :], in0=live[("n3", k)][:, j, :], in1=live["a3row"][:], op=ALU.mult)
+            live[("n3", k)] = n3a
+
+        def y1_mm(t):
+            cols = slice(t * P, (t + 1) * P)
+            y1 = bank([P, D], F32, "y1", "y1")
+            nc.tensor.matmul_mx(
+                out=y1[:], lhsT=xq[:, cols].bitcast(FP8X4), lhsT_scale=xs[:, cols],
+                rhs=u1q[:].bitcast(FP8X4), rhs_scale=u1s[:], start=True, stop=True,
+            )
+            live[("y1", t)] = y1
+
+        def stat(name, k):
+            if (name, k) not in live:
+                live[(name, k)] = small.tile([P, 2], F32, name=name, tag=name, bufs=6)
+            return live[(name, k)]
+
+        def bias1(t):
+            k, j = t // 2, t % 2
+            t1 = work.tile([P, D], F32, name="t1", tag="t1", bufs=8)
+            nc.vector.scalar_tensor_tensor(
+                out=t1[:], in0=live[("y1", t)][:], scalar=1.0, in1=b1row[:], op0=ALU.mult, op1=ALU.add,
+                accum_out=stat("sum1", k)[:, j : j + 1],
+            )
+            live[("t1", t)] = t1
+
+        def square1(t):
+            k, j = t // 2, t % 2
+            sq = work.tile([P, D], BF16, name="sq", tag="sq", bufs=2)
+            nc.scalar.activation(
+                out=sq[:], in_=live[("t1", t)][:], func=ACT.Square, scale=-float(D), bias=stat("sum1", k)[:, j : j + 1],
+                accum_out=stat("ssq1", k)[:, j : j + 1],
+            )
+
+        def std1(k):
+            nc.scalar.activation(
+                out=stat("sd1", k)[:], in_=stat("ssq1", k)[:], func=ACT.Sqrt, bias=eps_t[:, 0:1], scale=1.0 / D**3
+            )
+
+        def rstd1(k):
+            nc.vector.reciprocal(out=stat("rs1", k)[:], in_=stat("sd1", k)[:])
+
+        def mean1(k):
+            for j in range(2):
+                nc.gpsimd.tensor_scalar(
+                    out=stat("nm1", k)[:, j : j + 1], in0=stat("sum1", k)[:, j : j + 1],
+                    scalar1=stat("rs1", k)[:, j : j + 1], scalar2=-1.0 / D, op0=ALU.mult, op1=ALU.mult,
+                )
+
+        def norm1(k):
+            n1 = work.tile([P, 2, D], F32, name="n1", tag="n1", bufs=GL)
+            for j in range(2):
+                nc.gpsimd.tensor_scalar(
+                    out=n1[:, j, :], in0=live[("t1", 2 * k + j)][:], scalar1=stat("rs1", k)[:, j : j + 1],
+                    scalar2=stat("nm1", k)[:, j : j + 1], op0=ALU.mult, op1=ALU.add,
+                )
+            live[("n1", k)] = n1
+
+        def turn(k, br, h):
+            b = bank([P, 2, 2, P], F32, "nT", "nT")
             for cc in range(2):
                 c = 2 * h + cc
                 for j in range(2):
-                    nc.tensor.transpose(bank[:, cc, j, :], src[:, j, c * P : (c + 1) * P], ident_f[:])
-            live[("nT", k, br, h)] = bank
+                    nc.tensor.transpose(b[:, cc, j, :], live[("n%d" % br, k)][:, j, c * P : (c + 1) * P], ident_f[:])
+            live[("nT", k, br, h)] = b
 
-        def p_D(k, br, h):
-            bank = live[("nT", k, br, h)]
-            dst = get("av" if br == 1 else "bv", k, [P, 4, 2, P], F32, work, BUFS["ab"])
+        def affine(k, br, h):
+            key = ("o%d" % br, k)
+            if key not in live:
+                live[key] = work.tile([P, 4, 2, P], F32, name="o%d" % br, tag="o%d" % br, bufs=2)
             sc, bi = (g1, be1) if br == 1 else (a3, c3)
-            eng = (DENG_T if k >= TAILK else DENG)["%d%d" % (br, h)]
             for cc in range(2):
                 c = 2 * h + cc
-                if eng == "S":
-                    nc.scalar.activation(
-                        out=dst[:, c, :, :], in_=bank[:, cc, :, :], func=ACT.Identity,
-                        scale=sc[:, c : c + 1], bias=bi[:, c : c + 1],
-                    )
-                else:
-                    nc.vector.tensor_scalar(
-                        out=dst[:, c, :, :], in0=bank[:, cc, :, :], scalar1=sc[:, c : c + 1],
-                        scalar2=bi[:, c : c + 1], op0=ALU.mult, op1=ALU.add,
-                    )
+                nc.scalar.activation(
+                    out=live[key][:, c, :, :], in_=live[("nT", k, br, h)][:, cc, :, :], func=ACT.Identity,
+                    scale=sc[:, c : c + 1], bias=bi[:, c : c + 1],
+                )
 
-        def p_PRP(k):
-            hp = get("hp", k, [P, 4, 2, P], BF16, work, BUFS["hp"])
-            eng = nc.gpsimd if (PRENG_T if k >= TAILK else PRENG) == "G" else nc.vector
-            eng.tensor_tensor(
-                out=hp[:].rearrange("p c j r -> p (c j r)"),
-                in0=live[("av", k)][:].rearrange("p c j r -> p (c j r)"),
-                in1=live[("bv", k)][:].rearrange("p c j r -> p (c j r)"),
-                op=ALU.mult,
-            )
-
-        def p_RG(k):
-            hg = get("hg", k, [P, 2, P, 4], BF16, work, BUFS["hg"], 64)
-            src = live[("hp", k)][:].rearrange("p c j r -> p j r c")
-            eng = RGENG_T if k >= TAILK else RGENG
-            if eng == "G":
-                nc.gpsimd.tensor_scalar(out=hg[:], in0=src, scalar1=1.0, scalar2=0.0, op0=ALU.mult, op1=ALU.add)
-            elif eng == "V":
-                nc.vector.tensor_copy(out=hg[:], in_=src)
+        def gate(k, h):
+            if ("hp", k) not in live:
+                live[("hp", k)] = work.tile([P, 4, 2, P], BF16, name="hp", tag="hp", bufs=2)
+            hp, o1 = live[("hp", k)], live[("o1", k)]
+            if row_scaled(k):
+                for cc in range(2):
+                    c = 2 * h + cc
+                    nc.vector.scalar_tensor_tensor(
+                        out=hp[:, c, :, :], in0=live[("nT", k, 3, h)][:, cc, :, :], scalar=c3[:, c : c + 1],
+                        in1=o1[:, c, :, :], op0=ALU.add, op1=ALU.mult,
+                    )
             else:
-                nc.scalar.copy(out=hg[:], in_=src)
+                o3 = live[("o3", k)]
+                nc.vector.tensor_tensor(
+                    out=hp[:, 2 * h : 2 * h + 2].rearrange("p c j r -> p (c j r)"),
+                    in0=o1[:, 2 * h : 2 * h + 2].rearrange("p c j r -> p (c j r)"),
+                    in1=o3[:, 2 * h : 2 * h + 2].rearrange("p c j r -> p (c j r)"), op=ALU.mult,
+                )
 
-        def p_QH(k):
+        def regroup(k):
+            hg = work.tile([P, 2, P, 4], BF16, name="hg", tag="hg", bufs=2, align_bytes=64)
+            nc.gpsimd.tensor_scalar(
+                out=hg[:], in0=live[("hp", k)][:].rearrange("p c j r -> p j r c"), scalar1=1.0, scalar2=0.0,
+                op0=ALU.mult, op1=ALU.add,
+            )
+            live[("hg", k)] = hg
+
+        def h_quant(k):
             cols = slice(2 * k * P, 2 * (k + 1) * P)
             nc.vector.quantize_mx(
                 out=hq[:, cols].bitcast(FP8X4), scales=hs[:, cols],
                 in_=live[("hg", k)][:].rearrange("p j r c -> p (j r c)"),
             )
 
-        def p_O(t):
+        def o_mm(t):
             cols = slice(t * P, (t + 1) * P)
-            o = get("o", t, [P, D], F32, psum, 0)
-            for rep_i in range(DUP):
-                nc.tensor.matmul_mx(
-                    out=o[:], lhsT=hq[:, cols].bitcast(FP8X4), lhsT_scale=hs[:, cols],
-                    rhs=cq[:].bitcast(FP8X4), rhs_scale=cs[:], start=True, stop=True,
-                )
+            o = bank([P, D], F32, "o")
+            nc.tensor.matmul_mx(
+                out=o[:], lhsT=hq[:, cols].bitcast(FP8X4), lhsT_scale=hs[:, cols],
+                rhs=cq[:].bitcast(FP8X4), rhs_scale=cs[:], start=True, stop=True,
+            )
+            live[("o", t)] = o
 
-        def p_OB(t):
-            ost = get("ost", t // 2, [P, 2, D], F32, work, BUFS["ost"])
-            nc.vector.tensor_tensor(out=ost[:, t % 2, :], in0=live[("o", t)][:], in1=cbrow[:], op=ALU.add)
+        def o_bias(t):
+            if ("ost", t // 2) not in live:
+                live[("ost", t // 2)] = work.tile([P, 2, D], F32, name="ost", tag="ost", bufs=3)
+            nc.vector.tensor_tensor(
+                out=live[("ost", t // 2)][:, t % 2, :], in0=live[("o", t)][:], in1=live["cbrow"][:], op=ALU.add
+            )
 
-        def p_ST(k):
+        def store(k):
             nc.sync.dma_start(out=ov[:, 2 * k : 2 * k + 2, :], in_=live[("ost", k)][:])
 
-        tile_pieces = {"Y1": p_Y1, "Y3": p_Y3, "A1": p_A1, "BS": p_BS, "BA": p_BA, "C1": p_C1, "C3": p_C3, "O": p_O, "OB": p_OB}
-        pair_pieces = {
-            "SQ": p_SQ, "RR": p_RR, "RM": p_RM, "QH": p_QH, "ST": p_ST, "PRP": p_PRP, "RG": p_RG, "W": p_W,
-            "WA0": lambda k: p_WA(k, 0), "WA1": lambda k: p_WA(k, 1), "WV": p_WV, "S3A": p_S3A, "S3B": p_S3B,
-            "R3R": p_R3R, "R3N": p_R3N,
-        }
-        a_pieces = {
-            "x0": lambda q: p_AX(q, 0), "e0": lambda q: p_EX(q, 0), "x1": lambda q: p_AX(q, 1),
-            "e1": lambda q: p_EX(q, 1), "z": p_AZ, "ez": p_EZ, "q": p_QX, "zc": p_ZC,
-        }
+        def pair(k):
+            return 0 <= k < NK
 
-        p_ZC(0)
-        if PIN:
-            ctx.enter_context(tc.manual_schedule())
-        lags = [b[1] for b in BODY]
-        for k in range(min(lags), NG + max(lags)):
-            for b in BODY:
-                i = k - b[1]
-                if b[0] == "AQ":
-                    if 0 <= i < 7:
-                        a_pieces[b[2]](i + 1)
-                    continue
-                if b[0] == "WQ":
-                    if 0 <= i < 8:
-                        pair_pieces[b[2]](2 * i + b[3])
-                    continue
-                if i < 0 or i >= NG:
-                    continue
-                if b[0] == "A":
-                    q = i // 2 + 1
-                    if q < 8 and i % 2 == b[3]:
-                        a_pieces[b[2]](q)
-                elif b[0] == "T":
-                    p_T(i, b[2], b[3])
-                elif b[0] == "D":
-                    p_D(i, b[2], b[3])
-                elif b[0] in tile_pieces:
-                    tile_pieces[b[0]](2 * i + b[2])
-                else:
-                    pair_pieces[b[0]](i)
+        def quad_at(s, lag):
+            q, odd = divmod(s - lag, 2)
+            return [q] if odd == 0 and 0 <= q < NQ else []
+
+        for s in range(-6, NK + GL + 4):
+            k = s - GL
+            if pair(k):
+                for h in range(2):
+                    turn(k, 1, h)
+                    turn(k, 3, h)
+            if pair(s - CL - 1):
+                norm3(2 * (s - CL - 1))
+                norm3(2 * (s - CL - 1) + 1)
+            for q in quad_at(s, CL):
+                z_std(q)
+            if pair(k):
+                for h in range(2):
+                    affine(k, 1, h)
+                    if not row_scaled(k):
+                        affine(k, 3, h)
+            if pair(k - 1):
+                regroup(k - 1)
+            if pair(s):
+                bias1(2 * s)
+                bias1(2 * s + 1)
+            if pair(s - 1):
+                rstd1(s - 1)
+            if pair(k - 3):
+                o_bias(2 * (k - 3))
+            if pair(s - 1):
+                mean1(s - 1)
+            if pair(k - 3):
+                o_bias(2 * (k - 3) + 1)
+                store(k - 3)
+            if pair(s - 1):
+                norm1(s - 1)
+            if pair(s - CL - 2) and row_scaled(s - CL - 2):
+                scale3(s - CL - 2)
+            if pair(s):
+                square1(2 * s)
+                square1(2 * s + 1)
+                std1(s)
+            if pair(s - CL + 2):
+                z_quad(s - CL + 2)
+                z_var(s - CL + 2)
+            if pair(k):
+                gate(k, 0)
+            if pair(s - CL + 2):
+                z_sum(s - CL + 2)
+            if pair(k):
+                gate(k, 1)
+            for q in quad_at(s, CL):
+                z_rstd(q)
+            if pair(k - 1):
+                h_quant(k - 1)
+            for q in quad_at(s, CL):
+                z_mean(2 * q)
+                z_mean(2 * q + 1)
+            if pair(k - 2):
+                o_mm(2 * (k - 2))
+                o_mm(2 * (k - 2) + 1)
+            if pair(s + 1):
+                y1_mm(2 * (s + 1))
+                y1_mm(2 * (s + 1) + 1)
+            if pair(s - CL):
+                y3_mm(2 * (s - CL))
+                y3_mm(2 * (s - CL) + 1)
+            if pair(s - CL + 3):
+                z_gram(s - CL + 3)
+            for q in quad_at(s, CL - 5):
+                z_turn(q)
+                z_cast(q)
+            if 0 <= s < 4:
+                c_words(s)
+            if s == 4:
+                c_quant()
+                live["cbrow"] = spread([prmT[:, 8 + c : 9 + c] for c in range(4)], "cbrow")
+            if s == -6:
+                u3_turn()
+            if s == 0:
+                live["a3row"] = spread([a3[:, c : c + 1] for c in range(4)], "a3row")
+            for q in quad_at(s, -4):
+                if q:
+                    x_words(q, 0)
+            for q in quad_at(s, -3):
+                if q:
+                    x_words(q, 1)
+            for q in quad_at(s, -2):
+                if q:
+                    x_quant(q)

@@ -22,6 +22,7 @@ EPS = 1e-6
 GW = DQ + 2
 GL = 3
 CL = 0
+U0 = 7
 FLOPS = 2 * TOK * (D * D * 2 + DQ * D)
 
 
@@ -39,8 +40,8 @@ def tile_polymlp_skiplora_pa_t_kernel(
         small = ctx.enter_context(tc.tile_pool(name="small", bufs=4))
         psum = ctx.enter_context(tc.psum_pool(name="psum", bufs=1))
 
-        def bank(shape, dtype, name, tag="misc"):
-            return psum.tile(shape, dtype, name=name, tag=tag, bufs={"y1": 2, "nT": 2, "y3": 2, "misc": 2}[tag])
+        def bank(shape, dtype, name):
+            return psum.tile(shape, dtype, name=name, tag="ps", bufs=8)
 
         x_sb = keep.tile([P, NT, D], BF16, name="x_sb")
         z_sb = keep.tile([P, NT, DQ], BF16, name="z_sb")
@@ -165,10 +166,6 @@ def tile_polymlp_skiplora_pa_t_kernel(
         nc.vector.tensor_copy(out=gm[:, DQ : DQ + 1], in_=ps3[:, 0:1])
         negb = keep.tile([P, 1], F32, name="negb")
         nc.vector.tensor_scalar(out=negb[:], in0=bsum[:], scalar1=-1.0 / D, scalar2=None, op0=ALU.mult)
-        nb2 = keep.tile([P, 2, 2], F32, name="nb2")
-        nc.gpsimd.memset(nb2[:], 0.0)
-        for j in range(2):
-            nc.vector.tensor_copy(out=nb2[:, j, 0:1], in_=negb[:])
         g1 = prmT[:, 12:16]
         be1 = prmT[:, 16:20]
         a3 = keep.tile([P, 4], F32, name="a3")
@@ -210,7 +207,7 @@ def tile_polymlp_skiplora_pa_t_kernel(
             ct = bank([P, 4, P], BF16, "ct")
             for t in range(4):
                 nc.tensor.transpose(ct[:, t, :], c_raw[:, dc, t * P : (t + 1) * P], ident_b[:])
-            nc.vector.tensor_copy(out=cg[:, dc * P : (dc + 1) * P, :], in_=ct[:].rearrange("p t r -> p r t"))
+            nc.scalar.copy(out=cg[:, dc * P : (dc + 1) * P, :], in_=ct[:].rearrange("p t r -> p r t"))
 
         def c_quant():
             nc.vector.quantize_mx(out=cq[:].bitcast(FP8X4), scales=cs[:], in_=cg[:].rearrange("p d t -> p (d t)"))
@@ -232,38 +229,33 @@ def tile_polymlp_skiplora_pa_t_kernel(
 
         def stat4(name, q):
             if (name, q) not in live:
-                live[(name, q)] = small.tile([P, 4], F32, name=name, tag=name, bufs=4)
+                live[(name, q)] = small.tile([P, 4], F32, name=name, tag=name, bufs=NQ)
             return live[(name, q)]
 
-        def z_gram(k):
-            w = bank([P, 2, GW], F32, "w")
-            for j in range(2):
-                lo = ((2 * k + j) % 4) * P
-                nc.tensor.matmul(w[:, j, :], lhsT=live[("zf", k // 2)][:, lo : lo + P], rhs=gm[:], start=True, stop=True)
-            live[("w", k)] = w
+        def z_gram(q):
+            for h in range(2):
+                w = bank([P, 2, GW], F32, "w")
+                for j in range(2):
+                    lo = (2 * h + j) * P
+                    nc.tensor.matmul(w[:, j, :], lhsT=live[("zf", q)][:, lo : lo + P], rhs=gm[:], start=True, stop=True)
+                live[("w", q, h)] = w
 
-        def z_quad(k):
+        def z_quad(q, h):
+            w = live[("w", q, h)]
             for j in range(2):
+                jj = 2 * h + j
                 junk = work.tile([P, DQ], F32, name="junk", tag="junk", bufs=2)
-                jj = 2 * (k % 2) + j
                 nc.vector.scalar_tensor_tensor(
-                    out=junk[:], in0=live[("w", k)][:, j, 0:DQ], scalar=1.0, in1=z_sb[:, 2 * k + j, :],
-                    op0=ALU.mult, op1=ALU.mult, accum_out=stat4("quad", k // 2)[:, jj : jj + 1],
+                    out=junk[:], in0=w[:, j, 0:DQ], scalar=1.0, in1=z_sb[:, 4 * q + jj, :],
+                    op0=ALU.mult, op1=ALU.mult, accum_out=stat4("quad", q)[:, jj : jj + 1],
                 )
+            if ("wm", q) not in live:
+                live[("wm", q)] = small.tile([P, 4, 2], F32, name="wm", tag="wm", bufs=NQ)
+            nc.vector.tensor_copy(out=live[("wm", q)][:, 2 * h : 2 * h + 2, :], in_=w[:, :, DQ : DQ + 2])
 
-        def z_var(k):
-            lo = 2 * (k % 2)
-            wm = small.tile([P, 2, 2], F32, name="wm", tag="wm", bufs=6)
-            live[("wm", k)] = wm
+        def z_sum(q):
             nc.vector.tensor_tensor(
-                out=wm[:], in0=live[("w", k)][:, :, DQ : DQ + 2], in1=nb2[:], op=ALU.add
-            )
-
-        def z_sum(k):
-            lo = 2 * (k % 2)
-            nc.gpsimd.tensor_tensor(
-                out=stat4("vs", k // 2)[:, lo : lo + 2], in0=stat4("quad", k // 2)[:, lo : lo + 2],
-                in1=live[("wm", k)][:, :, 1], op=ALU.add,
+                out=stat4("vs", q)[:], in0=stat4("quad", q)[:], in1=live[("wm", q)][:, :, 1], op=ALU.add
             )
 
         def z_std(q):
@@ -277,15 +269,14 @@ def tile_polymlp_skiplora_pa_t_kernel(
         def z_rstd(q):
             nc.vector.reciprocal(out=stat4("rs3", q)[:], in_=stat4("sd3", q)[:])
 
-        def z_mean(k):
-            lo = 2 * (k % 2)
-            nc.gpsimd.tensor_tensor(
-                out=stat4("nm3", k // 2)[:, lo : lo + 2], in0=live[("wm", k)][:, :, 0],
-                in1=stat4("rs3", k // 2)[:, lo : lo + 2], op=ALU.mult,
+        def z_mean(q):
+            nc.vector.scalar_tensor_tensor(
+                out=stat4("nm3", q)[:], in0=live[("wm", q)][:, :, 0], scalar=negb[:, 0:1], in1=stat4("rs3", q)[:],
+                op0=ALU.add, op1=ALU.mult,
             )
 
         def y3_mm(t):
-            y3 = bank([P, D], F32, "y3", "y3")
+            y3 = bank([P, D], F32, "y3")
             for c in range(4):
                 nc.tensor.matmul(
                     y3[:, c * P : (c + 1) * P], lhsT=prmT[:, 4 + c : 5 + c].to_broadcast([P, P]), rhs=ident_f[:],
@@ -304,18 +295,9 @@ def tile_polymlp_skiplora_pa_t_kernel(
                 scale=stat4("rs3", t // 4)[:, jj : jj + 1], bias=stat4("nm3", t // 4)[:, jj : jj + 1],
             )
 
-        def row_scaled(k):
-            return k % 2 == 1
-
-        def scale3(k):
-            n3a = work.tile([P, 2, D], F32, name="n3a", tag="n3a", bufs=2)
-            for j in range(2):
-                nc.gpsimd.tensor_tensor(out=n3a[:, j, :], in0=live[("n3", k)][:, j, :], in1=live["a3row"][:], op=ALU.mult)
-            live[("n3", k)] = n3a
-
         def y1_mm(t):
             cols = slice(t * P, (t + 1) * P)
-            y1 = bank([P, D], F32, "y1", "y1")
+            y1 = bank([P, D], F32, "y1")
             nc.tensor.matmul_mx(
                 out=y1[:], lhsT=xq[:, cols].bitcast(FP8X4), lhsT_scale=xs[:, cols],
                 rhs=u1q[:].bitcast(FP8X4), rhs_scale=u1s[:], start=True, stop=True,
@@ -353,23 +335,23 @@ def tile_polymlp_skiplora_pa_t_kernel(
             nc.vector.reciprocal(out=stat("rs1", k)[:], in_=stat("sd1", k)[:])
 
         def mean1(k):
-            for j in range(2):
-                nc.gpsimd.tensor_scalar(
-                    out=stat("nm1", k)[:, j : j + 1], in0=stat("sum1", k)[:, j : j + 1],
-                    scalar1=stat("rs1", k)[:, j : j + 1], scalar2=-1.0 / D, op0=ALU.mult, op1=ALU.mult,
-                )
+            nc.vector.scalar_tensor_tensor(
+                out=stat("nm1", k)[:], in0=stat("sum1", k)[:], scalar=-1.0 / D, in1=stat("rs1", k)[:],
+                op0=ALU.mult, op1=ALU.mult,
+            )
 
         def norm1(k):
             n1 = work.tile([P, 2, D], F32, name="n1", tag="n1", bufs=GL)
             for j in range(2):
-                nc.gpsimd.tensor_scalar(
+                eng = (nc.vector, nc.gpsimd)[j]
+                eng.tensor_scalar(
                     out=n1[:, j, :], in0=live[("t1", 2 * k + j)][:], scalar1=stat("rs1", k)[:, j : j + 1],
                     scalar2=stat("nm1", k)[:, j : j + 1], op0=ALU.mult, op1=ALU.add,
                 )
             live[("n1", k)] = n1
 
         def turn(k, br, h):
-            b = bank([P, 2, 2, P], F32, "nT", "nT")
+            b = bank([P, 2, 2, P], F32, "nT")
             for cc in range(2):
                 c = 2 * h + cc
                 for j in range(2):
@@ -392,20 +374,12 @@ def tile_polymlp_skiplora_pa_t_kernel(
             if ("hp", k) not in live:
                 live[("hp", k)] = work.tile([P, 4, 2, P], BF16, name="hp", tag="hp", bufs=2)
             hp, o1 = live[("hp", k)], live[("o1", k)]
-            if row_scaled(k):
-                for cc in range(2):
-                    c = 2 * h + cc
-                    nc.vector.scalar_tensor_tensor(
-                        out=hp[:, c, :, :], in0=live[("nT", k, 3, h)][:, cc, :, :], scalar=c3[:, c : c + 1],
-                        in1=o1[:, c, :, :], op0=ALU.add, op1=ALU.mult,
-                    )
-            else:
-                o3 = live[("o3", k)]
-                nc.vector.tensor_tensor(
-                    out=hp[:, 2 * h : 2 * h + 2].rearrange("p c j r -> p (c j r)"),
-                    in0=o1[:, 2 * h : 2 * h + 2].rearrange("p c j r -> p (c j r)"),
-                    in1=o3[:, 2 * h : 2 * h + 2].rearrange("p c j r -> p (c j r)"), op=ALU.mult,
-                )
+            o3 = live[("o3", k)]
+            nc.vector.tensor_tensor(
+                out=hp[:, 2 * h : 2 * h + 2].rearrange("p c j r -> p (c j r)"),
+                in0=o1[:, 2 * h : 2 * h + 2].rearrange("p c j r -> p (c j r)"),
+                in1=o3[:, 2 * h : 2 * h + 2].rearrange("p c j r -> p (c j r)"), op=ALU.mult,
+            )
 
         def regroup(k):
             hg = work.tile([P, 2, P, 4], BF16, name="hg", tag="hg", bufs=2, align_bytes=64)
@@ -444,11 +418,43 @@ def tile_polymlp_skiplora_pa_t_kernel(
         def pair(k):
             return 0 <= k < NK
 
-        def quad_at(s, lag):
-            q, odd = divmod(s - lag, 2)
-            return [q] if odd == 0 and 0 <= q < NQ else []
+        def quad(q):
+            return 0 <= q < NQ
 
-        for s in range(-6, NK + GL + 4):
+        def prepare(u):
+            if quad(u - 2):
+                z_gram(u - 2)
+            if quad(u):
+                z_turn(u)
+            if quad(u) and u:
+                x_words(u, 0)
+                x_words(u, 1)
+            if quad(u):
+                z_cast(u)
+            if quad(u - 4):
+                z_rstd(u - 4)
+            if quad(u - 2):
+                z_quad(u - 2, 0)
+            if quad(u - 4):
+                z_mean(u - 4)
+            if quad(u - 2):
+                z_quad(u - 2, 1)
+            if quad(u - 1) and u > 1:
+                x_quant(u - 1)
+            if quad(u - 2):
+                z_sum(u - 2)
+            if quad(u - 3):
+                z_std(u - 3)
+            if u == 1:
+                u3_turn()
+            if 4 <= u < 8:
+                c_words(u - 4)
+            if u == 8:
+                c_quant()
+            if u == 3:
+                live["cbrow"] = spread([prmT[:, 8 + c : 9 + c] for c in range(4)], "cbrow")
+
+        def step(s):
             k = s - GL
             if pair(k):
                 for h in range(2):
@@ -457,13 +463,10 @@ def tile_polymlp_skiplora_pa_t_kernel(
             if pair(s - CL - 1):
                 norm3(2 * (s - CL - 1))
                 norm3(2 * (s - CL - 1) + 1)
-            for q in quad_at(s, CL):
-                z_std(q)
             if pair(k):
                 for h in range(2):
                     affine(k, 1, h)
-                    if not row_scaled(k):
-                        affine(k, 3, h)
+                    affine(k, 3, h)
             if pair(k - 1):
                 regroup(k - 1)
             if pair(s):
@@ -480,28 +483,15 @@ def tile_polymlp_skiplora_pa_t_kernel(
                 store(k - 3)
             if pair(s - 1):
                 norm1(s - 1)
-            if pair(s - CL - 2) and row_scaled(s - CL - 2):
-                scale3(s - CL - 2)
             if pair(s):
                 square1(2 * s)
                 square1(2 * s + 1)
                 std1(s)
-            if pair(s - CL + 2):
-                z_quad(s - CL + 2)
-                z_var(s - CL + 2)
             if pair(k):
                 gate(k, 0)
-            if pair(s - CL + 2):
-                z_sum(s - CL + 2)
-            if pair(k):
                 gate(k, 1)
-            for q in quad_at(s, CL):
-                z_rstd(q)
             if pair(k - 1):
                 h_quant(k - 1)
-            for q in quad_at(s, CL):
-                z_mean(2 * q)
-                z_mean(2 * q + 1)
             if pair(k - 2):
                 o_mm(2 * (k - 2))
                 o_mm(2 * (k - 2) + 1)
@@ -511,26 +501,8 @@ def tile_polymlp_skiplora_pa_t_kernel(
             if pair(s - CL):
                 y3_mm(2 * (s - CL))
                 y3_mm(2 * (s - CL) + 1)
-            if pair(s - CL + 3):
-                z_gram(s - CL + 3)
-            for q in quad_at(s, CL - 5):
-                z_turn(q)
-                z_cast(q)
-            if 0 <= s < 4:
-                c_words(s)
-            if s == 4:
-                c_quant()
-                live["cbrow"] = spread([prmT[:, 8 + c : 9 + c] for c in range(4)], "cbrow")
-            if s == -6:
-                u3_turn()
-            if s == 0:
-                live["a3row"] = spread([a3[:, c : c + 1] for c in range(4)], "a3row")
-            for q in quad_at(s, -4):
-                if q:
-                    x_words(q, 0)
-            for q in quad_at(s, -3):
-                if q:
-                    x_words(q, 1)
-            for q in quad_at(s, -2):
-                if q:
-                    x_quant(q)
+
+        for u in range(U0 + NK + GL + 4):
+            if u < NQ + 5:
+                prepare(u)
+            step(u - U0)

@@ -20,6 +20,8 @@ D = 512
 DQ = 128
 EPS = 1e-6
 GW = DQ + 2
+VM = [(3, 1, 1)]
+VT = [(3, 1, 0), (3, 1, 1)]
 GL = 3
 CL = 0
 U0 = 7
@@ -85,8 +87,6 @@ def tile_polymlp_skiplora_pa_t_kernel(
 
         xq = keep.tile([P, TOK], U32, name="xq", align_bytes=64)
         xs = keep.tile([P, TOK], U8, name="xs", align_bytes=64)
-        hq = keep.tile([P, TOK], U32, name="hq", align_bytes=64)
-        hs = keep.tile([P, TOK], U8, name="hs", align_bytes=64)
         live = {}
         ctx.enter_context(tc.manual_schedule())
 
@@ -100,7 +100,7 @@ def tile_polymlp_skiplora_pa_t_kernel(
 
         def xg_view(q):
             if ("xg", q) not in live:
-                live[("xg", q)] = work.tile([P, 4 * D], BF16, name="xg", tag="xg", align_bytes=64)
+                live[("xg", q)] = work.tile([P, 4 * D], BF16, name="xg", tag="xg", bufs=3, align_bytes=64)
             return live[("xg", q)]
 
         def x_words(q, h):
@@ -221,7 +221,7 @@ def tile_polymlp_skiplora_pa_t_kernel(
             nc.scalar.copy(out=z2T[:, 512 * q : 512 * q + 512], in_=zt[:].rearrange("p j r -> p (j r)"))
 
         def z_cast(q):
-            zf = work.tile([P, 4 * P], F32, name="zf", tag="zf", bufs=2)
+            zf = work.tile([P, 4 * P], F32, name="zf", tag="zf", bufs=3)
             nc.gpsimd.tensor_scalar(
                 out=zf[:], in0=z2T[:, 512 * q : 512 * q + 512], scalar1=1.0, scalar2=0.0, op0=ALU.mult, op1=ALU.add
             )
@@ -343,7 +343,7 @@ def tile_polymlp_skiplora_pa_t_kernel(
         def norm1(k):
             n1 = work.tile([P, 2, D], F32, name="n1", tag="n1", bufs=GL)
             for j in range(2):
-                eng = (nc.vector, nc.gpsimd)[j]
+                eng = nc.gpsimd
                 eng.tensor_scalar(
                     out=n1[:, j, :], in0=live[("t1", 2 * k + j)][:], scalar1=stat("rs1", k)[:, j : j + 1],
                     scalar2=stat("nm1", k)[:, j : j + 1], op0=ALU.mult, op1=ALU.add,
@@ -365,39 +365,37 @@ def tile_polymlp_skiplora_pa_t_kernel(
             sc, bi = (g1, be1) if br == 1 else (a3, c3)
             for cc in range(2):
                 c = 2 * h + cc
-                nc.scalar.activation(
-                    out=live[key][:, c, :, :], in_=live[("nT", k, br, h)][:, cc, :, :], func=ACT.Identity,
-                    scale=sc[:, c : c + 1], bias=bi[:, c : c + 1],
-                )
+                out, in_ = live[key][:, c, :, :], live[("nT", k, br, h)][:, cc, :, :]
+                if (br, h, cc) in (VT if k >= NK - 3 else VM):
+                    nc.vector.tensor_scalar(
+                        out=out, in0=in_, scalar1=sc[:, c : c + 1], scalar2=bi[:, c : c + 1], op0=ALU.mult, op1=ALU.add
+                    )
+                else:
+                    nc.scalar.activation(
+                        out=out, in_=in_, func=ACT.Identity, scale=sc[:, c : c + 1], bias=bi[:, c : c + 1]
+                    )
 
-        def gate(k, h):
-            if ("hp", k) not in live:
-                live[("hp", k)] = work.tile([P, 4, 2, P], BF16, name="hp", tag="hp", bufs=2)
-            hp, o1 = live[("hp", k)], live[("o1", k)]
-            o3 = live[("o3", k)]
-            nc.vector.tensor_tensor(
-                out=hp[:, 2 * h : 2 * h + 2].rearrange("p c j r -> p (c j r)"),
-                in0=o1[:, 2 * h : 2 * h + 2].rearrange("p c j r -> p (c j r)"),
-                in1=o3[:, 2 * h : 2 * h + 2].rearrange("p c j r -> p (c j r)"), op=ALU.mult,
-            )
-
-        def regroup(k):
+        def gate(k):
             hg = work.tile([P, 2, P, 4], BF16, name="hg", tag="hg", bufs=2, align_bytes=64)
-            nc.gpsimd.tensor_scalar(
-                out=hg[:], in0=live[("hp", k)][:].rearrange("p c j r -> p j r c"), scalar1=1.0, scalar2=0.0,
-                op0=ALU.mult, op1=ALU.add,
+            order = "p c j (r i) -> p (j r) c i"
+            nc.vector.tensor_tensor(
+                out=hg[:].rearrange("p j (r i) c -> p (j r) c i", i=4),
+                in0=live[("o1", k)][:].rearrange(order, i=4), in1=live[("o3", k)][:].rearrange(order, i=4),
+                op=ALU.mult,
             )
             live[("hg", k)] = hg
 
         def h_quant(k):
-            cols = slice(2 * k * P, 2 * (k + 1) * P)
+            hq = work.tile([P, 2 * P], U32, name="hq", tag="hq", bufs=3, align_bytes=64)
+            hs = work.tile([P, 2 * P], U8, name="hs", tag="hs", bufs=3, align_bytes=64)
             nc.vector.quantize_mx(
-                out=hq[:, cols].bitcast(FP8X4), scales=hs[:, cols],
-                in_=live[("hg", k)][:].rearrange("p j r c -> p (j r c)"),
+                out=hq[:].bitcast(FP8X4), scales=hs[:], in_=live[("hg", k)][:].rearrange("p j r c -> p (j r c)")
             )
+            live[("hq", k)] = (hq, hs)
 
         def o_mm(t):
-            cols = slice(t * P, (t + 1) * P)
+            hq, hs = live[("hq", t // 2)]
+            cols = slice((t % 2) * P, (t % 2 + 1) * P)
             o = bank([P, D], F32, "o")
             nc.tensor.matmul_mx(
                 out=o[:], lhsT=hq[:, cols].bitcast(FP8X4), lhsT_scale=hs[:, cols],
@@ -422,36 +420,35 @@ def tile_polymlp_skiplora_pa_t_kernel(
             return 0 <= q < NQ
 
         def prepare(u):
-            if quad(u - 2):
-                z_gram(u - 2)
-            if quad(u):
-                z_turn(u)
             if quad(u) and u:
                 x_words(u, 0)
                 x_words(u, 1)
             if quad(u):
+                z_turn(u)
                 z_cast(u)
+            if quad(u - 6):
+                z_rstd(u - 6)
             if quad(u - 4):
-                z_rstd(u - 4)
-            if quad(u - 2):
-                z_quad(u - 2, 0)
+                z_quad(u - 4, 0)
+            if quad(u - 6):
+                z_mean(u - 6)
             if quad(u - 4):
-                z_mean(u - 4)
-            if quad(u - 2):
-                z_quad(u - 2, 1)
+                z_quad(u - 4, 1)
             if quad(u - 1) and u > 1:
                 x_quant(u - 1)
-            if quad(u - 2):
-                z_sum(u - 2)
+            if quad(u - 4):
+                z_sum(u - 4)
+            if quad(u - 5):
+                z_std(u - 5)
             if quad(u - 3):
-                z_std(u - 3)
+                z_gram(u - 3)
             if u == 1:
                 u3_turn()
-            if 4 <= u < 8:
-                c_words(u - 4)
-            if u == 8:
+            if 5 <= u < 9:
+                c_words(u - 5)
+            if u == 9:
                 c_quant()
-            if u == 3:
+            if u == 4:
                 live["cbrow"] = spread([prmT[:, 8 + c : 9 + c] for c in range(4)], "cbrow")
 
         def step(s):
@@ -464,11 +461,9 @@ def tile_polymlp_skiplora_pa_t_kernel(
                 norm3(2 * (s - CL - 1))
                 norm3(2 * (s - CL - 1) + 1)
             if pair(k):
-                for h in range(2):
-                    affine(k, 1, h)
-                    affine(k, 3, h)
-            if pair(k - 1):
-                regroup(k - 1)
+                affine(k, 1, 0)
+                affine(k, 3, 0)
+                affine(k, 1, 1)
             if pair(s):
                 bias1(2 * s)
                 bias1(2 * s + 1)
@@ -488,8 +483,8 @@ def tile_polymlp_skiplora_pa_t_kernel(
                 square1(2 * s + 1)
                 std1(s)
             if pair(k):
-                gate(k, 0)
-                gate(k, 1)
+                affine(k, 3, 1)
+                gate(k)
             if pair(k - 1):
                 h_quant(k - 1)
             if pair(k - 2):
@@ -503,6 +498,6 @@ def tile_polymlp_skiplora_pa_t_kernel(
                 y3_mm(2 * (s - CL) + 1)
 
         for u in range(U0 + NK + GL + 4):
-            if u < NQ + 5:
+            if u < NQ + 7:
                 prepare(u)
             step(u - U0)

@@ -21,10 +21,10 @@ DQ = 128
 EPS = 1e-6
 GW = DQ + 2
 VM = [(3, 1, 1)]
-VT = [(3, 1, 0), (3, 1, 1)]
+VT = []
 GL = 3
-CL = 0
-U0 = 7
+CL = 1
+U0 = 6
 FLOPS = 2 * TOK * (D * D * 2 + DQ * D)
 
 
@@ -60,12 +60,13 @@ def tile_polymlp_skiplora_pa_t_kernel(
         nc.sync.dma_start(out=u3_raw[:], in_=U3_w.rearrange("(c p) k -> p c k", p=P))
         nc.sync.dma_start(out=u1_raw[:], in_=U1_w.rearrange("(c p) k -> p c k", p=P))
         nc.sync.dma_start(out=x_sb[:, 0:4, :], in_=xv[:, 0:4, :])
-        nc.sync.dma_start(out=z_sb[:, 0:16, :], in_=zv[:, 0:16, :])
+        nc.sync.dma_start(out=z_sb[:, 0:8, :], in_=zv[:, 0:8, :])
         nc.sync.dma_start(out=x_sb[:, 4:8, :], in_=xv[:, 4:8, :])
-        nc.sync.dma_start(out=c_raw[:], in_=C_w.rearrange("(c p) k -> p c k", p=P))
         nc.sync.dma_start(out=x_sb[:, 8:12, :], in_=xv[:, 8:12, :])
-        nc.sync.dma_start(out=z_sb[:, 16:32, :], in_=zv[:, 16:32, :])
-        for q in range(3, NQ):
+        nc.sync.dma_start(out=z_sb[:, 8:32, :], in_=zv[:, 8:32, :])
+        nc.sync.dma_start(out=x_sb[:, 12:16, :], in_=xv[:, 12:16, :])
+        nc.sync.dma_start(out=c_raw[:], in_=C_w.rearrange("(c p) k -> p c k", p=P))
+        for q in range(4, NQ):
             nc.sync.dma_start(out=x_sb[:, 4 * q : 4 * q + 4, :], in_=xv[:, 4 * q : 4 * q + 4, :])
 
         eps_t = keep.tile([P, 1], F32, name="eps_t")
@@ -112,37 +113,6 @@ def tile_polymlp_skiplora_pa_t_kernel(
             cols = slice(512 * q, 512 * q + 512)
             nc.vector.quantize_mx(out=xq[:, cols].bitcast(FP8X4), scales=xs[:, cols], in_=xg_view(q)[:])
 
-        ps1 = bank([P, DQ], F32, "ps1")
-        for c in range(4):
-            nc.tensor.matmul(ps1[:], lhsT=ones_b[:], rhs=u3_raw[:, c, :], start=(c == 0), stop=(c == 3))
-        u3c = keep.tile([P, 4, DQ], F32, name="u3c")
-        for c in range(4):
-            nc.vector.scalar_tensor_tensor(
-                out=u3c[:, c, :], in0=ps1[:], scalar=-1.0 / D, in1=u3_raw[:, c, :], op0=ALU.mult, op1=ALU.add
-            )
-
-        u1g = keep.tile([P, 4 * D], BF16, name="u1g", align_bytes=64)
-        u1v = u1g[:].bitcast(F32).rearrange("p (j r u) -> p j r u", j=4, u=2)
-        for h in range(2):
-            b = words_T([u1_raw[:, 2 * h + j, :] for j in range(2)])
-            nc.scalar.copy(out=u1v[:, 2 * h : 2 * h + 2], in_=b[:].rearrange("p j u r -> p j r u"))
-        for h in range(2):
-            x_words(0, h)
-        u1q = keep.tile([P, D], U32, name="u1q", align_bytes=64)
-        u1s = keep.tile([P, D], U8, name="u1s", align_bytes=64)
-        nc.vector.quantize_mx(out=u1q[:].bitcast(FP8X4), scales=u1s[:], in_=u1g[:])
-
-        ps2 = bank([P, DQ], F32, "ps2")
-        for c in range(4):
-            nc.tensor.matmul(ps2[:], lhsT=u3c[:, c, :], rhs=u3c[:, c, :], start=(c == 0), stop=(c == 3))
-        gm = keep.tile([P, GW], F32, name="gm")
-        nc.vector.tensor_copy(out=gm[:, 0:DQ], in_=ps2[:])
-
-        pT = bank([P, P], BF16, "pT")
-        nc.tensor.transpose(pT[:], prm[:], ident_b[:])
-        prmT = keep.tile([P, 28], F32, name="prmT")
-        nc.vector.tensor_copy(out=prmT[:], in_=pT[:, 0:28])
-
         def spread(cols, name):
             b = bank([P, D], F32, "sbank")
             for c in range(4):
@@ -150,46 +120,6 @@ def tile_polymlp_skiplora_pa_t_kernel(
             row = keep.tile([P, D], F32, name=name)
             nc.vector.tensor_copy(out=row[:], in_=b[:])
             return row
-
-        b1row = spread([prmT[:, c : c + 1] for c in range(4)], "b1row")
-        x_quant(0)
-
-        psb = bank([P, 4], F32, "psb")
-        nc.tensor.matmul(psb[:], lhsT=ones_f[:], rhs=prmT[:, 4:8], start=True, stop=True)
-        ps3 = bank([P, 2], F32, "ps3")
-        for c in range(4):
-            nc.tensor.matmul(ps3[:], lhsT=u3_raw[:, c, :], rhs=negc[:], start=(c == 0), stop=(c == 3))
-        bsum = keep.tile([P, 1], F32, name="bsum")
-        nc.vector.reduce_sum(out=bsum[:], in_=psb[:], axis=mybir.AxisListType.X)
-        al = keep.tile([P, 1], F32, name="al")
-        nc.vector.tensor_copy(out=al[:], in_=al_b[:])
-        nc.vector.tensor_copy(out=gm[:, DQ : DQ + 1], in_=ps3[:, 0:1])
-        negb = keep.tile([P, 1], F32, name="negb")
-        nc.vector.tensor_scalar(out=negb[:], in0=bsum[:], scalar1=-1.0 / D, scalar2=None, op0=ALU.mult)
-        g1 = prmT[:, 12:16]
-        be1 = prmT[:, 16:20]
-        a3 = keep.tile([P, 4], F32, name="a3")
-        c3 = keep.tile([P, 4], F32, name="c3")
-        nc.vector.tensor_scalar(out=a3[:], in0=prmT[:, 20:24], scalar1=al[:, 0:1], scalar2=None, op0=ALU.mult)
-        nc.vector.tensor_scalar(
-            out=b3c[:, :, 0], in0=prmT[:, 4:8], scalar1=negb[:, 0:1], scalar2=None, op0=ALU.add
-        )
-        nc.vector.tensor_scalar(
-            out=c3[:], in0=prmT[:, 24:28], scalar1=al[:, 0:1], scalar2=1.0, op0=ALU.mult, op1=ALU.add
-        )
-        psd = bank([P, 2], F32, "psd")
-        for c in range(4):
-            nc.tensor.matmul(psd[:], lhsT=u3c[:, c, :], rhs=b3c[:, c, :], start=(c == 0), stop=(c == 3))
-        ps4 = bank([P, 2], F32, "ps4")
-        for c in range(4):
-            nc.tensor.matmul(
-                ps4[:], lhsT=b3c[:, c, 0:1].to_broadcast([P, P]), rhs=b3c[:, c, :], start=(c == 0), stop=(c == 3)
-            )
-        nc.vector.tensor_scalar(
-            out=gm[:, DQ + 1 : DQ + 2], in0=psd[:, 0:1], scalar1=2.0, scalar2=None, op0=ALU.mult
-        )
-        sdiv = keep.tile([P, 1], F32, name="sdiv")
-        nc.vector.tensor_scalar(out=sdiv[:], in0=ps4[:, 0:1], scalar1=1.0 / D, scalar2=None, op0=ALU.mult)
 
         u3T = keep.tile([P, D], BF16, name="u3T")
 
@@ -258,10 +188,12 @@ def tile_polymlp_skiplora_pa_t_kernel(
                 out=stat4("vs", q)[:], in0=stat4("quad", q)[:], in1=live[("wm", q)][:, :, 1], op=ALU.add
             )
 
-        def z_std(q):
+        def z_relu(q):
             nc.scalar.activation(
                 out=stat4("vr", q)[:], in_=stat4("vs", q)[:], func=ACT.Relu, bias=sdiv[:, 0:1], scale=1.0 / D
             )
+
+        def z_std(q):
             nc.scalar.activation(
                 out=stat4("sd3", q)[:], in_=stat4("vr", q)[:], func=ACT.Sqrt, bias=eps_t[:, 0:1], scale=1.0
             )
@@ -361,7 +293,7 @@ def tile_polymlp_skiplora_pa_t_kernel(
         def affine(k, br, h):
             key = ("o%d" % br, k)
             if key not in live:
-                live[key] = work.tile([P, 4, 2, P], F32, name="o%d" % br, tag="o%d" % br, bufs=2)
+                live[key] = work.tile([P, 4, 2, P], F32, name="o%d" % br, tag="o%d" % br, bufs=3)
             sc, bi = (g1, be1) if br == 1 else (a3, c3)
             for cc in range(2):
                 c = 2 * h + cc
@@ -413,6 +345,81 @@ def tile_polymlp_skiplora_pa_t_kernel(
         def store(k):
             nc.sync.dma_start(out=ov[:, 2 * k : 2 * k + 2, :], in_=live[("ost", k)][:])
 
+        ps1 = bank([P, DQ], F32, "ps1")
+        for c in range(4):
+            nc.tensor.matmul(ps1[:], lhsT=ones_b[:], rhs=u3_raw[:, c, :], start=(c == 0), stop=(c == 3))
+        u3c = keep.tile([P, 4, DQ], F32, name="u3c")
+        for c in range(4):
+            nc.vector.scalar_tensor_tensor(
+                out=u3c[:, c, :], in0=ps1[:], scalar=-1.0 / D, in1=u3_raw[:, c, :], op0=ALU.mult, op1=ALU.add
+            )
+
+        u1g = keep.tile([P, 4 * D], BF16, name="u1g", align_bytes=64)
+        u1v = u1g[:].bitcast(F32).rearrange("p (j r u) -> p j r u", j=4, u=2)
+        for h in range(2):
+            b = words_T([u1_raw[:, 2 * h + j, :] for j in range(2)])
+            nc.scalar.copy(out=u1v[:, 2 * h : 2 * h + 2], in_=b[:].rearrange("p j u r -> p j r u"))
+        for h in range(2):
+            x_words(0, h)
+        u1q = keep.tile([P, D], U32, name="u1q", align_bytes=64)
+        u1s = keep.tile([P, D], U8, name="u1s", align_bytes=64)
+        nc.vector.quantize_mx(out=u1q[:].bitcast(FP8X4), scales=u1s[:], in_=u1g[:])
+
+        ps2 = bank([P, DQ], F32, "ps2")
+        for c in range(4):
+            nc.tensor.matmul(ps2[:], lhsT=u3c[:, c, :], rhs=u3c[:, c, :], start=(c == 0), stop=(c == 3))
+        gm = keep.tile([P, GW], F32, name="gm")
+        nc.vector.tensor_copy(out=gm[:, 0:DQ], in_=ps2[:])
+
+        pT = bank([P, P], BF16, "pT")
+        nc.tensor.transpose(pT[:], prm[:], ident_b[:])
+        prmT = keep.tile([P, 28], F32, name="prmT")
+        nc.vector.tensor_copy(out=prmT[:], in_=pT[:, 0:28])
+
+        b1row = spread([prmT[:, c : c + 1] for c in range(4)], "b1row")
+        x_quant(0)
+
+        z_turn(0)
+        z_cast(0)
+        psb = bank([P, 4], F32, "psb")
+        nc.tensor.matmul(psb[:], lhsT=ones_f[:], rhs=prmT[:, 4:8], start=True, stop=True)
+        ps3 = bank([P, 2], F32, "ps3")
+        for c in range(4):
+            nc.tensor.matmul(ps3[:], lhsT=u3_raw[:, c, :], rhs=negc[:], start=(c == 0), stop=(c == 3))
+        bsum = keep.tile([P, 1], F32, name="bsum")
+        nc.vector.reduce_sum(out=bsum[:], in_=psb[:], axis=mybir.AxisListType.X)
+        al = keep.tile([P, 1], F32, name="al")
+        nc.vector.tensor_copy(out=al[:], in_=al_b[:])
+        nc.vector.tensor_copy(out=gm[:, DQ : DQ + 1], in_=ps3[:, 0:1])
+        negb = keep.tile([P, 1], F32, name="negb")
+        nc.vector.tensor_scalar(out=negb[:], in0=bsum[:], scalar1=-1.0 / D, scalar2=None, op0=ALU.mult)
+        g1 = prmT[:, 12:16]
+        be1 = prmT[:, 16:20]
+        a3 = keep.tile([P, 4], F32, name="a3")
+        c3 = keep.tile([P, 4], F32, name="c3")
+        nc.vector.tensor_scalar(out=a3[:], in0=prmT[:, 20:24], scalar1=al[:, 0:1], scalar2=None, op0=ALU.mult)
+        nc.vector.tensor_scalar(
+            out=b3c[:, :, 0], in0=prmT[:, 4:8], scalar1=negb[:, 0:1], scalar2=None, op0=ALU.add
+        )
+        nc.vector.tensor_scalar(
+            out=c3[:], in0=prmT[:, 24:28], scalar1=al[:, 0:1], scalar2=1.0, op0=ALU.mult, op1=ALU.add
+        )
+        x_words(1, 0)
+        x_words(1, 1)
+        psd = bank([P, 2], F32, "psd")
+        for c in range(4):
+            nc.tensor.matmul(psd[:], lhsT=u3c[:, c, :], rhs=b3c[:, c, :], start=(c == 0), stop=(c == 3))
+        ps4 = bank([P, 2], F32, "ps4")
+        for c in range(4):
+            nc.tensor.matmul(
+                ps4[:], lhsT=b3c[:, c, 0:1].to_broadcast([P, P]), rhs=b3c[:, c, :], start=(c == 0), stop=(c == 3)
+            )
+        nc.vector.tensor_scalar(
+            out=gm[:, DQ + 1 : DQ + 2], in0=psd[:, 0:1], scalar1=2.0, scalar2=None, op0=ALU.mult
+        )
+        sdiv = keep.tile([P, 1], F32, name="sdiv")
+        nc.vector.tensor_scalar(out=sdiv[:], in0=ps4[:, 0:1], scalar1=1.0 / D, scalar2=None, op0=ALU.mult)
+
         def pair(k):
             return 0 <= k < NK
 
@@ -420,10 +427,14 @@ def tile_polymlp_skiplora_pa_t_kernel(
             return 0 <= q < NQ
 
         def prepare(u):
-            if quad(u) and u:
+            if quad(u - 5):
+                z_relu(u - 5)
+            if quad(u) and u > 1:
                 x_words(u, 0)
                 x_words(u, 1)
-            if quad(u):
+            if quad(u - 5):
+                z_std(u - 5)
+            if quad(u) and u:
                 z_turn(u)
                 z_cast(u)
             if quad(u - 6):
@@ -438,8 +449,6 @@ def tile_polymlp_skiplora_pa_t_kernel(
                 x_quant(u - 1)
             if quad(u - 4):
                 z_sum(u - 4)
-            if quad(u - 5):
-                z_std(u - 5)
             if quad(u - 3):
                 z_gram(u - 3)
             if u == 1:
@@ -460,6 +469,8 @@ def tile_polymlp_skiplora_pa_t_kernel(
             if pair(s - CL - 1):
                 norm3(2 * (s - CL - 1))
                 norm3(2 * (s - CL - 1) + 1)
+            if pair(s - 1):
+                std1(s - 1)
             if pair(k):
                 affine(k, 1, 0)
                 affine(k, 3, 0)
@@ -467,24 +478,23 @@ def tile_polymlp_skiplora_pa_t_kernel(
             if pair(s):
                 bias1(2 * s)
                 bias1(2 * s + 1)
-            if pair(s - 1):
-                rstd1(s - 1)
             if pair(k - 3):
                 o_bias(2 * (k - 3))
             if pair(s - 1):
-                mean1(s - 1)
+                rstd1(s - 1)
             if pair(k - 3):
                 o_bias(2 * (k - 3) + 1)
                 store(k - 3)
             if pair(s - 1):
+                mean1(s - 1)
                 norm1(s - 1)
             if pair(s):
                 square1(2 * s)
                 square1(2 * s + 1)
-                std1(s)
+            if pair(k - 1):
+                gate(k - 1)
             if pair(k):
                 affine(k, 3, 1)
-                gate(k)
             if pair(k - 1):
                 h_quant(k - 1)
             if pair(k - 2):

@@ -22,6 +22,7 @@ EPS = 1e-6
 GW = DQ + 2
 VM = [(3, 1, 1)]
 VT = []
+SPLIT_Q = 6
 GL = 3
 CL = 1
 U0 = 6
@@ -50,18 +51,25 @@ def tile_polymlp_skiplora_pa_t_kernel(
         u1_raw = keep.tile([P, 4, D], BF16, name="u1_raw")
         u3_raw = keep.tile([P, 4, DQ], BF16, name="u3_raw")
         c_raw = keep.tile([P, 4, D], BF16, name="c_raw")
-        prm = keep.tile([P, P], BF16, name="prm")
-        nc.vector.memset(prm[:], 0.0)
-        vecs = [U1_b, U3_b, C_b, ln1_g, ln1_b, ln3_g, ln3_b]
-        for j, vec in enumerate(vecs):
-            nc.scalar.dma_start(out=prm[4 * j : 4 * j + 4, :], in_=vec.rearrange("(c p) -> c p", p=P))
+        eps_t = keep.tile([P, 1], F32, name="eps_t")
+        nc.vector.memset(eps_t[:], EPS)
+        warm = keep.tile([P, 1], F32, name="warm")
+        nc.scalar.activation(out=warm[:], in_=eps_t[:], func=ACT.Sqrt, bias=eps_t[:, 0:1], scale=1.0)
+        prm_a = keep.tile([P, P], BF16, name="prm_a")
+        nc.vector.memset(prm_a[:], 0.0)
+        prm_b = keep.tile([P, P], BF16, name="prm_b")
+        nc.gpsimd.memset(prm_b[:], 0.0)
+        for j, vec in enumerate([U1_b, U3_b]):
+            nc.scalar.dma_start(out=prm_a[4 * j : 4 * j + 4, :], in_=vec.rearrange("(c p) -> c p", p=P))
         al_b = keep.tile([P, 1], BF16, name="al_b")
-        nc.scalar.dma_start(out=al_b[:], in_=alpha.partition_broadcast(P))
         nc.sync.dma_start(out=u3_raw[:], in_=U3_w.rearrange("(c p) k -> p c k", p=P))
         nc.sync.dma_start(out=u1_raw[:], in_=U1_w.rearrange("(c p) k -> p c k", p=P))
         nc.sync.dma_start(out=x_sb[:, 0:4, :], in_=xv[:, 0:4, :])
         nc.sync.dma_start(out=z_sb[:, 0:8, :], in_=zv[:, 0:8, :])
         nc.sync.dma_start(out=x_sb[:, 4:8, :], in_=xv[:, 4:8, :])
+        for j, vec in enumerate([ln1_g, ln1_b, ln3_g, ln3_b, C_b]):
+            nc.sync.dma_start(out=prm_b[4 * j : 4 * j + 4, :], in_=vec.rearrange("(c p) -> c p", p=P))
+        nc.sync.dma_start(out=al_b[:], in_=alpha.partition_broadcast(P))
         nc.sync.dma_start(out=x_sb[:, 8:12, :], in_=xv[:, 8:12, :])
         nc.sync.dma_start(out=z_sb[:, 8:32, :], in_=zv[:, 8:32, :])
         nc.sync.dma_start(out=x_sb[:, 12:16, :], in_=xv[:, 12:16, :])
@@ -69,10 +77,6 @@ def tile_polymlp_skiplora_pa_t_kernel(
         for q in range(4, NQ):
             nc.sync.dma_start(out=x_sb[:, 4 * q : 4 * q + 4, :], in_=xv[:, 4 * q : 4 * q + 4, :])
 
-        eps_t = keep.tile([P, 1], F32, name="eps_t")
-        nc.vector.memset(eps_t[:], EPS)
-        warm = keep.tile([P, 1], F32, name="warm")
-        nc.scalar.activation(out=warm[:], in_=eps_t[:], func=ACT.Sqrt, bias=eps_t[:, 0:1], scale=1.0)
         ones_b = keep.tile([P, P], BF16, name="ones_b")
         nc.vector.memset(ones_b[:], 1.0)
         ones_f = keep.tile([P, P], F32, name="ones_f")
@@ -167,7 +171,14 @@ def tile_polymlp_skiplora_pa_t_kernel(
                 w = bank([P, 2, GW], F32, "w")
                 for j in range(2):
                     lo = (2 * h + j) * P
-                    nc.tensor.matmul(w[:, j, :], lhsT=live[("zf", q)][:, lo : lo + P], rhs=gm[:], start=True, stop=True)
+                    if q < SPLIT_Q:
+                        zt = z2T[:, 512 * q + lo : 512 * q + lo + P]
+                        nc.tensor.matmul(w[:, j, :], lhsT=zt, rhs=gm_hi[:], start=True, stop=False)
+                        nc.tensor.matmul(w[:, j, :], lhsT=zt, rhs=gm_lo[:], start=False, stop=True)
+                    else:
+                        nc.tensor.matmul(
+                            w[:, j, :], lhsT=live[("zf", q)][:, lo : lo + P], rhs=gm[:], start=True, stop=True
+                        )
                 live[("w", q, h)] = w
 
         def z_quad(q, h):
@@ -211,7 +222,7 @@ def tile_polymlp_skiplora_pa_t_kernel(
             y3 = bank([P, D], F32, "y3")
             for c in range(4):
                 nc.tensor.matmul(
-                    y3[:, c * P : (c + 1) * P], lhsT=prmT[:, 4 + c : 5 + c].to_broadcast([P, P]), rhs=ident_f[:],
+                    y3[:, c * P : (c + 1) * P], lhsT=prmA[:, 4 + c : 5 + c].to_broadcast([P, P]), rhs=ident_f[:],
                     is_transpose=True, start=(c == 0), stop=False,
                 )
             nc.tensor.matmul(y3[:], lhsT=z2T[:, t * P : (t + 1) * P], rhs=u3T[:], start=False, stop=True)
@@ -294,7 +305,8 @@ def tile_polymlp_skiplora_pa_t_kernel(
             key = ("o%d" % br, k)
             if key not in live:
                 live[key] = work.tile([P, 4, 2, P], F32, name="o%d" % br, tag="o%d" % br, bufs=3)
-            sc, bi = (g1, be1) if br == 1 else (a3, c3)
+            prmB = live["prmB"]
+            sc, bi = (prmB[:, 0:4], prmB[:, 4:8]) if br == 1 else (live["a3"], live["c3"])
             for cc in range(2):
                 c = 2 * h + cc
                 out, in_ = live[key][:, c, :, :], live[("nT", k, br, h)][:, cc, :, :]
@@ -372,37 +384,25 @@ def tile_polymlp_skiplora_pa_t_kernel(
         nc.vector.tensor_copy(out=gm[:, 0:DQ], in_=ps2[:])
 
         pT = bank([P, P], BF16, "pT")
-        nc.tensor.transpose(pT[:], prm[:], ident_b[:])
-        prmT = keep.tile([P, 28], F32, name="prmT")
-        nc.vector.tensor_copy(out=prmT[:], in_=pT[:, 0:28])
-
-        b1row = spread([prmT[:, c : c + 1] for c in range(4)], "b1row")
+        nc.tensor.transpose(pT[:], prm_a[:], ident_b[:])
+        prmA = keep.tile([P, 8], F32, name="prmA")
+        nc.vector.tensor_copy(out=prmA[:], in_=pT[:, 0:8])
+        b1row = spread([prmA[:, c : c + 1] for c in range(4)], "b1row")
         x_quant(0)
 
         z_turn(0)
-        z_cast(0)
         psb = bank([P, 4], F32, "psb")
-        nc.tensor.matmul(psb[:], lhsT=ones_f[:], rhs=prmT[:, 4:8], start=True, stop=True)
+        nc.tensor.matmul(psb[:], lhsT=ones_f[:], rhs=prmA[:, 4:8], start=True, stop=True)
         ps3 = bank([P, 2], F32, "ps3")
         for c in range(4):
             nc.tensor.matmul(ps3[:], lhsT=u3_raw[:, c, :], rhs=negc[:], start=(c == 0), stop=(c == 3))
         bsum = keep.tile([P, 1], F32, name="bsum")
         nc.vector.reduce_sum(out=bsum[:], in_=psb[:], axis=mybir.AxisListType.X)
-        al = keep.tile([P, 1], F32, name="al")
-        nc.vector.tensor_copy(out=al[:], in_=al_b[:])
         nc.vector.tensor_copy(out=gm[:, DQ : DQ + 1], in_=ps3[:, 0:1])
         negb = keep.tile([P, 1], F32, name="negb")
         nc.vector.tensor_scalar(out=negb[:], in0=bsum[:], scalar1=-1.0 / D, scalar2=None, op0=ALU.mult)
-        g1 = prmT[:, 12:16]
-        be1 = prmT[:, 16:20]
-        a3 = keep.tile([P, 4], F32, name="a3")
-        c3 = keep.tile([P, 4], F32, name="c3")
-        nc.vector.tensor_scalar(out=a3[:], in0=prmT[:, 20:24], scalar1=al[:, 0:1], scalar2=None, op0=ALU.mult)
         nc.vector.tensor_scalar(
-            out=b3c[:, :, 0], in0=prmT[:, 4:8], scalar1=negb[:, 0:1], scalar2=None, op0=ALU.add
-        )
-        nc.vector.tensor_scalar(
-            out=c3[:], in0=prmT[:, 24:28], scalar1=al[:, 0:1], scalar2=1.0, op0=ALU.mult, op1=ALU.add
+            out=b3c[:, :, 0], in0=prmA[:, 4:8], scalar1=negb[:, 0:1], scalar2=None, op0=ALU.add
         )
         x_words(1, 0)
         x_words(1, 1)
@@ -417,8 +417,12 @@ def tile_polymlp_skiplora_pa_t_kernel(
         nc.vector.tensor_scalar(
             out=gm[:, DQ + 1 : DQ + 2], in0=psd[:, 0:1], scalar1=2.0, scalar2=None, op0=ALU.mult
         )
+        gm_hi = keep.tile([P, GW], BF16, name="gm_hi")
+        nc.vector.tensor_copy(out=gm_hi[:], in_=gm[:])
+        gm_lo = keep.tile([P, GW], BF16, name="gm_lo")
         sdiv = keep.tile([P, 1], F32, name="sdiv")
         nc.vector.tensor_scalar(out=sdiv[:], in0=ps4[:, 0:1], scalar1=1.0 / D, scalar2=None, op0=ALU.mult)
+        nc.vector.tensor_tensor(out=gm_lo[:], in0=gm[:], in1=gm_hi[:], op=ALU.subtract)
 
         def pair(k):
             return 0 <= k < NK
@@ -426,7 +430,24 @@ def tile_polymlp_skiplora_pa_t_kernel(
         def quad(q):
             return 0 <= q < NQ
 
+        def affine_columns():
+            pT = bank([P, P], BF16, "pT")
+            nc.tensor.transpose(pT[:], prm_b[:], ident_b[:])
+            prmB = keep.tile([P, 20], F32, name="prmB")
+            nc.vector.tensor_copy(out=prmB[:], in_=pT[:, 0:20])
+            al = keep.tile([P, 1], F32, name="al")
+            nc.vector.tensor_copy(out=al[:], in_=al_b[:])
+            a3 = keep.tile([P, 4], F32, name="a3")
+            c3 = keep.tile([P, 4], F32, name="c3")
+            nc.vector.tensor_scalar(out=a3[:], in0=prmB[:, 8:12], scalar1=al[:, 0:1], scalar2=None, op0=ALU.mult)
+            nc.vector.tensor_scalar(
+                out=c3[:], in0=prmB[:, 12:16], scalar1=al[:, 0:1], scalar2=1.0, op0=ALU.mult, op1=ALU.add
+            )
+            live["prmB"], live["a3"], live["c3"] = prmB, a3, c3
+
         def prepare(u):
+            if u == 3:
+                affine_columns()
             if quad(u - 5):
                 z_relu(u - 5)
             if quad(u) and u > 1:
@@ -436,7 +457,8 @@ def tile_polymlp_skiplora_pa_t_kernel(
                 z_std(u - 5)
             if quad(u) and u:
                 z_turn(u)
-                z_cast(u)
+                if u >= SPLIT_Q:
+                    z_cast(u)
             if quad(u - 6):
                 z_rstd(u - 6)
             if quad(u - 4):
@@ -458,7 +480,7 @@ def tile_polymlp_skiplora_pa_t_kernel(
             if u == 9:
                 c_quant()
             if u == 4:
-                live["cbrow"] = spread([prmT[:, 8 + c : 9 + c] for c in range(4)], "cbrow")
+                live["cbrow"] = spread([live["prmB"][:, 16 + c : 17 + c] for c in range(4)], "cbrow")
 
         def step(s):
             k = s - GL

@@ -20,7 +20,7 @@ D = 512
 DQ = 128
 EPS = 1e-6
 GW = DQ + 2
-VM = [(3, 1, 1)]
+VM = []
 VT = []
 SPLIT_Q = 6
 GL = 3
@@ -319,13 +319,34 @@ def tile_polymlp_skiplora_pa_t_kernel(
                         out=out, in_=in_, func=ACT.Identity, scale=sc[:, c : c + 1], bias=bi[:, c : c + 1]
                     )
 
+        def packs_itself(k):
+            return k % 3 == 0
+
         def gate(k):
-            hg = work.tile([P, 2, P, 4], BF16, name="hg", tag="hg", bufs=2, align_bytes=64)
-            order = "p c j (r i) -> p (j r) c i"
-            nc.vector.tensor_tensor(
-                out=hg[:].rearrange("p j (r i) c -> p (j r) c i", i=4),
-                in0=live[("o1", k)][:].rearrange(order, i=4), in1=live[("o3", k)][:].rearrange(order, i=4),
-                op=ALU.mult,
+            o1, o3 = live[("o1", k)], live[("o3", k)]
+            if packs_itself(k):
+                hg = work.tile([P, 2, P, 4], BF16, name="hg", tag="hg", bufs=3, align_bytes=64)
+                order = "p c j (r i) -> p (j r) c i"
+                nc.vector.tensor_tensor(
+                    out=hg[:].rearrange("p j (r i) c -> p (j r) c i", i=4),
+                    in0=o1[:].rearrange(order, i=4), in1=o3[:].rearrange(order, i=4), op=ALU.mult,
+                )
+                live[("hg", k)] = hg
+            else:
+                hp = work.tile([P, 4, 2, P], BF16, name="hp", tag="hp", bufs=2)
+                flat = "p c j r -> p (c j r)"
+                nc.vector.tensor_tensor(
+                    out=hp[:].rearrange(flat), in0=o1[:].rearrange(flat), in1=o3[:].rearrange(flat), op=ALU.mult
+                )
+                live[("hp", k)] = hp
+
+        def regroup(k):
+            if packs_itself(k):
+                return
+            hg = work.tile([P, 2, P, 4], BF16, name="hg", tag="hg", bufs=3, align_bytes=64)
+            nc.gpsimd.tensor_scalar(
+                out=hg[:], in0=live[("hp", k)][:].rearrange("p c j r -> p j r c"), scalar1=1.0, scalar2=0.0,
+                op0=ALU.mult, op1=ALU.add,
             )
             live[("hg", k)] = hg
 
@@ -490,24 +511,26 @@ def tile_polymlp_skiplora_pa_t_kernel(
                     turn(k, 3, h)
             if pair(s - CL - 1):
                 norm3(2 * (s - CL - 1))
-                norm3(2 * (s - CL - 1) + 1)
             if pair(s - 1):
                 std1(s - 1)
+            if pair(s - CL - 1):
+                norm3(2 * (s - CL - 1) + 1)
             if pair(k):
                 affine(k, 1, 0)
                 affine(k, 3, 0)
                 affine(k, 1, 1)
+            if pair(k - 2):
+                regroup(k - 2)
             if pair(s):
                 bias1(2 * s)
                 bias1(2 * s + 1)
-            if pair(k - 3):
-                o_bias(2 * (k - 3))
+            if pair(k - 4):
+                o_bias(2 * (k - 4))
+            if pair(k - 4):
+                o_bias(2 * (k - 4) + 1)
+                store(k - 4)
             if pair(s - 1):
                 rstd1(s - 1)
-            if pair(k - 3):
-                o_bias(2 * (k - 3) + 1)
-                store(k - 3)
-            if pair(s - 1):
                 mean1(s - 1)
                 norm1(s - 1)
             if pair(s):
@@ -517,11 +540,11 @@ def tile_polymlp_skiplora_pa_t_kernel(
                 gate(k - 1)
             if pair(k):
                 affine(k, 3, 1)
-            if pair(k - 1):
-                h_quant(k - 1)
             if pair(k - 2):
-                o_mm(2 * (k - 2))
-                o_mm(2 * (k - 2) + 1)
+                h_quant(k - 2)
+            if pair(k - 3):
+                o_mm(2 * (k - 3))
+                o_mm(2 * (k - 3) + 1)
             if pair(s + 1):
                 y1_mm(2 * (s + 1))
                 y1_mm(2 * (s + 1) + 1)
@@ -529,7 +552,7 @@ def tile_polymlp_skiplora_pa_t_kernel(
                 y3_mm(2 * (s - CL))
                 y3_mm(2 * (s - CL) + 1)
 
-        for u in range(U0 + NK + GL + 4):
+        for u in range(U0 + NK + GL + 5):
             if u < NQ + 7:
                 prepare(u)
             step(u - U0)

from contextlib import ExitStack

import concourse.mybir as mybir
from concourse.masks import make_identity

F32 = mybir.dt.float32
BF16 = mybir.dt.bfloat16
U32 = mybir.dt.uint32
U8 = mybir.dt.uint8
FP8X4 = mybir.dt.float8_e4m3fn_x4
ALU = mybir.AluOpType
ACT = mybir.ActivationFunctionType

P = 128
TOK = 4096
NT = TOK // P
NK = NT // 2
NQ = NT // 4
D = 512
DQ = 128
EPS = 1e-6
GW = DQ + 2
VM = []
VT = []
SPLIT_Q = 6
GL = 3
CL = 1
U0 = 6
FLOPS = 2 * TOK * (D * D * 2 + DQ * D)


def tile_polymlp_skiplora_pa_t_kernel(
    tc, x, z2, U1_w, U1_b, U3_w, U3_b, C_w, C_b, ln1_g, ln1_b, ln3_g, ln3_b, alpha, out
):
    nc = tc.nc
    xv = x.flatten_outer_dims().rearrange("(p i) k -> p i k", i=NT)
    zv = z2.flatten_outer_dims().rearrange("(p i) k -> p i k", i=NT)
    ov = out.flatten_outer_dims().rearrange("(p i) d -> p i d", i=NT)

    with ExitStack() as ctx:
        keep = ctx.enter_context(tc.tile_pool(name="keep", bufs=1))
        work = ctx.enter_context(tc.tile_pool(name="work", bufs=2))
        small = ctx.enter_context(tc.tile_pool(name="small", bufs=4))
        psum = ctx.enter_context(tc.psum_pool(name="psum", bufs=1))

        def bank(shape, dtype, name):
            return psum.tile(shape, dtype, name=name, tag="ps", bufs=8)

        x_sb = keep.tile([P, NT, D], BF16, name="x_sb")
        z_sb = keep.tile([P, NT, DQ], BF16, name="z_sb")
        u1_raw = keep.tile([P, 4, D], BF16, name="u1_raw")
        u3_raw = keep.tile([P, 4, DQ], BF16, name="u3_raw")
        c_raw = keep.tile([P, 4, D], BF16, name="c_raw")
        eps_t = keep.tile([P, 1], F32, name="eps_t")
        nc.vector.memset(eps_t[:], EPS)
        warm = keep.tile([P, 1], F32, name="warm")
        nc.scalar.activation(out=warm[:], in_=eps_t[:], func=ACT.Sqrt, bias=eps_t[:, 0:1], scale=1.0)
        prm_a = keep.tile([P, P], BF16, name="prm_a")
        nc.vector.memset(prm_a[:], 0.0)
        prm_b = keep.tile([P, P], BF16, name="prm_b")
        nc.gpsimd.memset(prm_b[:], 0.0)
        for j, vec in enumerate([U1_b, U3_b]):
            nc.scalar.dma_start(out=prm_a[4 * j : 4 * j + 4, :], in_=vec.rearrange("(c p) -> c p", p=P))
        al_b = keep.tile([P, 1], BF16, name="al_b")
        nc.sync.dma_start(out=u3_raw[:], in_=U3_w.rearrange("(c p) k -> p c k", p=P))
        nc.sync.dma_start(out=u1_raw[:], in_=U1_w.rearrange("(c p) k -> p c k", p=P))
        nc.sync.dma_start(out=x_sb[:, 0:4, :], in_=xv[:, 0:4, :])
        nc.sync.dma_start(out=z_sb[:, 0:8, :], in_=zv[:, 0:8, :])
        nc.sync.dma_start(out=x_sb[:, 4:8, :], in_=xv[:, 4:8, :])
        for j, vec in enumerate([ln1_g, ln1_b, ln3_g, ln3_b, C_b]):
            nc.sync.dma_start(out=prm_b[4 * j : 4 * j + 4, :], in_=vec.rearrange("(c p) -> c p", p=P))
        nc.sync.dma_start(out=al_b[:], in_=alpha.partition_broadcast(P))
        nc.sync.dma_start(out=x_sb[:, 8:12, :], in_=xv[:, 8:12, :])
        nc.sync.dma_start(out=z_sb[:, 8:32, :], in_=zv[:, 8:32, :])
        nc.sync.dma_start(out=x_sb[:, 12:16, :], in_=xv[:, 12:16, :])
        nc.sync.dma_start(out=c_raw[:], in_=C_w.rearrange("(c p) k -> p c k", p=P))
        for q in range(4, NQ):
            nc.sync.dma_start(out=x_sb[:, 4 * q : 4 * q + 4, :], in_=xv[:, 4 * q : 4 * q + 4, :])

        ones_b = keep.tile([P, P], BF16, name="ones_b")
        nc.vector.memset(ones_b[:], 1.0)
        ones_f = keep.tile([P, P], F32, name="ones_f")
        nc.vector.memset(ones_f[:], 1.0)
        negc = keep.tile([P, 2], BF16, name="negc")
        nc.vector.memset(negc[:], -1.0 / D)
        b3c = keep.tile([P, 4, 2], F32, name="b3c")
        nc.vector.memset(b3c[:], 0.0)
        ident_f = keep.tile([P, P], F32, name="ident_f")
        make_identity(nc, ident_f[:])
        ident_b = keep.tile([P, P], BF16, name="ident_b")
        make_identity(nc, ident_b[:])

        xq = keep.tile([P, TOK], U32, name="xq", align_bytes=64)
        xs = keep.tile([P, TOK], U8, name="xs", align_bytes=64)
        live = {}
        ctx.enter_context(tc.manual_schedule())

        def words_T(rows_pair):
            b = bank([P, 2, 2, P], F32, "wbank")
            for j, rows in enumerate(rows_pair):
                w = rows.bitcast(F32)
                for u in range(2):
                    nc.tensor.transpose(b[:, j, u, :], w[:, u * P : (u + 1) * P], ident_f[:])
            return b

        def xg_view(q):
            if ("xg", q) not in live:
                live[("xg", q)] = work.tile([P, 4 * D], BF16, name="xg", tag="xg", bufs=3, align_bytes=64)
            return live[("xg", q)]

        def x_words(q, h):
            b = words_T([x_sb[:, 4 * q + 2 * h + j, :] for j in range(2)])
            v32 = xg_view(q)[:].bitcast(F32).rearrange("p (j r u) -> p j r u", j=4, u=2)
            nc.scalar.copy(out=v32[:, 2 * h : 2 * h + 2], in_=b[:].rearrange("p j u r -> p j r u"))

        def x_quant(q):
            cols = slice(512 * q, 512 * q + 512)
            nc.vector.quantize_mx(out=xq[:, cols].bitcast(FP8X4), scales=xs[:, cols], in_=xg_view(q)[:])

        def spread(cols, name):
            b = bank([P, D], F32, "sbank")
            for c in range(4):
                nc.tensor.transpose(b[:, c * P : (c + 1) * P], cols[c].to_broadcast([P, P]), ident_f[:])
            row = keep.tile([P, D], F32, name=name)
            nc.vector.tensor_copy(out=row[:], in_=b[:])
            return row

        u3T = keep.tile([P, D], BF16, name="u3T")

        def u3_turn():
            ut = bank([P, 4, P], BF16, "ut")
            for c in range(4):
                nc.tensor.transpose(ut[:, c, :], u3_raw[:, c, :], ident_b[:])
            nc.scalar.copy(out=u3T[:], in_=ut[:].rearrange("p c r -> p (c r)"))

        cq = keep.tile([P, D], U32, name="cq", align_bytes=64)
        cs = keep.tile([P, D], U8, name="cs", align_bytes=64)
        cg = keep.tile([P, D, 4], BF16, name="cg", align_bytes=64)

        def c_words(dc):
            ct = bank([P, 4, P], BF16, "ct")
            for t in range(4):
                nc.tensor.transpose(ct[:, t, :], c_raw[:, dc, t * P : (t + 1) * P], ident_b[:])
            nc.scalar.copy(out=cg[:, dc * P : (dc + 1) * P, :], in_=ct[:].rearrange("p t r -> p r t"))

        def c_quant():
            nc.vector.quantize_mx(out=cq[:].bitcast(FP8X4), scales=cs[:], in_=cg[:].rearrange("p d t -> p (d t)"))

        z2T = keep.tile([P, TOK], BF16, name="z2T")

        def z_turn(q):
            zt = bank([P, 4, P], BF16, "zt")
            for j in range(4):
                nc.tensor.transpose(zt[:, j, :], z_sb[:, 4 * q + j, :], ident_b[:])
            nc.scalar.copy(out=z2T[:, 512 * q : 512 * q + 512], in_=zt[:].rearrange("p j r -> p (j r)"))

        def z_cast(q):
            zf = work.tile([P, 4 * P], F32, name="zf", tag="zf", bufs=3)
            nc.gpsimd.tensor_scalar(
                out=zf[:], in0=z2T[:, 512 * q : 512 * q + 512], scalar1=1.0, scalar2=0.0, op0=ALU.mult, op1=ALU.add
            )
            live[("zf", q)] = zf

        def stat4(name, q):
            if (name, q) not in live:
                live[(name, q)] = small.tile([P, 4], F32, name=name, tag=name, bufs=NQ)
            return live[(name, q)]

        def z_gram(q):
            for h in range(2):
                w = bank([P, 2, GW], F32, "w")
                for j in range(2):
                    lo = (2 * h + j) * P
                    if q < SPLIT_Q:
                        zt = z2T[:, 512 * q + lo : 512 * q + lo + P]
                        nc.tensor.matmul(w[:, j, :], lhsT=zt, rhs=gm_hi[:], start=True, stop=False)
                        nc.tensor.matmul(w[:, j, :], lhsT=zt, rhs=gm_lo[:], start=False, stop=True)
                    else:
                        nc.tensor.matmul(
                            w[:, j, :], lhsT=live[("zf", q)][:, lo : lo + P], rhs=gm[:], start=True, stop=True
                        )
                live[("w", q, h)] = w

        def z_quad(q, h):
            w = live[("w", q, h)]
            for j in range(2):
                jj = 2 * h + j
                junk = work.tile([P, DQ], F32, name="junk", tag="junk", bufs=2)
                nc.vector.scalar_tensor_tensor(
                    out=junk[:], in0=w[:, j, 0:DQ], scalar=1.0, in1=z_sb[:, 4 * q + jj, :],
                    op0=ALU.mult, op1=ALU.mult, accum_out=stat4("quad", q)[:, jj : jj + 1],
                )
            if ("wm", q) not in live:
                live[("wm", q)] = small.tile([P, 4, 2], F32, name="wm", tag="wm", bufs=NQ)
            nc.vector.tensor_copy(out=live[("wm", q)][:, 2 * h : 2 * h + 2, :], in_=w[:, :, DQ : DQ + 2])

        def z_sum(q):
            nc.vector.tensor_tensor(
                out=stat4("vs", q)[:], in0=stat4("quad", q)[:], in1=live[("wm", q)][:, :, 1], op=ALU.add
            )

        def z_relu(q):
            nc.scalar.activation(
                out=stat4("vr", q)[:], in_=stat4("vs", q)[:], func=ACT.Relu, bias=sdiv[:, 0:1], scale=1.0 / D
            )

        def z_std(q):
            nc.scalar.activation(
                out=stat4("sd3", q)[:], in_=stat4("vr", q)[:], func=ACT.Sqrt, bias=eps_t[:, 0:1], scale=1.0
            )

        def z_rstd(q):
            nc.vector.reciprocal(out=stat4("rs3", q)[:], in_=stat4("sd3", q)[:])

        def z_mean(q):
            nc.vector.scalar_tensor_tensor(
                out=stat4("nm3", q)[:], in0=live[("wm", q)][:, :, 0], scalar=negb[:, 0:1], in1=stat4("rs3", q)[:],
                op0=ALU.add, op1=ALU.mult,
            )

        def y3_mm(t):
            y3 = bank([P, D], F32, "y3")
            for c in range(4):
                nc.tensor.matmul(
                    y3[:, c * P : (c + 1) * P], lhsT=prmA[:, 4 + c : 5 + c].to_broadcast([P, P]), rhs=ident_f[:],
                    is_transpose=True, start=(c == 0), stop=False,
                )
            nc.tensor.matmul(y3[:], lhsT=z2T[:, t * P : (t + 1) * P], rhs=u3T[:], start=False, stop=True)
            live[("y3", t)] = y3

        def norm3(t):
            k, j = t // 2, t % 2
            if ("n3", k) not in live:
                live[("n3", k)] = work.tile([P, 2, D], F32, name="n3", tag="n3", bufs=4)
            jj = t % 4
            nc.scalar.activation(
                out=live[("n3", k)][:, j, :], in_=live[("y3", t)][:], func=ACT.Identity,
                scale=stat4("rs3", t // 4)[:, jj : jj + 1], bias=stat4("nm3", t // 4)[:, jj : jj + 1],
            )

        def y1_mm(t):
            cols = slice(t * P, (t + 1) * P)
            y1 = bank([P, D], F32, "y1")
            nc.tensor.matmul_mx(
                out=y1[:], lhsT=xq[:, cols].bitcast(FP8X4), lhsT_scale=xs[:, cols],
                rhs=u1q[:].bitcast(FP8X4), rhs_scale=u1s[:], start=True, stop=True,
            )
            live[("y1", t)] = y1

        def stat(name, k):
            if (name, k) not in live:
                live[(name, k)] = small.tile([P, 2], F32, name=name, tag=name, bufs=6)
            return live[(name, k)]

        def bias1(t):
            k, j = t // 2, t % 2
            t1 = work.tile([P, D], F32, name="t1", tag="t1", bufs=8)
            nc.vector.scalar_tensor_tensor(
                out=t1[:], in0=live[("y1", t)][:], scalar=1.0, in1=b1row[:], op0=ALU.mult, op1=ALU.add,
                accum_out=stat("sum1", k)[:, j : j + 1],
            )
            live[("t1", t)] = t1

        def square1(t):
            k, j = t // 2, t % 2
            sq = work.tile([P, D], BF16, name="sq", tag="sq", bufs=2)
            nc.scalar.activation(
                out=sq[:], in_=live[("t1", t)][:], func=ACT.Square, scale=-float(D), bias=stat("sum1", k)[:, j : j + 1],
                accum_out=stat("ssq1", k)[:, j : j + 1],
            )

        def std1(k):
            nc.scalar.activation(
                out=stat("sd1", k)[:], in_=stat("ssq1", k)[:], func=ACT.Sqrt, bias=eps_t[:, 0:1], scale=1.0 / D**3
            )

        def rstd1(k):
            nc.vector.reciprocal(out=stat("rs1", k)[:], in_=stat("sd1", k)[:])

        def mean1(k):
            nc.vector.scalar_tensor_tensor(
                out=stat("nm1", k)[:], in0=stat("sum1", k)[:], scalar=-1.0 / D, in1=stat("rs1", k)[:],
                op0=ALU.mult, op1=ALU.mult,
            )

        def norm1(k):
            n1 = work.tile([P, 2, D], F32, name="n1", tag="n1", bufs=GL)
            for j in range(2):
                eng = nc.gpsimd
                eng.tensor_scalar(
                    out=n1[:, j, :], in0=live[("t1", 2 * k + j)][:], scalar1=stat("rs1", k)[:, j : j + 1],
                    scalar2=stat("nm1", k)[:, j : j + 1], op0=ALU.mult, op1=ALU.add,
                )
            live[("n1", k)] = n1

        def turn(k, br, h):
            b = bank([P, 2, 2, P], F32, "nT")
            for cc in range(2):
                c = 2 * h + cc
                for j in range(2):
                    nc.tensor.transpose(b[:, cc, j, :], live[("n%d" % br, k)][:, j, c * P : (c + 1) * P], ident_f[:])
            live[("nT", k, br, h)] = b

        def affine(k, br, h):
            key = ("o%d" % br, k)
            if key not in live:
                live[key] = work.tile([P, 4, 2, P], F32, name="o%d" % br, tag="o%d" % br, bufs=3)
            prmB = live["prmB"]
            sc, bi = (prmB[:, 0:4], prmB[:, 4:8]) if br == 1 else (live["a3"], live["c3"])
            for cc in range(2):
                c = 2 * h + cc
                out, in_ = live[key][:, c, :, :], live[("nT", k, br, h)][:, cc, :, :]
                if (br, h, cc) in (VT if k >= NK - 3 else VM):
                    nc.vector.tensor_scalar(
                        out=out, in0=in_, scalar1=sc[:, c : c + 1], scalar2=bi[:, c : c + 1], op0=ALU.mult, op1=ALU.add
                    )
                else:
                    nc.scalar.activation(
                        out=out, in_=in_, func=ACT.Identity, scale=sc[:, c : c + 1], bias=bi[:, c : c + 1]
                    )

        def packs_itself(k):
            return k % 3 == 0

        def gate(k):
            o1, o3 = live[("o1", k)], live[("o3", k)]
            if packs_itself(k):
                hg = work.tile([P, 2, P, 4], BF16, name="hg", tag="hg", bufs=3, align_bytes=64)
                order = "p c j (r i) -> p (j r) c i"
                nc.vector.tensor_tensor(
                    out=hg[:].rearrange("p j (r i) c -> p (j r) c i", i=4),
                    in0=o1[:].rearrange(order, i=4), in1=o3[:].rearrange(order, i=4), op=ALU.mult,
                )
                live[("hg", k)] = hg
            else:
                hp = work.tile([P, 4, 2, P], BF16, name="hp", tag="hp", bufs=2)
                flat = "p c j r -> p (c j r)"
                nc.vector.tensor_tensor(
                    out=hp[:].rearrange(flat), in0=o1[:].rearrange(flat), in1=o3[:].rearrange(flat), op=ALU.mult
                )
                live[("hp", k)] = hp

        def regroup(k):
            if packs_itself(k):
                return
            hg = work.tile([P, 2, P, 4], BF16, name="hg", tag="hg", bufs=3, align_bytes=64)
            nc.gpsimd.tensor_scalar(
                out=hg[:], in0=live[("hp", k)][:].rearrange("p c j r -> p j r c"), scalar1=1.0, scalar2=0.0,
                op0=ALU.mult, op1=ALU.add,
            )
            live[("hg", k)] = hg

        def h_quant(k):
            hq = work.tile([P, 2 * P], U32, name="hq", tag="hq", bufs=3, align_bytes=64)
            hs = work.tile([P, 2 * P], U8, name="hs", tag="hs", bufs=3, align_bytes=64)
            nc.vector.quantize_mx(
                out=hq[:].bitcast(FP8X4), scales=hs[:], in_=live[("hg", k)][:].rearrange("p j r c -> p (j r c)")
            )
            live[("hq", k)] = (hq, hs)

        def o_mm(t):
            hq, hs = live[("hq", t // 2)]
            cols = slice((t % 2) * P, (t % 2 + 1) * P)
            o = bank([P, D], F32, "o")
            nc.tensor.matmul_mx(
                out=o[:], lhsT=hq[:, cols].bitcast(FP8X4), lhsT_scale=hs[:, cols],
                rhs=cq[:].bitcast(FP8X4), rhs_scale=cs[:], start=True, stop=True,
            )
            live[("o", t)] = o

        def o_bias(t):
            if ("ost", t // 2) not in live:
                live[("ost", t // 2)] = work.tile([P, 2, D], F32, name="ost", tag="ost", bufs=3)
            nc.vector.tensor_tensor(
                out=live[("ost", t // 2)][:, t % 2, :], in0=live[("o", t)][:], in1=live["cbrow"][:], op=ALU.add
            )

        def store(k):
            nc.sync.dma_start(out=ov[:, 2 * k : 2 * k + 2, :], in_=live[("ost", k)][:])

        ps1 = bank([P, DQ], F32, "ps1")
        for c in range(4):
            nc.tensor.matmul(ps1[:], lhsT=ones_b[:], rhs=u3_raw[:, c, :], start=(c == 0), stop=(c == 3))
        u3c = keep.tile([P, 4, DQ], F32, name="u3c")
        for c in range(4):
            nc.vector.scalar_tensor_tensor(
                out=u3c[:, c, :], in0=ps1[:], scalar=-1.0 / D, in1=u3_raw[:, c, :], op0=ALU.mult, op1=ALU.add
            )

        u1g = keep.tile([P, 4 * D], BF16, name="u1g", align_bytes=64)
        u1v = u1g[:].bitcast(F32).rearrange("p (j r u) -> p j r u", j=4, u=2)
        for h in range(2):
            b = words_T([u1_raw[:, 2 * h + j, :] for j in range(2)])
            nc.scalar.copy(out=u1v[:, 2 * h : 2 * h + 2], in_=b[:].rearrange("p j u r -> p j r u"))
        for h in range(2):
            x_words(0, h)
        u1q = keep.tile([P, D], U32, name="u1q", align_bytes=64)
        u1s = keep.tile([P, D], U8, name="u1s", align_bytes=64)
        nc.vector.quantize_mx(out=u1q[:].bitcast(FP8X4), scales=u1s[:], in_=u1g[:])

        ps2 = bank([P, DQ], F32, "ps2")
        for c in range(4):
            nc.tensor.matmul(ps2[:], lhsT=u3c[:, c, :], rhs=u3c[:, c, :], start=(c == 0), stop=(c == 3))
        gm = keep.tile([P, GW], F32, name="gm")
        nc.vector.tensor_copy(out=gm[:, 0:DQ], in_=ps2[:])

        pT = bank([P, P], BF16, "pT")
        nc.tensor.transpose(pT[:], prm_a[:], ident_b[:])
        prmA = keep.tile([P, 8], F32, name="prmA")
        nc.vector.tensor_copy(out=prmA[:], in_=pT[:, 0:8])
        b1row = spread([prmA[:, c : c + 1] for c in range(4)], "b1row")
        x_quant(0)

        z_turn(0)
        psb = bank([P, 4], F32, "psb")
        nc.tensor.matmul(psb[:], lhsT=ones_f[:], rhs=prmA[:, 4:8], start=True, stop=True)
        ps3 = bank([P, 2], F32, "ps3")
        for c in range(4):
            nc.tensor.matmul(ps3[:], lhsT=u3_raw[:, c, :], rhs=negc[:], start=(c == 0), stop=(c == 3))
        bsum = keep.tile([P, 1], F32, name="bsum")
        nc.vector.reduce_sum(out=bsum[:], in_=psb[:], axis=mybir.AxisListType.X)
        nc.vector.tensor_copy(out=gm[:, DQ : DQ + 1], in_=ps3[:, 0:1])
        negb = keep.tile([P, 1], F32, name="negb")
        nc.vector.tensor_scalar(out=negb[:], in0=bsum[:], scalar1=-1.0 / D, scalar2=None, op0=ALU.mult)
        nc.vector.tensor_scalar(
            out=b3c[:, :, 0], in0=prmA[:, 4:8], scalar1=negb[:, 0:1], scalar2=None, op0=ALU.add
        )
        x_words(1, 0)
        x_words(1, 1)
        psd = bank([P, 2], F32, "psd")
        for c in range(4):
            nc.tensor.matmul(psd[:], lhsT=u3c[:, c, :], rhs=b3c[:, c, :], start=(c == 0), stop=(c == 3))
        ps4 = bank([P, 2], F32, "ps4")
        for c in range(4):
            nc.tensor.matmul(
                ps4[:], lhsT=b3c[:, c, 0:1].to_broadcast([P, P]), rhs=b3c[:, c, :], start=(c == 0), stop=(c == 3)
            )
        nc.vector.tensor_scalar(
            out=gm[:, DQ + 1 : DQ + 2], in0=psd[:, 0:1], scalar1=2.0, scalar2=None, op0=ALU.mult
        )
        gm_hi = keep.tile([P, GW], BF16, name="gm_hi")
        nc.vector.tensor_copy(out=gm_hi[:], in_=gm[:])
        gm_lo = keep.tile([P, GW], BF16, name="gm_lo")
        sdiv = keep.tile([P, 1], F32, name="sdiv")
        nc.vector.tensor_scalar(out=sdiv[:], in0=ps4[:, 0:1], scalar1=1.0 / D, scalar2=None, op0=ALU.mult)
        nc.vector.tensor_tensor(out=gm_lo[:], in0=gm[:], in1=gm_hi[:], op=ALU.subtract)

        def pair(k):
            return 0 <= k < NK

        def quad(q):
            return 0 <= q < NQ

        def affine_columns():
            pT = bank([P, P], BF16, "pT")
            nc.tensor.transpose(pT[:], prm_b[:], ident_b[:])
            prmB = keep.tile([P, 20], F32, name="prmB")
            nc.vector.tensor_copy(out=prmB[:], in_=pT[:, 0:20])
            al = keep.tile([P, 1], F32, name="al")
            nc.vector.tensor_copy(out=al[:], in_=al_b[:])
            a3 = keep.tile([P, 4], F32, name="a3")
            c3 = keep.tile([P, 4], F32, name="c3")
            nc.vector.tensor_scalar(out=a3[:], in0=prmB[:, 8:12], scalar1=al[:, 0:1], scalar2=None, op0=ALU.mult)
            nc.vector.tensor_scalar(
                out=c3[:], in0=prmB[:, 12:16], scalar1=al[:, 0:1], scalar2=1.0, op0=ALU.mult, op1=ALU.add
            )
            live["prmB"], live["a3"], live["c3"] = prmB, a3, c3

        def prepare(u):
            if u == 3:
                affine_columns()
            if quad(u - 5):
                z_relu(u - 5)
            if quad(u) and u > 1:
                x_words(u, 0)
                x_words(u, 1)
            if quad(u - 5):
                z_std(u - 5)
            if quad(u) and u:
                z_turn(u)
                if u >= SPLIT_Q:
                    z_cast(u)
            if quad(u - 6):
                z_rstd(u - 6)
            if quad(u - 4):
                z_quad(u - 4, 0)
            if quad(u - 6):
                z_mean(u - 6)
            if quad(u - 4):
                z_quad(u - 4, 1)
            if quad(u - 1) and u > 1:
                x_quant(u - 1)
            if quad(u - 4):
                z_sum(u - 4)
            if quad(u - 3):
                z_gram(u - 3)
            if u == 1:
                u3_turn()
            if 5 <= u < 9:
                c_words(u - 5)
            if u == 9:
                c_quant()
            if u == 4:
                live["cbrow"] = spread([live["prmB"][:, 16 + c : 17 + c] for c in range(4)], "cbrow")

        def step(s):
            k = s - GL
            if pair(k):
                for h in range(2):
                    turn(k, 1, h)
                    turn(k, 3, h)
            if pair(s - CL - 1):
                norm3(2 * (s - CL - 1))
            if pair(s - 1):
                std1(s - 1)
            if pair(s - CL - 1):
                norm3(2 * (s - CL - 1) + 1)
            if pair(k):
                affine(k, 1, 0)
                affine(k, 3, 0)
                affine(k, 1, 1)
            if pair(k - 2):
                regroup(k - 2)
            if pair(s):
                bias1(2 * s)
                bias1(2 * s + 1)
            if pair(k - 4):
                o_bias(2 * (k - 4))
            if pair(k - 4):
                o_bias(2 * (k - 4) + 1)
                store(k - 4)
            if pair(s - 1):
                rstd1(s - 1)
                mean1(s - 1)
                norm1(s - 1)
            if pair(s):
                square1(2 * s)
                square1(2 * s + 1)
            if pair(k - 1):
                gate(k - 1)
            if pair(k):
                affine(k, 3, 1)
            if pair(k - 2):
                h_quant(k - 2)
            if pair(k - 3):
                o_mm(2 * (k - 3))
                o_mm(2 * (k - 3) + 1)
            if pair(s + 1):
                y1_mm(2 * (s + 1))
                y1_mm(2 * (s + 1) + 1)
            if pair(s - CL):
                y3_mm(2 * (s - CL))
                y3_mm(2 * (s - CL) + 1)

        for u in range(U0 + NK + GL + 5):
            if u < NQ + 7:
                prepare(u)
            step(u - U0)
